import numpy as np
import ml_dtypes


def mxq(x, axis, fmt="e4m3"):
    dtype, down = {"e4m3": (ml_dtypes.float8_e4m3fn, 7), "e5m2": (ml_dtypes.float8_e5m2, 14)}[fmt]
    v = np.moveaxis(np.asarray(x, np.float32).astype(ml_dtypes.bfloat16).astype(np.float64), axis, -1)
    blocks = v.reshape(v.shape[:-1] + (-1, 32))
    amax = np.abs(blocks).max(-1, keepdims=True)
    byte = np.maximum(np.where(amax > 0, np.frexp(amax)[1] - 1 + 127, 0) - down, 1)
    scale = np.exp2(byte - 127.0)
    codes = (blocks / scale).astype(np.float32).astype(dtype).astype(np.float64)
    return np.moveaxis((codes * scale).reshape(v.shape), -1, axis)


WIDE = False


def mx_kscale(k):
    if not WIDE:
        return np.ones(k)
    levels = np.array([10, -10, 5, -5, 0])
    a = np.random.permutation(np.resize(levels, k // 512 * 4)).reshape(k // 512, 4)
    idx = np.arange(k)
    return np.exp2(a[idx // 512, idx % 128 // 32])


BF16 = ml_dtypes.bfloat16


def bf(x):
    return np.asarray(x, np.float32).astype(BF16)


def f64(x):
    return np.asarray(x).astype(np.float64)


B, N, C, L = 16, 16, 1024, 2
EPS = 1e-5


def sigmoid(v):
    return 1.0 / (1.0 + np.exp(-v))


def bn(t, w, o):
    mean = t.mean(axis=(0, -1), keepdims=True)
    var = np.square(t - mean).mean(axis=(0, -1), keepdims=True)
    return (t - mean) / np.sqrt(var + EPS) * w[None, :, None] + o[None, :, None]


def setup_inputs():
    s = mx_kscale(C)

    def wx(g):
        return bf(np.random.standard_normal((C, C)) * g / np.sqrt(C) / s[None, :])

    return {
        "x": bf(np.random.standard_normal((B, N, C)) * s),
        "edge": bf(np.random.standard_normal((B, N * N, C)) * 1.5),
        "Wu": wx(0.5),
        "Wv": wx(6.0),
        "Wa": wx(1.0),
        "Wb": wx(1.0),
        "We": bf(np.random.standard_normal((C, C)) / np.sqrt(C)),
        "bnv_w": bf(1.0 + 0.1 * np.random.standard_normal(N)),
        "bnv_b": bf(0.1 * np.random.standard_normal(N)),
        "bne_w": bf(1.0 + 0.1 * np.random.standard_normal(N * N)),
        "bne_b": bf(0.1 * np.random.standard_normal(N * N)),
    }


def reference(x, edge, Wu, Wv, Wa, Wb, We, bnv_w, bnv_b, bne_w, bne_b):
    edge = f64(edge)
    xq = mxq(f64(x).reshape(B * N, C), 1, "e4m3")
    ax = (xq @ mxq(f64(Wa), 1, "e4m3").T).reshape(B, N, C)
    bx = (xq @ mxq(f64(Wb), 1, "e4m3").T).reshape(B, N, C)
    ee = (mxq(edge.reshape(B * N * N, C), 1, "e4m3") @ mxq(f64(We), 1, "e4m3").T).reshape(B, N * N, C)
    m = np.repeat(ax, N, axis=1) + np.tile(bx, (1, N, 1)) + ee
    edge_new = edge + np.maximum(bn(m, f64(bne_w), f64(bne_b)), 0.0)
    g = sigmoid(edge_new).reshape(B * N, N, C)
    p = np.exp(g - g.max(axis=1, keepdims=True))
    p = (p / p.sum(axis=1, keepdims=True)).reshape(B, N * N, C)
    vx = (xq @ mxq(f64(Wv), 1, "e4m3").T).reshape(B, N, C)
    agg = (p * np.tile(vx, (1, N, 1))).reshape(B * N, N, C).sum(axis=1).reshape(B, N, C)
    y = (xq @ mxq(f64(Wu), 1, "e4m3").T).reshape(B, N, C) + agg / N
    x_new = y + np.maximum(bn(y, f64(bnv_w), f64(bnv_b)), 0.0)
    return (x_new, edge_new)

@@ -1,0 +1,437 @@
+from contextlib import ExitStack
+
+import concourse.mybir as mybir
+from concourse.masks import make_identity
+
+F32 = mybir.dt.float32
+BF16 = mybir.dt.bfloat16
+U32 = mybir.dt.uint32
+U8 = mybir.dt.uint8
+FP8X4 = mybir.dt.float8_e4m3fn_x4
+ACT = mybir.ActivationFunctionType
+ALU = mybir.AluOpType
+AX = mybir.AxisListType
+
+P = 128
+C = 1024
+NODES = 16
+TILES = 32
+EPS = 1e-5
+FLOPS = 2 * (4096 + 4 * 256) * 1024 * 1024
+
+W_E, W_A, W_B, W_V, W_U = 0, 1, 2, 3, 4
+
+SEQ = [
+    ("B0", 0), ("C2", -1), ("A3", 1), ("B1", 0), ("C3", -1), ("A1", 2), ("H", -3), ("I", -4), ("C4", -1),
+    ("F1", -2), ("D", -1), ("C1a", 0), ("VX", -2), ("C1b", 0), ("A2", 2), ("E", -1), ("F2", -2), ("G", -3),
+]
+
+
+def tile_gnn_s2_pa_t_kernel(
+    tc, x, edge, Wu, Wv, Wa, Wb, We, bnv_w, bnv_b, bne_w, bne_b, out_0, out_1
+):
+    nc = tc.nc
+    weights = [We, Wa, Wb, Wv, Wu]
+    ev = edge.rearrange("b (l h j) c -> (b l) h j c", h=2, j=NODES)
+    o1 = out_1.rearrange("b (l h j) c -> (b l) h j c", h=2, j=NODES)
+    xv = x.rearrange("b (l h) c -> (b l) h c", h=2)
+    o0 = out_0.rearrange("b (l h) c -> (b l) h c", h=2)
+    halves = [slice(0, 512), slice(512, 1024)]
+
+    with ExitStack() as ctx:
+        keep = ctx.enter_context(tc.tile_pool(name="keep", bufs=1))
+        stage = ctx.enter_context(tc.tile_pool(name="stage", bufs=2))
+        work = ctx.enter_context(tc.tile_pool(name="work", bufs=2))
+        small = ctx.enter_context(tc.tile_pool(name="small", bufs=4))
+        psum = ctx.enter_context(tc.psum_pool(name="psum", bufs=1))
+
+        ident = keep.tile([P, P], F32, name="ident")
+        make_identity(nc, ident[:])
+
+        ctx.enter_context(tc.manual_schedule())
+
+        same_l = keep.tile([P, 8], F32, name="same_l")
+        nc.vector.tensor_reduce(
+            out=same_l[:], in_=ident[:].rearrange("p (b l) -> p l b", l=8), axis=AX.X, op=ALU.add
+        )
+        avg_pos = keep.tile([P, P], F32, name="avg_pos")
+        avg_neg = keep.tile([P, P], F32, name="avg_neg")
+        nc.vector.tensor_scalar(
+            out=avg_pos[:].rearrange("p (b l) -> p b l", l=8),
+            in0=same_l[:].unsqueeze(1).to_broadcast([P, 16, 8]),
+            scalar1=1.0 / 16.0, scalar2=None, op0=ALU.mult,
+        )
+        nc.vector.tensor_scalar(
+            out=avg_neg[:].rearrange("p (b l) -> p b l", l=8),
+            in0=same_l[:].unsqueeze(1).to_broadcast([P, 16, 8]),
+            scalar1=-1.0 / 16.0, scalar2=None, op0=ALU.mult,
+        )
+        eps_row = keep.tile([P, 4], F32, name="eps_row")
+        nc.vector.memset(eps_row[:], 0.0)
+        nc.vector.memset(eps_row[:, 1:2], EPS)
+        minus_half = keep.tile([P, 1], F32, name="minus_half")
+        nc.vector.memset(minus_half[:], -0.5)
+
+        wc = [keep.tile([P, 2, C], U32, name="wc%d" % i, align_bytes=64) for i in range(5)]
+        ws = [keep.tile([P, 2, C], U8, name="ws%d" % i, align_bytes=64) for i in range(5)]
+        xnc = keep.tile([P, 2, 256], U32, name="xnc", align_bytes=64)
+        xns = keep.tile([P, 2, 256], U8, name="xns", align_bytes=64)
+        xrc = keep.tile([P, NODES, 256], U32, name="xrc", align_bytes=64)
+        xrs = keep.tile([P, NODES, 256], U8, name="xrs", align_bytes=64)
+        ed = [[keep.tile([P, 4, C], BF16, name="ed%d_%d" % (h, q)) for q in range(4)] for h in range(2)]
+        sum_e = [keep.tile([P, C], F32, name="sum_e%d" % h) for h in range(2)]
+        sum_ev = [keep.tile([P, C], F32, name="sum_ev%d" % h) for h in range(2)]
+
+        def transpose_words(bank, src_words):
+            for k in range(4):
+                nc.tensor.transpose(
+                    bank[:, k * P:(k + 1) * P], src_words[:, k * P:(k + 1) * P], ident[:]
+                )
+
+        def bank_view(bank):
+            return bank.rearrange("p (g u r) -> p g r u", g=2, u=2)
+
+        def load_half(i):
+            w, h = i // 2, i % 2
+            wst = stage.tile([P, 4, C], BF16, name="wst", tag="wst")
+            nc.sync.dma_start(
+                out=wst[:], in_=weights[w][h * 512:(h + 1) * 512, :].rearrange("(a p) k -> p a k", p=P)
+            )
+            return wst
+
+        def new_group_tile():
+            grp = stage.tile([P, 4096], BF16, name="grp", tag="grp", align_bytes=64)
+            return grp
+
+        def weight_rows(wst, grp, a, bank):
+            transpose_words(bank, wst[:].bitcast(F32)[:, a, :])
+            dst = grp[:].bitcast(F32).rearrange("p (g c u) -> p g c u", g=2, u=2)[:, :, a * P:(a + 1) * P, :]
+            nc.scalar.copy(out=dst, in_=bank_view(bank))
+
+        def weight_quantise(i, grp):
+            w, h = i // 2, i % 2
+            for g in range(2):
+                nc.vector.quantize_mx(
+                    out=wc[w][:, g, h * 512:(h + 1) * 512].bitcast(FP8X4),
+                    scales=ws[w][:, g, h * 512:(h + 1) * 512],
+                    in_=grp[:, g * 2048:(g + 1) * 2048],
+                )
+
+        def prep_half(i, wst, tags):
+            grp = new_group_tile()
+            for a2 in range(2):
+                tag = tags[a2]
+                big = psum.tile([P, C], F32, name="big", tag=tag, bufs=(2 if tag == "m" else 1))
+                for k in range(2):
+                    weight_rows(wst, grp, 2 * a2 + k, big[:, halves[k]])
+            weight_quantise(i, grp)
+
+        def mx_group(acc, operands):
+            last = len(operands) - 1
+            for i, (lc, ls, rc, rs) in enumerate(operands):
+                nc.tensor.matmul_mx(
+                    out=acc, lhsT=lc.bitcast(FP8X4), lhsT_scale=ls, rhs=rc.bitcast(FP8X4), rhs_scale=rs,
+                    start=(i == 0), stop=(i == last),
+                )
+
+        def pair(lc, ls, w, cols):
+            return [
+                (lc[:, g * P:(g + 1) * P], ls[:, g * P:(g + 1) * P], wc[w][:, g, cols], ws[w][:, g, cols])
+                for g in range(2)
+            ]
+
+        tr, egrp, ecod, escl, m_ps, st6, mv, ps4, sb, sc, en, ex, exv, vx = (
+            {}, {}, {}, {}, {}, {}, {}, {}, {}, {}, {}, {}, {}, {}
+        )
+
+        def edge_in(t):
+            j, h = t // 2, t % 2
+            return ed[h][j // 4][:, j % 4, :]
+
+        def stats_half(t, n, src):
+            if n == 0:
+                st6[t] = small.tile([P, 2, 6], F32, name="st6", tag="st6")
+            nc.vector.bn_stats(out=st6[t][:, n, :], in_=src)
+            if n == 1:
+                mv[t] = small.tile([P, 2], F32, name="mv", tag="mv")
+                nc.vector.bn_aggr(out=mv[t][:], in_=st6[t][:].rearrange("p a s -> p (a s)"))
+                nc.vector.scalar_tensor_tensor(
+                    out=mv[t][:, 1:2], in0=mv[t][:, 0:1], scalar=mv[t][:, 0:1], in1=mv[t][:, 1:2],
+                    op0=ALU.mult, op1=ALU.add,
+                )
+
+        def st_c2(t):
+            ps4[t] = psum.tile([P, 4], F32, name="ps4", tag="st")
+            nc.tensor.matmul(ps4[t][:, 0:2], lhsT=avg_pos[:], rhs=mv[t][:], start=True, stop=True)
+            nc.tensor.matmul(ps4[t][:, 2:4], lhsT=avg_neg[:], rhs=mv[t][:], start=True, stop=True)
+
+        def st_c3(t):
+            sb[t] = small.tile([P, 4], F32, name="sb", tag="sb")
+            nc.vector.tensor_tensor(out=sb[t][:], in0=ps4[t][:], in1=eps_row[:], op=ALU.add)
+
+        def st_c4(t, w_col, o_col):
+            sc[t] = small.tile([P, 4], F32, name="sc", tag="sc")
+            a, b = sc[t], sb[t]
+            nc.gpsimd.tensor_scalar(
+                out=a[:, 0:1], in0=b[:, 0:1], scalar1=b[:, 2:3], scalar2=b[:, 1:2], op0=ALU.mult, op1=ALU.add
+            )
+            nc.gpsimd.tensor_tensor(out=a[:, 1:2], in0=a[:, 0:1], in1=minus_half[:], op=ALU.pow)
+            nc.gpsimd.tensor_tensor(out=a[:, 2:3], in0=a[:, 1:2], in1=w_col, op=ALU.mult)
+            nc.gpsimd.tensor_scalar(
+                out=a[:, 3:4], in0=a[:, 2:3], scalar1=b[:, 2:3], scalar2=o_col, op0=ALU.mult, op1=ALU.add
+            )
+
+        def st_a1(t):
+            tr[t] = psum.tile([P, 512], F32, name="tr", tag="tr")
+            transpose_words(tr[t], edge_in(t).bitcast(F32))
+
+        def st_a2(t):
+            egrp[t] = work.tile([P, C], BF16, name="egrp", tag="egrp", align_bytes=64)
+            nc.scalar.copy(
+                out=egrp[t][:].bitcast(F32).rearrange("p (g r u) -> p g r u", g=2, u=2), in_=bank_view(tr[t])
+            )
+
+        def st_a3(t):
+            ecod[t] = work.tile([P, 256], U32, name="ecod", tag="ecod", bufs=3, align_bytes=64)
+            escl[t] = work.tile([P, 256], U8, name="escl", tag="escl", bufs=3, align_bytes=64)
+            nc.vector.quantize_mx(out=ecod[t][:].bitcast(FP8X4), scales=escl[t][:], in_=egrp[t][:])
+
+        def st_b(t, n):
+            j, h = t // 2, t % 2
+            if n == 0:
+                m_ps[t] = psum.tile([P, C], F32, name="m_ps", tag="m", bufs=2)
+            mx_group(
+                m_ps[t][:, halves[n]],
+                pair(ecod[t], escl[t], W_E, halves[n])
+                + pair(xnc[:, h, :], xns[:, h, :], W_A, halves[n])
+                + pair(xrc[:, j, :], xrs[:, j, :], W_B, halves[n]),
+            )
+
+        def st_d(t):
+            en[t] = work.tile([P, C], F32, name="en", tag="en", bufs=3)
+            for n in range(2):
+                nc.scalar.activation(
+                    out=en[t][:, halves[n]], in_=m_ps[t][:, halves[n]], func=ACT.Relu,
+                    bias=sc[t][:, 3:4], scale=sc[t][:, 2:3],
+                )
+
+        def st_e(t):
+            j, h = t // 2, t % 2
+            nc.vector.tensor_tensor(out=en[t][:], in0=en[t][:], in1=edge_in(t), op=ALU.add)
+            nc.sync.dma_start(out=o1[:, h, j, :], in_=en[t][:])
+
+        def st_f1(t):
+            if t < 2:
+                ex[t] = sum_e[t]
+            else:
+                ex[t] = work.tile([P, C], F32, name="ex", tag="ex", bufs=3)
+            nc.scalar.activation(out=ex[t][:], in_=en[t][:], func=ACT.Tanh, scale=0.5)
+
+        def st_f2(t):
+            nc.scalar.activation(out=ex[t][:], in_=ex[t][:], func=ACT.Exp, scale=0.5)
+
+        def st_g(t):
+            if t >= 2:
+                for n in range(2):
+                    nc.gpsimd.tensor_tensor(
+                        out=sum_e[t % 2][:, halves[n]], in0=sum_e[t % 2][:, halves[n]], in1=ex[t][:, halves[n]],
+                        op=ALU.add,
+                    )
+
+        def st_h(t):
+            if t < 2:
+                exv[t] = sum_ev[t]
+            else:
+                exv[t] = work.tile([P, C], F32, name="exv", tag="exv", bufs=2)
+            for n in range(2):
+                nc.vector.tensor_tensor(
+                    out=exv[t][:, halves[n]], in0=ex[t][:, halves[n]], in1=vx[t // 2][:, halves[n]], op=ALU.mult
+                )
+
+        def st_i(t):
+            if t >= 2:
+                nc.vector.tensor_tensor(out=sum_ev[t % 2][:], in0=sum_ev[t % 2][:], in1=exv[t][:], op=ALU.add)
+
+        def st_vx(j):
+            vx[j] = psum.tile([P, C], F32, name="vx_ps", tag="vx")
+            for n in range(2):
+                mx_group(vx[j][:, halves[n]], pair(xrc[:, j, :], xrs[:, j, :], W_V, halves[n]))
+
+        def edge_cols(t):
+            col = (t % 2) * NODES + t // 2
+            return prm[:, col:col + 1], prm[:, 32 + col:33 + col]
+
+        def period(t):
+            for name, off in SEQ:
+                s = t + off
+                if name == "VX":
+                    if s >= 0 and s % 2 == 0 and s // 2 < NODES:
+                        st_vx(s // 2)
+                    continue
+                if s < 0 or s >= TILES:
+                    continue
+                if name == "A1":
+                    st_a1(s)
+                elif name == "A2":
+                    st_a2(s)
+                elif name == "A3":
+                    st_a3(s)
+                elif name == "B0":
+                    st_b(s, 0)
+                elif name == "B1":
+                    st_b(s, 1)
+                elif name == "C1a":
+                    stats_half(s, 0, m_ps[s][:, halves[0]])
+                elif name == "C1b":
+                    stats_half(s, 1, m_ps[s][:, halves[1]])
+                elif name == "C2":
+                    st_c2(s)
+                elif name == "C3":
+                    st_c3(s)
+                elif name == "C4":
+                    w_col, o_col = edge_cols(s)
+                    st_c4(s, w_col, o_col)
+                elif name == "D":
+                    st_d(s)
+                elif name == "E":
+                    st_e(s)
+                elif name == "F1":
+                    st_f1(s)
+                elif name == "F2":
+                    st_f2(s)
+                elif name == "G":
+                    st_g(s)
+                elif name == "H":
+                    st_h(s)
+                elif name == "I":
+                    st_i(s)
+
+        xs = work.tile([P, 2, C], BF16, name="xs", tag="en", bufs=3)
+        nc.sync.dma_start(out=xs[:], in_=xv)
+        pst = keep.tile([P, 96], BF16, name="pst")
+        nc.vector.memset(pst[:], 0.0)
+        nc.sync.dma_start(out=pst[0:8, 0:32], in_=bne_w.rearrange("(l x) -> l x", l=8))
+        nc.sync.dma_start(out=pst[0:8, 32:64], in_=bne_b.rearrange("(l x) -> l x", l=8))
+        nc.sync.dma_start(out=pst[0:8, 64:66], in_=bnv_w.rearrange("(l x) -> l x", l=8))
+        nc.sync.dma_start(out=pst[0:8, 80:82], in_=bnv_b.rearrange("(l x) -> l x", l=8))
+        loaded = [load_half(0), load_half(1)]
+
+        xbank = psum.tile([P, C], F32, name="xbank", tag="m", bufs=2)
+        xg = []
+        for h in range(2):
+            transpose_words(xbank[:, halves[h]], xs[:].bitcast(F32)[:, h, :])
+            g_t = work.tile([P, C], BF16, name="xg", tag="egrp", align_bytes=64)
+            nc.scalar.copy(
+                out=g_t[:].bitcast(F32).rearrange("p (g r u) -> p g r u", g=2, u=2),
+                in_=bank_view(xbank[:, halves[h]]),
+            )
+            xg.append(g_t)
+        for h in range(2):
+            nc.vector.quantize_mx(out=xnc[:, h, :].bitcast(FP8X4), scales=xns[:, h, :], in_=xg[h][:])
+
+        def repeat_x(q):
+            grp = new_group_tile()
+            dst = grp[:].bitcast(F32).rearrange(
+                "p (jj g b l u) -> p jj g b l u", jj=4, g=2, b=16, l=8, u=2
+            )
+            for jj in range(4):
+                j = 4 * q + jj
+                src = xg[j % 2][:].bitcast(F32).rearrange("p (g b l u) -> p g b l u", g=2, b=16, l=8, u=2)
+                for g in range(2):
+                    nc.vector.tensor_copy(
+                        out=dst[:, jj, g, :, :, :],
+                        in_=src[:, g, :, j // 2, :].unsqueeze(2).to_broadcast([P, 16, 8, 2]),
+                    )
+            nc.vector.quantize_mx(
+                out=xrc[:, 4 * q:4 * q + 4, :].rearrange("p j w -> p (j w)").bitcast(FP8X4),
+                scales=xrs[:, 4 * q:4 * q + 4, :].rearrange("p j w -> p (j w)"),
+                in_=grp[:],
+            )
+
+        rota = [["m", "vx"], ["m", "m"], ["vx", "m"]]
+        for i in range(6):
+            if i == 1:
+                pf = keep.tile([P, 96], F32, name="pf")
+                nc.vector.tensor_scalar(out=pf[:], in0=pst[:], scalar1=16.0, scalar2=None, op0=ALU.mult)
+                pp = psum.tile([P, 96], F32, name="pp", tag="st")
+                nc.tensor.matmul(pp[:], lhsT=avg_pos[:], rhs=pf[:], start=True, stop=True)
+                prm = keep.tile([P, 96], F32, name="prm")
+                nc.vector.tensor_copy(out=prm[:], in_=pp[:])
+            if i < 4:
+                repeat_x(i)
+            prep_half(i, loaded[i], rota[i % 3])
+            if i == 2:
+                for h in range(2):
+                    nc.sync.dma_start(out=ed[h][0][:], in_=ev[:, h, 0:4, :])
+            loaded.append(load_half(i + 2))
+            if i == 3:
+                period(-2)
+                period(-1)
+        for q in range(1, 4):
+            for h in range(2):
+                nc.sync.dma_start(out=ed[h][q][:], in_=ev[:, h, 4 * q:4 * q + 4, :])
+
+        u_grp = {}
+        u_ps = {}
+        for t in range(TILES + 5):
+            period(t)
+            if t < 2:
+                prep_half(6 + t, loaded[6 + t], ["vx", "vx"])
+                loaded.append(load_half(8 + t))
+            if 4 <= t < 12:
+                hu, a = (t - 4) // 4, (t - 4) % 4
+                if a == 0:
+                    u_grp[hu] = new_group_tile()
+                tr_u = psum.tile([P, 512], F32, name="tr_u", tag="tr")
+                weight_rows(loaded[8 + hu], u_grp[hu], a, tr_u[:])
+                if a == 3:
+                    weight_quantise(8 + hu, u_grp[hu])
+            if t == TILES:
+                for h in range(2):
+                    u_ps[h] = psum.tile([P, C], F32, name="u_ps", tag="m", bufs=2)
+                    for n in range(2):
+                        mx_group(u_ps[h][:, halves[n]], pair(xnc[:, h, :], xns[:, h, :], W_U, halves[n]))
+
+        y = {}
+        r = {}
+
+        def node_inverse(h):
+            nc.scalar.activation(out=sum_e[h][:], in_=sum_e[h][:], func=ACT.Ln)
+            nc.scalar.activation(out=sum_e[h][:], in_=sum_e[h][:], func=ACT.Exp, scale=-1.0)
+
+        def node_mul(h):
+            nc.vector.tensor_tensor(out=sum_ev[h][:], in0=sum_ev[h][:], in1=sum_e[h][:], op=ALU.mult)
+
+        def node_y(h):
+            y[h] = work.tile([P, C], F32, name="y", tag="en", bufs=3)
+            for n in range(2):
+                nc.vector.scalar_tensor_tensor(
+                    out=y[h][:, halves[n]], in0=sum_ev[h][:, halves[n]], scalar=1.0 / NODES,
+                    in1=u_ps[h][:, halves[n]], op0=ALU.mult, op1=ALU.add,
+                )
+                stats_half(100 + h, n, y[h][:, halves[n]])
+
+        def node_scale(h):
+            st_c3(100 + h)
+            st_c4(100 + h, prm[:, 64 + h:65 + h], prm[:, 80 + h:81 + h])
+            r[h] = work.tile([P, C], F32, name="r", tag="ex", bufs=3)
+            nc.scalar.activation(
+                out=r[h][:], in_=y[h][:], func=ACT.Relu, bias=sc[100 + h][:, 3:4], scale=sc[100 + h][:, 2:3]
+            )
+
+        def node_out(h):
+            nc.vector.tensor_tensor(out=r[h][:], in0=r[h][:], in1=y[h][:], op=ALU.add)
+            nc.sync.dma_start(out=o0[:, h, :], in_=r[h][:])
+
+        node_inverse(0)
+        node_inverse(1)
+        node_mul(0)
+        node_y(0)
+        st_c2(100)
+        node_mul(1)
+        node_scale(0)
+        node_y(1)
+        st_c2(101)
+        node_out(0)
+        node_scale(1)
+        node_out(1)

@@ -22,8 +22,7 @@ FLOPS = 2 * (4096 + 4 * 256) * 1024 * 1024
 W_E, W_A, W_B, W_V, W_U = 0, 1, 2, 3, 4
 
 SEQ = [
-    ("B0", 0), ("C2", -1), ("A3", 1), ("B1", 0), ("C3", -1), ("A1", 2), ("H", -3), ("I", -4), ("C4", -1),
-    ("F1", -2), ("D", -1), ("C1a", 0), ("VX", -2), ("C1b", 0), ("A2", 2), ("E", -1), ("F2", -2), ("G", -3),
+    ("C2", -1), ("C3", -1), ("C4", -1), ("B0", 0), ("M0", 0), ("A3", 1), ("H", -3), ("B1", 0), ("M1", 0), ("GI", -3), ("A1", 2), ("A2", 2), ("D", -1), ("E", -1), ("F1", -2), ("F2", -2), ("VX", -2),
 ]
 
 
@@ -42,7 +41,7 @@ def tile_gnn_s2_pa_t_kernel(
         keep = ctx.enter_context(tc.tile_pool(name="keep", bufs=1))
         stage = ctx.enter_context(tc.tile_pool(name="stage", bufs=2))
         work = ctx.enter_context(tc.tile_pool(name="work", bufs=2))
-        small = ctx.enter_context(tc.tile_pool(name="small", bufs=4))
+        small = ctx.enter_context(tc.tile_pool(name="small", bufs=6))
         psum = ctx.enter_context(tc.psum_pool(name="psum", bufs=1))
 
         ident = keep.tile([P, P], F32, name="ident")
@@ -59,12 +58,12 @@ def tile_gnn_s2_pa_t_kernel(
         nc.vector.tensor_scalar(
             out=avg_pos[:].rearrange("p (b l) -> p b l", l=8),
             in0=same_l[:].unsqueeze(1).to_broadcast([P, 16, 8]),
-            scalar1=1.0 / 16.0, scalar2=None, op0=ALU.mult,
+            scalar1=1.0 / 16384.0, scalar2=None, op0=ALU.mult,
         )
         nc.vector.tensor_scalar(
             out=avg_neg[:].rearrange("p (b l) -> p b l", l=8),
             in0=same_l[:].unsqueeze(1).to_broadcast([P, 16, 8]),
-            scalar1=-1.0 / 16.0, scalar2=None, op0=ALU.mult,
+            scalar1=-1.0 / 16384.0, scalar2=None, op0=ALU.mult,
         )
         eps_row = keep.tile([P, 4], F32, name="eps_row")
         nc.vector.memset(eps_row[:], 0.0)
@@ -78,9 +77,7 @@ def tile_gnn_s2_pa_t_kernel(
         xns = keep.tile([P, 2, 256], U8, name="xns", align_bytes=64)
         xrc = keep.tile([P, NODES, 256], U32, name="xrc", align_bytes=64)
         xrs = keep.tile([P, NODES, 256], U8, name="xrs", align_bytes=64)
-        ed = [[keep.tile([P, 4, C], BF16, name="ed%d_%d" % (h, q)) for q in range(4)] for h in range(2)]
-        sum_e = [keep.tile([P, C], F32, name="sum_e%d" % h) for h in range(2)]
-        sum_ev = [keep.tile([P, C], F32, name="sum_ev%d" % h) for h in range(2)]
+        sums = [keep.tile([P, 2, C], F32, name="sums%d" % h) for h in range(2)]
 
         def transpose_words(bank, src_words):
             for k in range(4):
@@ -91,46 +88,41 @@ def tile_gnn_s2_pa_t_kernel(
         def bank_view(bank):
             return bank.rearrange("p (g u r) -> p g r u", g=2, u=2)
 
-        def load_half(i):
-            w, h = i // 2, i % 2
-            wst = stage.tile([P, 4, C], BF16, name="wst", tag="wst")
+        def load_piece(k):
+            w, part = k // 4, k % 4
+            wst = stage.tile([P, 2, C], BF16, name="wst", tag="wst", bufs=4)
             nc.sync.dma_start(
-                out=wst[:], in_=weights[w][h * 512:(h + 1) * 512, :].rearrange("(a p) k -> p a k", p=P)
+                out=wst[:],
+                in_=weights[w][part * 256:(part + 1) * 256, :].rearrange("(a p) k -> p a k", p=P),
             )
             return wst
 
         def new_group_tile():
-            grp = stage.tile([P, 4096], BF16, name="grp", tag="grp", align_bytes=64)
+            grp = stage.tile([P, 2048], BF16, name="grp", tag="grp", bufs=3, align_bytes=64)
             return grp
 
-        def weight_rows(wst, grp, a, bank):
+        def weight_rows(wst, grp, a, bank, on_scalar):
             transpose_words(bank, wst[:].bitcast(F32)[:, a, :])
             dst = grp[:].bitcast(F32).rearrange("p (g c u) -> p g c u", g=2, u=2)[:, :, a * P:(a + 1) * P, :]
-            nc.scalar.copy(out=dst, in_=bank_view(bank))
+            if on_scalar:
+                nc.scalar.copy(out=dst, in_=bank_view(bank))
+            else:
+                nc.vector.tensor_copy(out=dst, in_=bank_view(bank))
 
-        def weight_quantise(i, grp):
-            w, h = i // 2, i % 2
+        def weight_quantise(k, grp):
+            w, part = k // 4, k % 4
             for g in range(2):
                 nc.vector.quantize_mx(
-                    out=wc[w][:, g, h * 512:(h + 1) * 512].bitcast(FP8X4),
-                    scales=ws[w][:, g, h * 512:(h + 1) * 512],
-                    in_=grp[:, g * 2048:(g + 1) * 2048],
+                    out=wc[w][:, g, part * 256:(part + 1) * 256].bitcast(FP8X4),
+                    scales=ws[w][:, g, part * 256:(part + 1) * 256],
+                    in_=grp[:, g * 1024:(g + 1) * 1024],
                 )
 
-        def prep_half(i, wst, tags):
-            grp = new_group_tile()
-            for a2 in range(2):
-                tag = tags[a2]
-                big = psum.tile([P, C], F32, name="big", tag=tag, bufs=(2 if tag == "m" else 1))
-                for k in range(2):
-                    weight_rows(wst, grp, 2 * a2 + k, big[:, halves[k]])
-            weight_quantise(i, grp)
-
-        def mx_group(acc, operands):
+        def mx_group(acc_ps, operands):
             last = len(operands) - 1
             for i, (lc, ls, rc, rs) in enumerate(operands):
                 nc.tensor.matmul_mx(
-                    out=acc, lhsT=lc.bitcast(FP8X4), lhsT_scale=ls, rhs=rc.bitcast(FP8X4), rhs_scale=rs,
+                    out=acc_ps, lhsT=lc.bitcast(FP8X4), lhsT_scale=ls, rhs=rc.bitcast(FP8X4), rhs_scale=rs,
                     start=(i == 0), stop=(i == last),
                 )
 
@@ -140,45 +132,64 @@ def tile_gnn_s2_pa_t_kernel(
                 for g in range(2)
             ]
 
-        tr, egrp, ecod, escl, m_ps, st6, mv, ps4, sb, sc, en, ex, exv, vx = (
-            {}, {}, {}, {}, {}, {}, {}, {}, {}, {}, {}, {}, {}, {}
+        ed, tr, egrp, ecod, escl, m_ps, acc, ps4, sb, sc, en, exx, vx = (
+            {}, {}, {}, {}, {}, {}, {}, {}, {}, {}, {}, {}, {}
         )
+
+        def load_edges(h, q, lo, hi):
+            if lo == 0:
+                ed[(h, q)] = stage.tile([P, 4, C], BF16, name="ed", tag="ed%d" % h, bufs=2)
+            nc.sync.dma_start(out=ed[(h, q)][:, lo:hi, :], in_=ev[:, h, 4 * q + lo:4 * q + hi, :])
 
         def edge_in(t):
             j, h = t // 2, t % 2
-            return ed[h][j // 4][:, j % 4, :]
+            return ed[(h, j // 4)][:, j % 4, :]
 
-        def stats_half(t, n, src):
+        def sums_half(key, n, src, ident_out):
             if n == 0:
-                st6[t] = small.tile([P, 2, 6], F32, name="st6", tag="st6")
-            nc.vector.bn_stats(out=st6[t][:, n, :], in_=src)
-            if n == 1:
-                mv[t] = small.tile([P, 2], F32, name="mv", tag="mv")
-                nc.vector.bn_aggr(out=mv[t][:], in_=st6[t][:].rearrange("p a s -> p (a s)"))
-                nc.vector.scalar_tensor_tensor(
-                    out=mv[t][:, 1:2], in0=mv[t][:, 0:1], scalar=mv[t][:, 0:1], in1=mv[t][:, 1:2],
-                    op0=ALU.mult, op1=ALU.add,
-                )
-
-        def st_c2(t):
-            ps4[t] = psum.tile([P, 4], F32, name="ps4", tag="st")
-            nc.tensor.matmul(ps4[t][:, 0:2], lhsT=avg_pos[:], rhs=mv[t][:], start=True, stop=True)
-            nc.tensor.matmul(ps4[t][:, 2:4], lhsT=avg_neg[:], rhs=mv[t][:], start=True, stop=True)
-
-        def st_c3(t):
-            sb[t] = small.tile([P, 4], F32, name="sb", tag="sb")
-            nc.vector.tensor_tensor(out=sb[t][:], in0=ps4[t][:], in1=eps_row[:], op=ALU.add)
-
-        def st_c4(t, w_col, o_col):
-            sc[t] = small.tile([P, 4], F32, name="sc", tag="sc")
-            a, b = sc[t], sb[t]
-            nc.gpsimd.tensor_scalar(
-                out=a[:, 0:1], in0=b[:, 0:1], scalar1=b[:, 2:3], scalar2=b[:, 1:2], op0=ALU.mult, op1=ALU.add
+                acc[key] = small.tile([P, 4], F32, name="acc", tag="acc")
+            nc.scalar.activation(
+                out=ident_out, in_=src, func=ACT.Identity, accum_out=acc[key][:, 2 * n:2 * n + 1]
             )
-            nc.gpsimd.tensor_tensor(out=a[:, 1:2], in0=a[:, 0:1], in1=minus_half[:], op=ALU.pow)
-            nc.gpsimd.tensor_tensor(out=a[:, 2:3], in0=a[:, 1:2], in1=w_col, op=ALU.mult)
+            junk = work.tile([P, 512], BF16, name="junk", tag="junk", bufs=2)
+            nc.scalar.activation(
+                out=junk[:], in_=src, func=ACT.Square, accum_out=acc[key][:, 2 * n + 1:2 * n + 2]
+            )
+
+        def st_c2(key):
+            ps4[key] = psum.tile([P, 4], F32, name="ps4", tag="st")
+            for i, mat in enumerate((avg_pos, avg_neg)):
+                for n in range(2):
+                    nc.tensor.matmul(
+                        ps4[key][:, 2 * i:2 * i + 2], lhsT=mat[:], rhs=acc[key][:, 2 * n:2 * n + 2],
+                        start=(n == 0), stop=(n == 1),
+                    )
+
+        def st_c3(key):
+            sb[key] = small.tile([P, 8], F32, name="sb", tag="sb")
+            b = sb[key]
+            nc.vector.tensor_tensor(out=b[:, 0:4], in0=ps4[key][:], in1=eps_row[:], op=ALU.add)
+            nc.vector.scalar_tensor_tensor(
+                out=b[:, 4:5], in0=b[:, 0:1], scalar=b[:, 2:3], in1=b[:, 1:2], op0=ALU.mult, op1=ALU.add
+            )
+
+        def st_c4(key, w_col, o_col):
+            sc[key] = small.tile([P, 4], F32, name="sc", tag="sc")
+            a, b = sc[key], sb[key]
+            nc.gpsimd.tensor_tensor(out=a[:, 0:1], in0=b[:, 4:5], in1=minus_half[:], op=ALU.pow)
+            nc.gpsimd.tensor_tensor(out=a[:, 1:2], in0=a[:, 0:1], in1=w_col, op=ALU.mult)
             nc.gpsimd.tensor_scalar(
-                out=a[:, 3:4], in0=a[:, 2:3], scalar1=b[:, 2:3], scalar2=o_col, op0=ALU.mult, op1=ALU.add
+                out=a[:, 2:3], in0=a[:, 1:2], scalar1=b[:, 0:1], scalar2=o_col, op0=ALU.mult, op1=ALU.subtract
+            )
+
+        def norm_relu(key, dst, src):
+            nc.vector.tensor_scalar(
+                out=dst, in0=src, scalar1=sc[key][:, 1:2], scalar2=sc[key][:, 2:3], op0=ALU.mult, op1=ALU.max
+            )
+
+        def add_back(key, dst, src, other):
+            nc.vector.scalar_tensor_tensor(
+                out=dst, in0=src, scalar=sc[key][:, 2:3], in1=other, op0=ALU.subtract, op1=ALU.add
             )
 
         def st_a1(t):
@@ -198,68 +209,61 @@ def tile_gnn_s2_pa_t_kernel(
 
         def st_b(t, n):
             j, h = t // 2, t % 2
-            if n == 0:
-                m_ps[t] = psum.tile([P, C], F32, name="m_ps", tag="m", bufs=2)
+            m_ps[(t, n)] = psum.tile([P, 512], F32, name="m_ps", tag="m", bufs=4)
             mx_group(
-                m_ps[t][:, halves[n]],
+                m_ps[(t, n)][:],
                 pair(ecod[t], escl[t], W_E, halves[n])
                 + pair(xnc[:, h, :], xns[:, h, :], W_A, halves[n])
                 + pair(xrc[:, j, :], xrs[:, j, :], W_B, halves[n]),
             )
 
+        def st_m(t, n):
+            if n == 0:
+                en[t] = work.tile([P, C], F32, name="en", tag="en", bufs=5)
+            sums_half(t, n, m_ps[(t, n)][:], en[t][:, halves[n]])
+
         def st_d(t):
-            en[t] = work.tile([P, C], F32, name="en", tag="en", bufs=3)
-            for n in range(2):
-                nc.scalar.activation(
-                    out=en[t][:, halves[n]], in_=m_ps[t][:, halves[n]], func=ACT.Relu,
-                    bias=sc[t][:, 3:4], scale=sc[t][:, 2:3],
-                )
+            norm_relu(t, en[t][:], en[t][:])
 
         def st_e(t):
             j, h = t // 2, t % 2
-            nc.vector.tensor_tensor(out=en[t][:], in0=en[t][:], in1=edge_in(t), op=ALU.add)
+            add_back(t, en[t][:], en[t][:], edge_in(t))
             nc.sync.dma_start(out=o1[:, h, j, :], in_=en[t][:])
 
         def st_f1(t):
             if t < 2:
-                ex[t] = sum_e[t]
+                exx[t] = sums[t]
             else:
-                ex[t] = work.tile([P, C], F32, name="ex", tag="ex", bufs=3)
-            nc.scalar.activation(out=ex[t][:], in_=en[t][:], func=ACT.Tanh, scale=0.5)
+                exx[t] = work.tile([P, 2, C], F32, name="exx", tag="exx", bufs=3)
+            nc.scalar.activation(out=exx[t][:, 0, :], in_=en[t][:], func=ACT.Tanh, scale=0.5)
 
         def st_f2(t):
-            nc.scalar.activation(out=ex[t][:], in_=ex[t][:], func=ACT.Exp, scale=0.5)
-
-        def st_g(t):
-            if t >= 2:
-                for n in range(2):
-                    nc.gpsimd.tensor_tensor(
-                        out=sum_e[t % 2][:, halves[n]], in0=sum_e[t % 2][:, halves[n]], in1=ex[t][:, halves[n]],
-                        op=ALU.add,
-                    )
+            nc.scalar.activation(out=exx[t][:, 0, :], in_=exx[t][:, 0, :], func=ACT.Exp, scale=0.5)
 
         def st_h(t):
-            if t < 2:
-                exv[t] = sum_ev[t]
-            else:
-                exv[t] = work.tile([P, C], F32, name="exv", tag="exv", bufs=2)
             for n in range(2):
                 nc.vector.tensor_tensor(
-                    out=exv[t][:, halves[n]], in0=ex[t][:, halves[n]], in1=vx[t // 2][:, halves[n]], op=ALU.mult
+                    out=exx[t][:, 1, halves[n]], in0=exx[t][:, 0, halves[n]], in1=vx[t // 2][:, halves[n]],
+                    op=ALU.mult,
                 )
 
-        def st_i(t):
+        def st_gi(t):
             if t >= 2:
-                nc.vector.tensor_tensor(out=sum_ev[t % 2][:], in0=sum_ev[t % 2][:], in1=exv[t][:], op=ALU.add)
+                nc.vector.tensor_tensor(out=sums[t % 2][:], in0=sums[t % 2][:], in1=exx[t][:], op=ALU.add)
 
         def st_vx(j):
             vx[j] = psum.tile([P, C], F32, name="vx_ps", tag="vx")
             for n in range(2):
                 mx_group(vx[j][:, halves[n]], pair(xrc[:, j, :], xrs[:, j, :], W_V, halves[n]))
 
-        def edge_cols(t):
+        def st_c4_edge(t):
             col = (t % 2) * NODES + t // 2
-            return prm[:, col:col + 1], prm[:, 32 + col:33 + col]
+            st_c4(t, prm[:, col:col + 1], prm[:, 32 + col:33 + col])
+
+        stages = {
+            "A1": st_a1, "A2": st_a2, "A3": st_a3, "C2": st_c2, "C3": st_c3, "C4": st_c4_edge, "D": st_d,
+            "E": st_e, "F1": st_f1, "F2": st_f2, "H": st_h, "GI": st_gi,
+        }
 
         def period(t):
             for name, off in SEQ:
@@ -267,75 +271,47 @@ def tile_gnn_s2_pa_t_kernel(
                 if name == "VX":
                     if s >= 0 and s % 2 == 0 and s // 2 < NODES:
                         st_vx(s // 2)
-                    continue
-                if s < 0 or s >= TILES:
-                    continue
-                if name == "A1":
-                    st_a1(s)
-                elif name == "A2":
-                    st_a2(s)
-                elif name == "A3":
-                    st_a3(s)
-                elif name == "B0":
-                    st_b(s, 0)
-                elif name == "B1":
-                    st_b(s, 1)
-                elif name == "C1a":
-                    stats_half(s, 0, m_ps[s][:, halves[0]])
-                elif name == "C1b":
-                    stats_half(s, 1, m_ps[s][:, halves[1]])
-                elif name == "C2":
-                    st_c2(s)
-                elif name == "C3":
-                    st_c3(s)
-                elif name == "C4":
-                    w_col, o_col = edge_cols(s)
-                    st_c4(s, w_col, o_col)
-                elif name == "D":
-                    st_d(s)
-                elif name == "E":
-                    st_e(s)
-                elif name == "F1":
-                    st_f1(s)
-                elif name == "F2":
-                    st_f2(s)
-                elif name == "G":
-                    st_g(s)
-                elif name == "H":
-                    st_h(s)
-                elif name == "I":
-                    st_i(s)
+                elif 0 <= s < TILES:
+                    if name in ("B0", "B1"):
+                        st_b(s, int(name[1]))
+                    elif name in ("M0", "M1"):
+                        st_m(s, int(name[1]))
+                    else:
+                        stages[name](s)
 
-        xs = work.tile([P, 2, C], BF16, name="xs", tag="en", bufs=3)
-        nc.sync.dma_start(out=xs[:], in_=xv)
         pst = keep.tile([P, 96], BF16, name="pst")
         nc.vector.memset(pst[:], 0.0)
         nc.sync.dma_start(out=pst[0:8, 0:32], in_=bne_w.rearrange("(l x) -> l x", l=8))
         nc.sync.dma_start(out=pst[0:8, 32:64], in_=bne_b.rearrange("(l x) -> l x", l=8))
         nc.sync.dma_start(out=pst[0:8, 64:66], in_=bnv_w.rearrange("(l x) -> l x", l=8))
         nc.sync.dma_start(out=pst[0:8, 80:82], in_=bnv_b.rearrange("(l x) -> l x", l=8))
-        loaded = [load_half(0), load_half(1)]
+        xs = work.tile([P, 2, C], BF16, name="xs", tag="en", bufs=5)
+        nc.sync.dma_start(out=xs[:], in_=xv)
+        loaded = [load_piece(k) for k in range(4)]
+        pf = keep.tile([P, 96], F32, name="pf")
+        nc.vector.tensor_scalar(out=pf[:], in0=pst[:], scalar1=16384.0, scalar2=None, op0=ALU.mult)
+        pp = psum.tile([P, 96], F32, name="pp", tag="st")
+        nc.tensor.matmul(pp[:], lhsT=avg_pos[:], rhs=pf[:], start=True, stop=True)
+        prm = keep.tile([P, 96], F32, name="prm")
+        nc.vector.tensor_copy(out=prm[:], in_=pp[:])
 
-        xbank = psum.tile([P, C], F32, name="xbank", tag="m", bufs=2)
         xg = []
         for h in range(2):
-            transpose_words(xbank[:, halves[h]], xs[:].bitcast(F32)[:, h, :])
-            g_t = work.tile([P, C], BF16, name="xg", tag="egrp", align_bytes=64)
+            xbank = psum.tile([P, 512], F32, name="xbank", tag="m", bufs=4)
+            transpose_words(xbank[:], xs[:].bitcast(F32)[:, h, :])
+            g_t = keep.tile([P, C], BF16, name="xg%d" % h, align_bytes=64)
             nc.scalar.copy(
-                out=g_t[:].bitcast(F32).rearrange("p (g r u) -> p g r u", g=2, u=2),
-                in_=bank_view(xbank[:, halves[h]]),
+                out=g_t[:].bitcast(F32).rearrange("p (g r u) -> p g r u", g=2, u=2), in_=bank_view(xbank[:])
             )
             xg.append(g_t)
         for h in range(2):
             nc.vector.quantize_mx(out=xnc[:, h, :].bitcast(FP8X4), scales=xns[:, h, :], in_=xg[h][:])
 
         def repeat_x(q):
-            grp = new_group_tile()
-            dst = grp[:].bitcast(F32).rearrange(
-                "p (jj g b l u) -> p jj g b l u", jj=4, g=2, b=16, l=8, u=2
-            )
-            for jj in range(4):
-                j = 4 * q + jj
+            rep = stage.tile([P, 2048], BF16, name="rep", tag="rep", bufs=2, align_bytes=64)
+            dst = rep[:].bitcast(F32).rearrange("p (jj g b l u) -> p jj g b l u", jj=2, g=2, b=16, l=8, u=2)
+            for jj in range(2):
+                j = 2 * q + jj
                 src = xg[j % 2][:].bitcast(F32).rearrange("p (g b l u) -> p g b l u", g=2, b=16, l=8, u=2)
                 for g in range(2):
                     nc.vector.tensor_copy(
@@ -343,95 +319,100 @@ def tile_gnn_s2_pa_t_kernel(
                         in_=src[:, g, :, j // 2, :].unsqueeze(2).to_broadcast([P, 16, 8, 2]),
                     )
             nc.vector.quantize_mx(
-                out=xrc[:, 4 * q:4 * q + 4, :].rearrange("p j w -> p (j w)").bitcast(FP8X4),
-                scales=xrs[:, 4 * q:4 * q + 4, :].rearrange("p j w -> p (j w)"),
-                in_=grp[:],
+                out=xrc[:, 2 * q:2 * q + 2, :].rearrange("p j w -> p (j w)").bitcast(FP8X4),
+                scales=xrs[:, 2 * q:2 * q + 2, :].rearrange("p j w -> p (j w)"),
+                in_=rep[:],
             )
 
-        rota = [["m", "vx"], ["m", "m"], ["vx", "m"]]
-        for i in range(6):
-            if i == 1:
-                pf = keep.tile([P, 96], F32, name="pf")
-                nc.vector.tensor_scalar(out=pf[:], in0=pst[:], scalar1=16.0, scalar2=None, op0=ALU.mult)
-                pp = psum.tile([P, 96], F32, name="pp", tag="st")
-                nc.tensor.matmul(pp[:], lhsT=avg_pos[:], rhs=pf[:], start=True, stop=True)
-                prm = keep.tile([P, 96], F32, name="prm")
-                nc.vector.tensor_copy(out=prm[:], in_=pp[:])
-            if i < 4:
-                repeat_x(i)
-            prep_half(i, loaded[i], rota[i % 3])
-            if i == 2:
+        def prep_piece(k, banks, on_scalar):
+            grp = new_group_tile()
+            for a in range(2):
+                weight_rows(loaded[k], grp, a, banks[a], on_scalar)
+            weight_quantise(k, grp)
+
+        def ring_banks():
+            b0 = psum.tile([P, 512], F32, name="wb0", tag="m", bufs=4)
+            b1 = psum.tile([P, 512], F32, name="wb1", tag="m", bufs=4)
+            return [b0[:], b1[:]]
+
+        for k in range(12):
+            if k % 2 == 0:
+                repeat_x(k // 2)
+            prep_piece(k, ring_banks(), True)
+            if k == 4:
                 for h in range(2):
-                    nc.sync.dma_start(out=ed[h][0][:], in_=ev[:, h, 0:4, :])
-            loaded.append(load_half(i + 2))
-            if i == 3:
+                    load_edges(h, 0, 0, 1)
+            if k == 8:
+                for h in range(2):
+                    load_edges(h, 0, 1, 2)
+            loaded.append(load_piece(k + 4))
+            if k == 7:
                 period(-2)
                 period(-1)
-        for q in range(1, 4):
-            for h in range(2):
-                nc.sync.dma_start(out=ed[h][q][:], in_=ev[:, h, 4 * q:4 * q + 4, :])
+        for h in range(2):
+            load_edges(h, 0, 2, 4)
+        for h in range(2):
+            load_edges(h, 1, 0, 4)
 
         u_grp = {}
         u_ps = {}
-        for t in range(TILES + 5):
+        for t in range(TILES + 4):
             period(t)
             if t < 2:
-                prep_half(6 + t, loaded[6 + t], ["vx", "vx"])
-                loaded.append(load_half(8 + t))
+                for k in (12 + 2 * t, 13 + 2 * t):
+                    big = psum.tile([P, C], F32, name="big", tag="vx")
+                    prep_piece(k, [big[:, halves[0]], big[:, halves[1]]], False)
+                    loaded.append(load_piece(k + 4))
+            if t in (12, 13):
+                repeat_x(t - 6)
             if 4 <= t < 12:
-                hu, a = (t - 4) // 4, (t - 4) % 4
+                k, a = 16 + (t - 4) // 2, (t - 4) % 2
                 if a == 0:
-                    u_grp[hu] = new_group_tile()
+                    u_grp[k] = new_group_tile()
                 tr_u = psum.tile([P, 512], F32, name="tr_u", tag="tr")
-                weight_rows(loaded[8 + hu], u_grp[hu], a, tr_u[:])
-                if a == 3:
-                    weight_quantise(8 + hu, u_grp[hu])
+                weight_rows(loaded[k], u_grp[k], a, tr_u[:], True)
+                if a == 1:
+                    weight_quantise(k, u_grp[k])
+            if t in (9, 17):
+                for h in range(2):
+                    load_edges(h, (t + 7) // 8, 0, 4)
             if t == TILES:
                 for h in range(2):
-                    u_ps[h] = psum.tile([P, C], F32, name="u_ps", tag="m", bufs=2)
                     for n in range(2):
-                        mx_group(u_ps[h][:, halves[n]], pair(xnc[:, h, :], xns[:, h, :], W_U, halves[n]))
+                        u_ps[(h, n)] = psum.tile([P, 512], F32, name="u_ps", tag="m", bufs=4)
+                        mx_group(u_ps[(h, n)][:], pair(xnc[:, h, :], xns[:, h, :], W_U, halves[n]))
 
         y = {}
         r = {}
 
         def node_inverse(h):
-            nc.scalar.activation(out=sum_e[h][:], in_=sum_e[h][:], func=ACT.Ln)
-            nc.scalar.activation(out=sum_e[h][:], in_=sum_e[h][:], func=ACT.Exp, scale=-1.0)
-
-        def node_mul(h):
-            nc.vector.tensor_tensor(out=sum_ev[h][:], in0=sum_ev[h][:], in1=sum_e[h][:], op=ALU.mult)
+            nc.scalar.activation(out=sums[h][:, 0, :], in_=sums[h][:, 0, :], func=ACT.Ln)
+            nc.scalar.activation(out=sums[h][:, 0, :], in_=sums[h][:, 0, :], func=ACT.Exp, scale=-1.0)
 
         def node_y(h):
-            y[h] = work.tile([P, C], F32, name="y", tag="en", bufs=3)
+            nc.vector.tensor_tensor(out=sums[h][:, 1, :], in0=sums[h][:, 1, :], in1=sums[h][:, 0, :], op=ALU.mult)
+            y[h] = work.tile([P, C], F32, name="y", tag="en", bufs=5)
             for n in range(2):
                 nc.vector.scalar_tensor_tensor(
-                    out=y[h][:, halves[n]], in0=sum_ev[h][:, halves[n]], scalar=1.0 / NODES,
-                    in1=u_ps[h][:, halves[n]], op0=ALU.mult, op1=ALU.add,
+                    out=y[h][:, halves[n]], in0=sums[h][:, 1, halves[n]], scalar=1.0 / NODES,
+                    in1=u_ps[(h, n)][:], op0=ALU.mult, op1=ALU.add,
                 )
-                stats_half(100 + h, n, y[h][:, halves[n]])
-
-        def node_scale(h):
-            st_c3(100 + h)
-            st_c4(100 + h, prm[:, 64 + h:65 + h], prm[:, 80 + h:81 + h])
-            r[h] = work.tile([P, C], F32, name="r", tag="ex", bufs=3)
-            nc.scalar.activation(
-                out=r[h][:], in_=y[h][:], func=ACT.Relu, bias=sc[100 + h][:, 3:4], scale=sc[100 + h][:, 2:3]
-            )
+                junk2 = work.tile([P, 512], BF16, name="junk2", tag="junk2", bufs=2)
+                sums_half(100 + h, n, y[h][:, halves[n]], junk2[:])
 
         def node_out(h):
-            nc.vector.tensor_tensor(out=r[h][:], in0=r[h][:], in1=y[h][:], op=ALU.add)
+            st_c3(100 + h)
+            st_c4(100 + h, prm[:, 64 + h:65 + h], prm[:, 80 + h:81 + h])
+            r[h] = work.tile([P, C], F32, name="r", tag="en", bufs=5)
+            norm_relu(100 + h, r[h][:], y[h][:])
+            add_back(100 + h, r[h][:], r[h][:], y[h][:])
             nc.sync.dma_start(out=o0[:, h, :], in_=r[h][:])
 
         node_inverse(0)
         node_inverse(1)
-        node_mul(0)
         node_y(0)
         st_c2(100)
-        node_mul(1)
-        node_scale(0)
         node_y(1)
-        st_c2(101)
         node_out(0)
-        node_scale(1)
+        st_c2(101)
         node_out(1)

@@ -22,7 +22,7 @@ FLOPS = 2 * (4096 + 4 * 256) * 1024 * 1024
 W_E, W_A, W_B, W_V, W_U = 0, 1, 2, 3, 4
 
 SEQ = [
-    ("C2", -1), ("C3", -1), ("C4", -1), ("B0", 0), ("M0", 0), ("A3", 1), ("H", -3), ("B1", 0), ("M1", 0), ("GI", -3), ("A1", 2), ("A2", 2), ("D", -1), ("E", -1), ("F1", -2), ("F2", -2), ("VX", -2),
+    ("C2", -1), ("A1", 2), ("XP", 0), ("C3", -1), ("XQ", 0), ("M1", 0), ("B0", 1), ("C4", -1), ("A2", 2), ("XS", 0), ("F1", -2), ("B1", 1), ("F2", -2), ("H", -4), ("VX", -3), ("M0", 1), ("GI", -4), ("A3", 2), ("D", -1), ("E", -1),
 ]
 
 
@@ -193,7 +193,7 @@ def tile_gnn_s2_pa_t_kernel(
             )
 
         def st_a1(t):
-            tr[t] = psum.tile([P, 512], F32, name="tr", tag="tr")
+            tr[t] = psum.tile([P, 512], F32, name="tr", tag="tr", bufs=2)
             transpose_words(tr[t], edge_in(t).bitcast(F32))
 
         def st_a2(t):
@@ -209,7 +209,7 @@ def tile_gnn_s2_pa_t_kernel(
 
         def st_b(t, n):
             j, h = t // 2, t % 2
-            m_ps[(t, n)] = psum.tile([P, 512], F32, name="m_ps", tag="m", bufs=4)
+            m_ps[(t, n)] = psum.tile([P, 512], F32, name="m_ps", tag="m", bufs=3)
             mx_group(
                 m_ps[(t, n)][:],
                 pair(ecod[t], escl[t], W_E, halves[n])
@@ -243,7 +243,7 @@ def tile_gnn_s2_pa_t_kernel(
         def st_h(t):
             for n in range(2):
                 nc.vector.tensor_tensor(
-                    out=exx[t][:, 1, halves[n]], in0=exx[t][:, 0, halves[n]], in1=vx[t // 2][:, halves[n]],
+                    out=exx[t][:, 1, halves[n]], in0=exx[t][:, 0, halves[n]], in1=vx[(t // 2, n)][:],
                     op=ALU.mult,
                 )
 
@@ -252,9 +252,9 @@ def tile_gnn_s2_pa_t_kernel(
                 nc.vector.tensor_tensor(out=sums[t % 2][:], in0=sums[t % 2][:], in1=exx[t][:], op=ALU.add)
 
         def st_vx(j):
-            vx[j] = psum.tile([P, C], F32, name="vx_ps", tag="vx")
             for n in range(2):
-                mx_group(vx[j][:, halves[n]], pair(xrc[:, j, :], xrs[:, j, :], W_V, halves[n]))
+                vx[(j, n)] = psum.tile([P, 512], F32, name="vx_ps", tag="vx", bufs=2)
+                mx_group(vx[(j, n)][:], pair(xrc[:, j, :], xrs[:, j, :], W_V, halves[n]))
 
         def st_c4_edge(t):
             col = (t % 2) * NODES + t // 2
@@ -268,7 +268,9 @@ def tile_gnn_s2_pa_t_kernel(
         def period(t):
             for name, off in SEQ:
                 s = t + off
-                if name == "VX":
+                if name in ("XP", "XS", "XQ"):
+                    late_weights(name, t)
+                elif name == "VX":
                     if s >= 0 and s % 2 == 0 and s // 2 < NODES:
                         st_vx(s // 2)
                 elif 0 <= s < TILES:
@@ -295,9 +297,18 @@ def tile_gnn_s2_pa_t_kernel(
         prm = keep.tile([P, 96], F32, name="prm")
         nc.vector.tensor_copy(out=prm[:], in_=pp[:])
 
+        rotation = [("m", 3), ("vx", 2), ("tr", 2), ("m", 3), ("vx", 2), ("tr", 2), ("m", 3)]
+        n_banks = [0]
+
+        def next_bank():
+            tag, bufs = rotation[n_banks[0] % 7]
+            n_banks[0] += 1
+            bank = psum.tile([P, 512], F32, name="bank", tag=tag, bufs=bufs)
+            return bank
+
         xg = []
         for h in range(2):
-            xbank = psum.tile([P, 512], F32, name="xbank", tag="m", bufs=4)
+            xbank = next_bank()
             transpose_words(xbank[:], xs[:].bitcast(F32)[:, h, :])
             g_t = keep.tile([P, C], BF16, name="xg%d" % h, align_bytes=64)
             nc.scalar.copy(
@@ -331,9 +342,43 @@ def tile_gnn_s2_pa_t_kernel(
             weight_quantise(k, grp)
 
         def ring_banks():
-            b0 = psum.tile([P, 512], F32, name="wb0", tag="m", bufs=4)
-            b1 = psum.tile([P, 512], F32, name="wb1", tag="m", bufs=4)
+            b0 = next_bank()
+            b1 = next_bank()
             return [b0[:], b1[:]]
+
+        late = {}
+        u_grp = {}
+
+        def late_weights(name, t):
+            if -1 <= t <= 2:
+                k = 13 + t
+                if name == "XP":
+                    late[k] = [psum.tile([P, 512], F32, name="wv_b", tag="vx", bufs=2) for a in range(2)]
+                    for a in range(2):
+                        transpose_words(late[k][a][:], loaded[k][:].bitcast(F32)[:, a, :])
+                    loaded.append(load_piece(k + 4))
+                elif name == "XS":
+                    u_grp[k] = new_group_tile()
+                    for a in range(2):
+                        evacuate_rows(u_grp[k], a, late[k][a][:])
+            if 4 <= t < 12:
+                k, a = 16 + (t - 4) // 2, (t - 4) % 2
+                if name == "XP":
+                    late[(k, a)] = psum.tile([P, 512], F32, name="wu_b", tag="tr", bufs=2)
+                    transpose_words(late[(k, a)][:], loaded[k][:].bitcast(F32)[:, a, :])
+                elif name == "XS":
+                    if a == 0:
+                        u_grp[k] = new_group_tile()
+                    evacuate_rows(u_grp[k], a, late[(k, a)][:])
+            if name == "XQ":
+                if 0 <= t <= 3:
+                    weight_quantise(12 + t, u_grp[12 + t])
+                if 6 <= t <= 12 and t % 2 == 0:
+                    weight_quantise(13 + t // 2, u_grp[13 + t // 2])
+
+        def evacuate_rows(grp, a, bank):
+            dst = grp[:].bitcast(F32).rearrange("p (g c u) -> p g c u", g=2, u=2)[:, :, a * P:(a + 1) * P, :]
+            nc.scalar.copy(out=dst, in_=bank_view(bank))
 
         for k in range(12):
             if k % 2 == 0:
@@ -348,42 +393,30 @@ def tile_gnn_s2_pa_t_kernel(
             loaded.append(load_piece(k + 4))
             if k == 7:
                 period(-2)
-                period(-1)
         for h in range(2):
             load_edges(h, 0, 2, 4)
         for h in range(2):
             load_edges(h, 1, 0, 4)
 
-        u_grp = {}
+        period(-1)
         u_ps = {}
-        for t in range(TILES + 4):
+        for t in range(TILES + 5):
             period(t)
-            if t < 2:
-                for k in (12 + 2 * t, 13 + 2 * t):
-                    big = psum.tile([P, C], F32, name="big", tag="vx")
-                    prep_piece(k, [big[:, halves[0]], big[:, halves[1]]], False)
-                    loaded.append(load_piece(k + 4))
-            if t in (12, 13):
-                repeat_x(t - 6)
-            if 4 <= t < 12:
-                k, a = 16 + (t - 4) // 2, (t - 4) % 2
-                if a == 0:
-                    u_grp[k] = new_group_tile()
-                tr_u = psum.tile([P, 512], F32, name="tr_u", tag="tr")
-                weight_rows(loaded[k], u_grp[k], a, tr_u[:], True)
-                if a == 1:
-                    weight_quantise(k, u_grp[k])
+            if t in (0, 1):
+                repeat_x(t + 6)
             if t in (9, 17):
                 for h in range(2):
                     load_edges(h, (t + 7) // 8, 0, 4)
             if t == TILES:
                 for h in range(2):
                     for n in range(2):
-                        u_ps[(h, n)] = psum.tile([P, 512], F32, name="u_ps", tag="m", bufs=4)
+                        u_tag, u_bufs = (("m", 3), ("m", 3), ("m", 3), ("tr", 2))[2 * h + n]
+                        u_ps[(h, n)] = psum.tile([P, 512], F32, name="u_ps", tag=u_tag, bufs=u_bufs)
                         mx_group(u_ps[(h, n)][:], pair(xnc[:, h, :], xns[:, h, :], W_U, halves[n]))
 
         y = {}
         r = {}
+        st6 = {}
 
         def node_inverse(h):
             nc.scalar.activation(out=sums[h][:, 0, :], in_=sums[h][:, 0, :], func=ACT.Ln)
@@ -392,13 +425,23 @@ def tile_gnn_s2_pa_t_kernel(
         def node_y(h):
             nc.vector.tensor_tensor(out=sums[h][:, 1, :], in0=sums[h][:, 1, :], in1=sums[h][:, 0, :], op=ALU.mult)
             y[h] = work.tile([P, C], F32, name="y", tag="en", bufs=5)
+            st6[h] = small.tile([P, 2, 6], F32, name="st6", tag="st6")
             for n in range(2):
                 nc.vector.scalar_tensor_tensor(
                     out=y[h][:, halves[n]], in0=sums[h][:, 1, halves[n]], scalar=1.0 / NODES,
                     in1=u_ps[(h, n)][:], op0=ALU.mult, op1=ALU.add,
                 )
-                junk2 = work.tile([P, 512], BF16, name="junk2", tag="junk2", bufs=2)
-                sums_half(100 + h, n, y[h][:, halves[n]], junk2[:])
+                nc.vector.bn_stats(out=st6[h][:, n, :], in_=y[h][:, halves[n]])
+            mv = small.tile([P, 2], F32, name="mv", tag="mv")
+            nc.vector.bn_aggr(out=mv[:], in_=st6[h][:].rearrange("p a s -> p (a s)"))
+            nc.vector.scalar_tensor_tensor(
+                out=mv[:, 1:2], in0=mv[:, 0:1], scalar=mv[:, 0:1], in1=mv[:, 1:2], op0=ALU.mult, op1=ALU.add
+            )
+            acc[100 + h] = small.tile([P, 4], F32, name="acc", tag="acc")
+            for n in range(2):
+                nc.vector.tensor_scalar(
+                    out=acc[100 + h][:, 2 * n:2 * n + 2], in0=mv[:], scalar1=512.0, scalar2=None, op0=ALU.mult
+                )
 
         def node_out(h):
             st_c3(100 + h)

@@ -22,7 +22,7 @@ FLOPS = 2 * (4096 + 4 * 256) * 1024 * 1024
 W_E, W_A, W_B, W_V, W_U = 0, 1, 2, 3, 4
 
 SEQ = [
-    ("C2", -1), ("A1", 2), ("XP", 0), ("C3", -1), ("XQ", 0), ("M1", 0), ("B0", 1), ("C4", -1), ("A2", 2), ("XS", 0), ("F1", -2), ("B1", 1), ("F2", -2), ("H", -4), ("VX", -3), ("M0", 1), ("GI", -4), ("A3", 2), ("D", -1), ("E", -1),
+    ("C2", -1), ("Gv", -5), ("M1", 0), ("XS", -1), ("H", -4), ("F1", -3), ("F2", -3), ("C3", -1), ("XQ", -2), ("A2", 3), ("B0", 1), ("B1", 1), ("E", -2), ("VX", -3), ("Ge", -4), ("A3", 3), ("C4", -1), ("M0", 1), ("A1", 4), ("XP", 0), ("D", -1),
 ]
 
 
@@ -136,14 +136,14 @@ def tile_gnn_s2_pa_t_kernel(
             {}, {}, {}, {}, {}, {}, {}, {}, {}, {}, {}, {}, {}
         )
 
-        def load_edges(h, q, lo, hi):
-            if lo == 0:
-                ed[(h, q)] = stage.tile([P, 4, C], BF16, name="ed", tag="ed%d" % h, bufs=2)
-            nc.sync.dma_start(out=ed[(h, q)][:, lo:hi, :], in_=ev[:, h, 4 * q + lo:4 * q + hi, :])
+        def load_edges(q):
+            for h in range(2):
+                ed[(h, q)] = stage.tile([P, 2, C], BF16, name="ed", tag="ed%d" % h, bufs=4)
+                nc.sync.dma_start(out=ed[(h, q)][:], in_=ev[:, h, 2 * q:2 * q + 2, :])
 
         def edge_in(t):
             j, h = t // 2, t % 2
-            return ed[(h, j // 4)][:, j % 4, :]
+            return ed[(h, j // 2)][:, j % 2, :]
 
         def sums_half(key, n, src, ident_out):
             if n == 0:
@@ -182,8 +182,8 @@ def tile_gnn_s2_pa_t_kernel(
                 out=a[:, 2:3], in0=a[:, 1:2], scalar1=b[:, 0:1], scalar2=o_col, op0=ALU.mult, op1=ALU.subtract
             )
 
-        def norm_relu(key, dst, src):
-            nc.vector.tensor_scalar(
+        def norm_relu(engine, key, dst, src):
+            engine.tensor_scalar(
                 out=dst, in0=src, scalar1=sc[key][:, 1:2], scalar2=sc[key][:, 2:3], op0=ALU.mult, op1=ALU.max
             )
 
@@ -198,7 +198,7 @@ def tile_gnn_s2_pa_t_kernel(
 
         def st_a2(t):
             egrp[t] = work.tile([P, C], BF16, name="egrp", tag="egrp", align_bytes=64)
-            nc.scalar.copy(
+            nc.vector.tensor_copy(
                 out=egrp[t][:].bitcast(F32).rearrange("p (g r u) -> p g r u", g=2, u=2), in_=bank_view(tr[t])
             )
 
@@ -223,7 +223,7 @@ def tile_gnn_s2_pa_t_kernel(
             sums_half(t, n, m_ps[(t, n)][:], en[t][:, halves[n]])
 
         def st_d(t):
-            norm_relu(t, en[t][:], en[t][:])
+            norm_relu(nc.gpsimd, t, en[t][:], en[t][:])
 
         def st_e(t):
             j, h = t // 2, t % 2
@@ -247,9 +247,17 @@ def tile_gnn_s2_pa_t_kernel(
                     op=ALU.mult,
                 )
 
-        def st_gi(t):
+        def st_ge(t):
             if t >= 2:
-                nc.vector.tensor_tensor(out=sums[t % 2][:], in0=sums[t % 2][:], in1=exx[t][:], op=ALU.add)
+                nc.gpsimd.tensor_tensor(
+                    out=sums[t % 2][:, 0, :], in0=sums[t % 2][:, 0, :], in1=exx[t][:, 0, :], op=ALU.add
+                )
+
+        def st_gv(t):
+            if t >= 2:
+                nc.vector.tensor_tensor(
+                    out=sums[t % 2][:, 1, :], in0=sums[t % 2][:, 1, :], in1=exx[t][:, 1, :], op=ALU.add
+                )
 
         def st_vx(j):
             for n in range(2):
@@ -262,14 +270,14 @@ def tile_gnn_s2_pa_t_kernel(
 
         stages = {
             "A1": st_a1, "A2": st_a2, "A3": st_a3, "C2": st_c2, "C3": st_c3, "C4": st_c4_edge, "D": st_d,
-            "E": st_e, "F1": st_f1, "F2": st_f2, "H": st_h, "GI": st_gi,
+            "E": st_e, "F1": st_f1, "F2": st_f2, "H": st_h, "Ge": st_ge, "Gv": st_gv,
         }
 
         def period(t):
             for name, off in SEQ:
                 s = t + off
                 if name in ("XP", "XS", "XQ"):
-                    late_weights(name, t)
+                    late_weights(name, s)
                 elif name == "VX":
                     if s >= 0 and s % 2 == 0 and s // 2 < NODES:
                         st_vx(s // 2)
@@ -297,11 +305,11 @@ def tile_gnn_s2_pa_t_kernel(
         prm = keep.tile([P, 96], F32, name="prm")
         nc.vector.tensor_copy(out=prm[:], in_=pp[:])
 
-        rotation = [("m", 3), ("vx", 2), ("tr", 2), ("m", 3), ("vx", 2), ("tr", 2), ("m", 3)]
+        rotation = [("m", 3), ("vx", 2), ("m", 3), ("vx", 2), ("m", 3)]
         n_banks = [0]
 
         def next_bank():
-            tag, bufs = rotation[n_banks[0] % 7]
+            tag, bufs = rotation[n_banks[0] % 5]
             n_banks[0] += 1
             bank = psum.tile([P, 512], F32, name="bank", tag=tag, bufs=bufs)
             return bank
@@ -350,8 +358,8 @@ def tile_gnn_s2_pa_t_kernel(
         u_grp = {}
 
         def late_weights(name, t):
-            if -1 <= t <= 2:
-                k = 13 + t
+            if -2 <= t <= 1:
+                k = 14 + t
                 if name == "XP":
                     late[k] = [psum.tile([P, 512], F32, name="wv_b", tag="vx", bufs=2) for a in range(2)]
                     for a in range(2):
@@ -361,6 +369,8 @@ def tile_gnn_s2_pa_t_kernel(
                     u_grp[k] = new_group_tile()
                     for a in range(2):
                         evacuate_rows(u_grp[k], a, late[k][a][:])
+                else:
+                    weight_quantise(k, u_grp[k])
             if 4 <= t < 12:
                 k, a = 16 + (t - 4) // 2, (t - 4) % 2
                 if name == "XP":
@@ -370,11 +380,8 @@ def tile_gnn_s2_pa_t_kernel(
                     if a == 0:
                         u_grp[k] = new_group_tile()
                     evacuate_rows(u_grp[k], a, late[(k, a)][:])
-            if name == "XQ":
-                if 0 <= t <= 3:
-                    weight_quantise(12 + t, u_grp[12 + t])
-                if 6 <= t <= 12 and t % 2 == 0:
-                    weight_quantise(13 + t // 2, u_grp[13 + t // 2])
+                elif a == 1:
+                    weight_quantise(k, u_grp[k])
 
         def evacuate_rows(grp, a, bank):
             dst = grp[:].bitcast(F32).rearrange("p (g c u) -> p g c u", g=2, u=2)[:, :, a * P:(a + 1) * P, :]
@@ -385,28 +392,23 @@ def tile_gnn_s2_pa_t_kernel(
                 repeat_x(k // 2)
             prep_piece(k, ring_banks(), True)
             if k == 4:
-                for h in range(2):
-                    load_edges(h, 0, 0, 1)
-            if k == 8:
-                for h in range(2):
-                    load_edges(h, 0, 1, 2)
+                load_edges(0)
             loaded.append(load_piece(k + 4))
             if k == 7:
-                period(-2)
-        for h in range(2):
-            load_edges(h, 0, 2, 4)
-        for h in range(2):
-            load_edges(h, 1, 0, 4)
+                period(-4)
+                period(-3)
+        for q in range(1, 4):
+            load_edges(q)
 
+        period(-2)
         period(-1)
         u_ps = {}
-        for t in range(TILES + 5):
+        for t in range(TILES + 6):
             period(t)
             if t in (0, 1):
                 repeat_x(t + 6)
-            if t in (9, 17):
-                for h in range(2):
-                    load_edges(h, (t + 7) // 8, 0, 4)
+            if t in (6, 10, 14, 18):
+                load_edges((t + 10) // 4)
             if t == TILES:
                 for h in range(2):
                     for n in range(2):
@@ -447,7 +449,7 @@ def tile_gnn_s2_pa_t_kernel(
             st_c3(100 + h)
             st_c4(100 + h, prm[:, 64 + h:65 + h], prm[:, 80 + h:81 + h])
             r[h] = work.tile([P, C], F32, name="r", tag="en", bufs=5)
-            norm_relu(100 + h, r[h][:], y[h][:])
+            norm_relu(nc.vector, 100 + h, r[h][:], y[h][:])
             add_back(100 + h, r[h][:], r[h][:], y[h][:])
             nc.sync.dma_start(out=o0[:, h, :], in_=r[h][:])
 

@@ -22,7 +22,7 @@ FLOPS = 2 * (4096 + 4 * 256) * 1024 * 1024
 W_E, W_A, W_B, W_V, W_U = 0, 1, 2, 3, 4
 
 SEQ = [
-    ("C2", -1), ("Gv", -5), ("M1", 0), ("XS", -1), ("H", -4), ("F1", -3), ("F2", -3), ("C3", -1), ("XQ", -2), ("A2", 3), ("B0", 1), ("B1", 1), ("E", -2), ("VX", -3), ("Ge", -4), ("A3", 3), ("C4", -1), ("M0", 1), ("A1", 4), ("XP", 0), ("D", -1),
+    ("C2", -1), ("A1", 2), ("XP", 0), ("C3", -1), ("XQ", 0), ("M1", 0), ("B0", 1), ("C4", -1), ("A2", 2), ("XS", 0), ("F1", -2), ("B1", 1), ("F2", -2), ("H", -4), ("VX", -3), ("M0", 1), ("GI", -4), ("A3", 2), ("D", -1), ("E", -1),
 ]
 
 
@@ -47,7 +47,6 @@ def tile_gnn_s2_pa_t_kernel(
         ident = keep.tile([P, P], F32, name="ident")
         make_identity(nc, ident[:])
 
-        ctx.enter_context(tc.manual_schedule())
 
         same_l = keep.tile([P, 8], F32, name="same_l")
         nc.vector.tensor_reduce(
@@ -136,14 +135,14 @@ def tile_gnn_s2_pa_t_kernel(
             {}, {}, {}, {}, {}, {}, {}, {}, {}, {}, {}, {}, {}
         )
 
-        def load_edges(q):
-            for h in range(2):
-                ed[(h, q)] = stage.tile([P, 2, C], BF16, name="ed", tag="ed%d" % h, bufs=4)
-                nc.sync.dma_start(out=ed[(h, q)][:], in_=ev[:, h, 2 * q:2 * q + 2, :])
+        def load_edges(h, q, lo, hi):
+            if lo == 0:
+                ed[(h, q)] = stage.tile([P, 4, C], BF16, name="ed", tag="ed%d" % h, bufs=2)
+            nc.sync.dma_start(out=ed[(h, q)][:, lo:hi, :], in_=ev[:, h, 4 * q + lo:4 * q + hi, :])
 
         def edge_in(t):
             j, h = t // 2, t % 2
-            return ed[(h, j // 2)][:, j % 2, :]
+            return ed[(h, j // 4)][:, j % 4, :]
 
         def sums_half(key, n, src, ident_out):
             if n == 0:
@@ -182,8 +181,8 @@ def tile_gnn_s2_pa_t_kernel(
                 out=a[:, 2:3], in0=a[:, 1:2], scalar1=b[:, 0:1], scalar2=o_col, op0=ALU.mult, op1=ALU.subtract
             )
 
-        def norm_relu(engine, key, dst, src):
-            engine.tensor_scalar(
+        def norm_relu(key, dst, src):
+            nc.vector.tensor_scalar(
                 out=dst, in0=src, scalar1=sc[key][:, 1:2], scalar2=sc[key][:, 2:3], op0=ALU.mult, op1=ALU.max
             )
 
@@ -198,7 +197,7 @@ def tile_gnn_s2_pa_t_kernel(
 
         def st_a2(t):
             egrp[t] = work.tile([P, C], BF16, name="egrp", tag="egrp", align_bytes=64)
-            nc.vector.tensor_copy(
+            nc.scalar.copy(
                 out=egrp[t][:].bitcast(F32).rearrange("p (g r u) -> p g r u", g=2, u=2), in_=bank_view(tr[t])
             )
 
@@ -223,7 +222,7 @@ def tile_gnn_s2_pa_t_kernel(
             sums_half(t, n, m_ps[(t, n)][:], en[t][:, halves[n]])
 
         def st_d(t):
-            norm_relu(nc.gpsimd, t, en[t][:], en[t][:])
+            norm_relu(t, en[t][:], en[t][:])
 
         def st_e(t):
             j, h = t // 2, t % 2
@@ -247,17 +246,9 @@ def tile_gnn_s2_pa_t_kernel(
                     op=ALU.mult,
                 )
 
-        def st_ge(t):
+        def st_gi(t):
             if t >= 2:
-                nc.gpsimd.tensor_tensor(
-                    out=sums[t % 2][:, 0, :], in0=sums[t % 2][:, 0, :], in1=exx[t][:, 0, :], op=ALU.add
-                )
-
-        def st_gv(t):
-            if t >= 2:
-                nc.vector.tensor_tensor(
-                    out=sums[t % 2][:, 1, :], in0=sums[t % 2][:, 1, :], in1=exx[t][:, 1, :], op=ALU.add
-                )
+                nc.vector.tensor_tensor(out=sums[t % 2][:], in0=sums[t % 2][:], in1=exx[t][:], op=ALU.add)
 
         def st_vx(j):
             for n in range(2):
@@ -270,14 +261,14 @@ def tile_gnn_s2_pa_t_kernel(
 
         stages = {
             "A1": st_a1, "A2": st_a2, "A3": st_a3, "C2": st_c2, "C3": st_c3, "C4": st_c4_edge, "D": st_d,
-            "E": st_e, "F1": st_f1, "F2": st_f2, "H": st_h, "Ge": st_ge, "Gv": st_gv,
+            "E": st_e, "F1": st_f1, "F2": st_f2, "H": st_h, "GI": st_gi,
         }
 
         def period(t):
             for name, off in SEQ:
                 s = t + off
                 if name in ("XP", "XS", "XQ"):
-                    late_weights(name, s)
+                    late_weights(name, t)
                 elif name == "VX":
                     if s >= 0 and s % 2 == 0 and s // 2 < NODES:
                         st_vx(s // 2)
@@ -305,11 +296,11 @@ def tile_gnn_s2_pa_t_kernel(
         prm = keep.tile([P, 96], F32, name="prm")
         nc.vector.tensor_copy(out=prm[:], in_=pp[:])
 
-        rotation = [("m", 3), ("vx", 2), ("m", 3), ("vx", 2), ("m", 3)]
+        rotation = [("m", 3), ("vx", 2), ("tr", 2), ("m", 3), ("vx", 2), ("tr", 2), ("m", 3)]
         n_banks = [0]
 
         def next_bank():
-            tag, bufs = rotation[n_banks[0] % 5]
+            tag, bufs = rotation[n_banks[0] % 7]
             n_banks[0] += 1
             bank = psum.tile([P, 512], F32, name="bank", tag=tag, bufs=bufs)
             return bank
@@ -358,8 +349,8 @@ def tile_gnn_s2_pa_t_kernel(
         u_grp = {}
 
         def late_weights(name, t):
-            if -2 <= t <= 1:
-                k = 14 + t
+            if -1 <= t <= 2:
+                k = 13 + t
                 if name == "XP":
                     late[k] = [psum.tile([P, 512], F32, name="wv_b", tag="vx", bufs=2) for a in range(2)]
                     for a in range(2):
@@ -369,8 +360,6 @@ def tile_gnn_s2_pa_t_kernel(
                     u_grp[k] = new_group_tile()
                     for a in range(2):
                         evacuate_rows(u_grp[k], a, late[k][a][:])
-                else:
-                    weight_quantise(k, u_grp[k])
             if 4 <= t < 12:
                 k, a = 16 + (t - 4) // 2, (t - 4) % 2
                 if name == "XP":
@@ -380,8 +369,11 @@ def tile_gnn_s2_pa_t_kernel(
                     if a == 0:
                         u_grp[k] = new_group_tile()
                     evacuate_rows(u_grp[k], a, late[(k, a)][:])
-                elif a == 1:
-                    weight_quantise(k, u_grp[k])
+            if name == "XQ":
+                if 0 <= t <= 3:
+                    weight_quantise(12 + t, u_grp[12 + t])
+                if 6 <= t <= 12 and t % 2 == 0:
+                    weight_quantise(13 + t // 2, u_grp[13 + t // 2])
 
         def evacuate_rows(grp, a, bank):
             dst = grp[:].bitcast(F32).rearrange("p (g c u) -> p g c u", g=2, u=2)[:, :, a * P:(a + 1) * P, :]
@@ -392,23 +384,28 @@ def tile_gnn_s2_pa_t_kernel(
                 repeat_x(k // 2)
             prep_piece(k, ring_banks(), True)
             if k == 4:
-                load_edges(0)
+                for h in range(2):
+                    load_edges(h, 0, 0, 1)
+            if k == 8:
+                for h in range(2):
+                    load_edges(h, 0, 1, 2)
             loaded.append(load_piece(k + 4))
             if k == 7:
-                period(-4)
-                period(-3)
-        for q in range(1, 4):
-            load_edges(q)
+                period(-2)
+        for h in range(2):
+            load_edges(h, 0, 2, 4)
+        for h in range(2):
+            load_edges(h, 1, 0, 4)
 
-        period(-2)
         period(-1)
         u_ps = {}
-        for t in range(TILES + 6):
+        for t in range(TILES + 5):
             period(t)
             if t in (0, 1):
                 repeat_x(t + 6)
-            if t in (6, 10, 14, 18):
-                load_edges((t + 10) // 4)
+            if t in (9, 17):
+                for h in range(2):
+                    load_edges(h, (t + 7) // 8, 0, 4)
             if t == TILES:
                 for h in range(2):
                     for n in range(2):
@@ -449,7 +446,7 @@ def tile_gnn_s2_pa_t_kernel(
             st_c3(100 + h)
             st_c4(100 + h, prm[:, 64 + h:65 + h], prm[:, 80 + h:81 + h])
             r[h] = work.tile([P, C], F32, name="r", tag="en", bufs=5)
-            norm_relu(nc.vector, 100 + h, r[h][:], y[h][:])
+            norm_relu(100 + h, r[h][:], y[h][:])
             add_back(100 + h, r[h][:], r[h][:], y[h][:])
             nc.sync.dma_start(out=o0[:, h, :], in_=r[h][:])
 

@@ -197,9 +197,11 @@ def tile_gnn_s2_pa_t_kernel(
 
         def st_a2(t):
             egrp[t] = work.tile([P, C], BF16, name="egrp", tag="egrp", align_bytes=64)
-            nc.scalar.copy(
-                out=egrp[t][:].bitcast(F32).rearrange("p (g r u) -> p g r u", g=2, u=2), in_=bank_view(tr[t])
-            )
+            dst = egrp[t][:].bitcast(F32).rearrange("p (g r u) -> p g r u", g=2, u=2)
+            if t % 4 == 0:
+                nc.scalar.copy(out=dst, in_=bank_view(tr[t]))
+            else:
+                nc.vector.tensor_copy(out=dst, in_=bank_view(tr[t]))
 
         def st_a3(t):
             ecod[t] = work.tile([P, 256], U32, name="ecod", tag="ecod", bufs=3, align_bytes=64)
@@ -248,7 +250,12 @@ def tile_gnn_s2_pa_t_kernel(
 
         def st_gi(t):
             if t >= 2:
-                nc.vector.tensor_tensor(out=sums[t % 2][:], in0=sums[t % 2][:], in1=exx[t][:], op=ALU.add)
+                nc.gpsimd.tensor_tensor(
+                    out=sums[t % 2][:, 0, :], in0=sums[t % 2][:, 0, :], in1=exx[t][:, 0, :], op=ALU.add
+                )
+                nc.vector.tensor_tensor(
+                    out=sums[t % 2][:, 1, :], in0=sums[t % 2][:, 1, :], in1=exx[t][:, 1, :], op=ALU.add
+                )
 
         def st_vx(j):
             for n in range(2):

@@ -77,6 +77,8 @@ def tile_gnn_s2_pa_t_kernel(
         xrc = keep.tile([P, NODES, 256], U32, name="xrc", align_bytes=64)
         xrs = keep.tile([P, NODES, 256], U8, name="xrs", align_bytes=64)
         sums = [keep.tile([P, 2, C], F32, name="sums%d" % h) for h in range(2)]
+        accs = keep.tile([P, 8, 4], F32, name="accs")
+        nc.vector.memset(accs[:], 0.0)
 
         def transpose_words(bank, src_words):
             for k in range(4):
@@ -131,8 +133,8 @@ def tile_gnn_s2_pa_t_kernel(
                 for g in range(2)
             ]
 
-        ed, tr, egrp, ecod, escl, m_ps, acc, ps4, sb, sc, en, exx, vx = (
-            {}, {}, {}, {}, {}, {}, {}, {}, {}, {}, {}, {}, {}
+        ed, tr, egrp, ecod, escl, m_ps, acc, ps4, sb, sc, rs, en, exx, vx = (
+            {}, {}, {}, {}, {}, {}, {}, {}, {}, {}, {}, {}, {}, {}
         )
 
         def load_edges(h, q, lo, hi):
@@ -144,16 +146,6 @@ def tile_gnn_s2_pa_t_kernel(
             j, h = t // 2, t % 2
             return ed[(h, j // 4)][:, j % 4, :]
 
-        def sums_half(key, n, src, ident_out):
-            if n == 0:
-                acc[key] = small.tile([P, 4], F32, name="acc", tag="acc")
-            nc.scalar.activation(
-                out=ident_out, in_=src, func=ACT.Identity, accum_out=acc[key][:, 2 * n:2 * n + 1]
-            )
-            junk = work.tile([P, 512], BF16, name="junk", tag="junk", bufs=2)
-            nc.scalar.activation(
-                out=junk[:], in_=src, func=ACT.Square, accum_out=acc[key][:, 2 * n + 1:2 * n + 2]
-            )
 
         def st_c2(key):
             ps4[key] = psum.tile([P, 4], F32, name="ps4", tag="st")
@@ -175,9 +167,10 @@ def tile_gnn_s2_pa_t_kernel(
         def st_c4(key, w_col, o_col):
             sc[key] = small.tile([P, 4], F32, name="sc", tag="sc")
             a, b = sc[key], sb[key]
-            nc.gpsimd.tensor_tensor(out=a[:, 0:1], in0=b[:, 4:5], in1=minus_half[:], op=ALU.pow)
-            nc.gpsimd.tensor_tensor(out=a[:, 1:2], in0=a[:, 0:1], in1=w_col, op=ALU.mult)
-            nc.gpsimd.tensor_scalar(
+            rs[key] = small.tile([P, 1], F32, name="rs", tag="rs")
+            nc.gpsimd.tensor_tensor(out=rs[key][:], in0=b[:, 4:5], in1=minus_half[:], op=ALU.pow)
+            nc.vector.tensor_tensor(out=a[:, 1:2], in0=rs[key][:], in1=w_col, op=ALU.mult)
+            nc.vector.tensor_scalar(
                 out=a[:, 2:3], in0=a[:, 1:2], scalar1=b[:, 0:1], scalar2=o_col, op0=ALU.mult, op1=ALU.subtract
             )
 
@@ -196,16 +189,14 @@ def tile_gnn_s2_pa_t_kernel(
             transpose_words(tr[t], edge_in(t).bitcast(F32))
 
         def st_a2(t):
-            egrp[t] = work.tile([P, C], BF16, name="egrp", tag="egrp", align_bytes=64)
-            dst = egrp[t][:].bitcast(F32).rearrange("p (g r u) -> p g r u", g=2, u=2)
-            if t % 4 == 0:
-                nc.scalar.copy(out=dst, in_=bank_view(tr[t]))
-            else:
-                nc.vector.tensor_copy(out=dst, in_=bank_view(tr[t]))
+            egrp[t] = work.tile([P, C], BF16, name="egrp", tag="egrp", bufs=3, align_bytes=64)
+            nc.scalar.copy(
+                out=egrp[t][:].bitcast(F32).rearrange("p (g r u) -> p g r u", g=2, u=2), in_=bank_view(tr[t])
+            )
 
         def st_a3(t):
-            ecod[t] = work.tile([P, 256], U32, name="ecod", tag="ecod", bufs=3, align_bytes=64)
-            escl[t] = work.tile([P, 256], U8, name="escl", tag="escl", bufs=3, align_bytes=64)
+            ecod[t] = work.tile([P, 256], U32, name="ecod", tag="ecod", bufs=4, align_bytes=64)
+            escl[t] = work.tile([P, 256], U8, name="escl", tag="escl", bufs=4, align_bytes=64)
             nc.vector.quantize_mx(out=ecod[t][:].bitcast(FP8X4), scales=escl[t][:], in_=egrp[t][:])
 
         def st_b(t, n):
@@ -220,8 +211,15 @@ def tile_gnn_s2_pa_t_kernel(
 
         def st_m(t, n):
             if n == 0:
-                en[t] = work.tile([P, C], F32, name="en", tag="en", bufs=5)
-            sums_half(t, n, m_ps[(t, n)][:], en[t][:, halves[n]])
+                en[t] = work.tile([P, C], F32, name="en", tag="en", bufs=6)
+                acc[t] = accs[:, t % 8, :]
+            nc.scalar.activation(
+                out=en[t][:, halves[n]], in_=m_ps[(t, n)][:], func=ACT.Identity,
+                accum_out=acc[t][:, 2 * n:2 * n + 1],
+            )
+            if n == 1:
+                junk = work.tile([P, C], BF16, name="junk", tag="junk", bufs=2)
+                nc.scalar.activation(out=junk[:], in_=en[t][:], func=ACT.Square, accum_out=acc[t][:, 1:2])
 
         def st_d(t):
             norm_relu(t, en[t][:], en[t][:])
@@ -235,13 +233,24 @@ def tile_gnn_s2_pa_t_kernel(
             if t < 2:
                 exx[t] = sums[t]
             else:
-                exx[t] = work.tile([P, 2, C], F32, name="exx", tag="exx", bufs=3)
+                exx[t] = work.tile([P, 2, C], F32, name="exx", tag="exx", bufs=4, align_bytes=64)
             nc.scalar.activation(out=exx[t][:, 0, :], in_=en[t][:], func=ACT.Tanh, scale=0.5)
 
         def st_f2(t):
             nc.scalar.activation(out=exx[t][:, 0, :], in_=exx[t][:, 0, :], func=ACT.Exp, scale=0.5)
 
         def st_h(t):
+            if t >= TILES - 2:
+                nc.vector.tensor_tensor(
+                    out=sums[t % 2][:, 0, :], in0=sums[t % 2][:, 0, :], in1=exx[t][:, 0, :], op=ALU.add
+                )
+                if t % 2 == 0:
+                    node_ln(0)
+                else:
+                    with tc.manual_schedule():
+                        node_ln(1)
+                        node_exp(1)
+                        node_exp(0)
             for n in range(2):
                 nc.vector.tensor_tensor(
                     out=exx[t][:, 1, halves[n]], in0=exx[t][:, 0, halves[n]], in1=vx[(t // 2, n)][:],
@@ -249,10 +258,9 @@ def tile_gnn_s2_pa_t_kernel(
                 )
 
         def st_gi(t):
-            if t >= 2:
-                nc.gpsimd.tensor_tensor(
-                    out=sums[t % 2][:, 0, :], in0=sums[t % 2][:, 0, :], in1=exx[t][:, 0, :], op=ALU.add
-                )
+            if 2 <= t < TILES - 2:
+                nc.vector.tensor_tensor(out=sums[t % 2][:], in0=sums[t % 2][:], in1=exx[t][:], op=ALU.add)
+            elif t >= 2:
                 nc.vector.tensor_tensor(
                     out=sums[t % 2][:, 1, :], in0=sums[t % 2][:, 1, :], in1=exx[t][:, 1, :], op=ALU.add
                 )
@@ -293,7 +301,7 @@ def tile_gnn_s2_pa_t_kernel(
         nc.sync.dma_start(out=pst[0:8, 32:64], in_=bne_b.rearrange("(l x) -> l x", l=8))
         nc.sync.dma_start(out=pst[0:8, 64:66], in_=bnv_w.rearrange("(l x) -> l x", l=8))
         nc.sync.dma_start(out=pst[0:8, 80:82], in_=bnv_b.rearrange("(l x) -> l x", l=8))
-        xs = work.tile([P, 2, C], BF16, name="xs", tag="en", bufs=5)
+        xs = work.tile([P, 2, C], BF16, name="xs", tag="en", bufs=6)
         nc.sync.dma_start(out=xs[:], in_=xv)
         loaded = [load_piece(k) for k in range(4)]
         pf = keep.tile([P, 96], F32, name="pf")
@@ -325,7 +333,7 @@ def tile_gnn_s2_pa_t_kernel(
             nc.vector.quantize_mx(out=xnc[:, h, :].bitcast(FP8X4), scales=xns[:, h, :], in_=xg[h][:])
 
         def repeat_x(q):
-            rep = stage.tile([P, 2048], BF16, name="rep", tag="rep", bufs=2, align_bytes=64)
+            rep = work.tile([P, 2048], BF16, name="rep", tag="exx", bufs=4, align_bytes=64)
             dst = rep[:].bitcast(F32).rearrange("p (jj g b l u) -> p jj g b l u", jj=2, g=2, b=16, l=8, u=2)
             for jj in range(2):
                 j = 2 * q + jj
@@ -404,6 +412,12 @@ def tile_gnn_s2_pa_t_kernel(
         for h in range(2):
             load_edges(h, 1, 0, 4)
 
+        def node_ln(h):
+            nc.scalar.activation(out=sums[h][:, 0, :], in_=sums[h][:, 0, :], func=ACT.Ln)
+
+        def node_exp(h):
+            nc.scalar.activation(out=sums[h][:, 0, :], in_=sums[h][:, 0, :], func=ACT.Exp, scale=-1.0)
+
         period(-1)
         u_ps = {}
         for t in range(TILES + 5):
@@ -413,6 +427,9 @@ def tile_gnn_s2_pa_t_kernel(
             if t in (9, 17):
                 for h in range(2):
                     load_edges(h, (t + 7) // 8, 0, 4)
+            if t == TILES + 1:
+                warm = small.tile([P, 1], F32, name="warm", tag="warm")
+                nc.scalar.activation(out=warm[:], in_=exx[TILES - 1][:, 0, 0:1], func=ACT.Ln)
             if t == TILES:
                 for h in range(2):
                     for n in range(2):
@@ -424,15 +441,14 @@ def tile_gnn_s2_pa_t_kernel(
         r = {}
         st6 = {}
 
-        def node_inverse(h):
-            nc.scalar.activation(out=sums[h][:, 0, :], in_=sums[h][:, 0, :], func=ACT.Ln)
-            nc.scalar.activation(out=sums[h][:, 0, :], in_=sums[h][:, 0, :], func=ACT.Exp, scale=-1.0)
-
         def node_y(h):
-            nc.vector.tensor_tensor(out=sums[h][:, 1, :], in0=sums[h][:, 1, :], in1=sums[h][:, 0, :], op=ALU.mult)
-            y[h] = work.tile([P, C], F32, name="y", tag="en", bufs=5)
+            y[h] = work.tile([P, C], F32, name="y", tag="en", bufs=6)
             st6[h] = small.tile([P, 2, 6], F32, name="st6", tag="st6")
             for n in range(2):
+                nc.vector.tensor_tensor(
+                    out=sums[h][:, 1, halves[n]], in0=sums[h][:, 1, halves[n]], in1=sums[h][:, 0, halves[n]],
+                    op=ALU.mult,
+                )
                 nc.vector.scalar_tensor_tensor(
                     out=y[h][:, halves[n]], in0=sums[h][:, 1, halves[n]], scalar=1.0 / NODES,
                     in1=u_ps[(h, n)][:], op0=ALU.mult, op1=ALU.add,
@@ -450,15 +466,15 @@ def tile_gnn_s2_pa_t_kernel(
                 )
 
         def node_out(h):
-            st_c3(100 + h)
-            st_c4(100 + h, prm[:, 64 + h:65 + h], prm[:, 80 + h:81 + h])
-            r[h] = work.tile([P, C], F32, name="r", tag="en", bufs=5)
-            norm_relu(100 + h, r[h][:], y[h][:])
-            add_back(100 + h, r[h][:], r[h][:], y[h][:])
-            nc.sync.dma_start(out=o0[:, h, :], in_=r[h][:])
+            key = 100 + h
+            st_c3(key)
+            st_c4(key, prm[:, 64 + h:65 + h], prm[:, 80 + h:81 + h])
+            r[h] = work.tile([P, C], F32, name="r", tag="en", bufs=6)
+            for n in range(2):
+                norm_relu(key, r[h][:, halves[n]], y[h][:, halves[n]])
+                add_back(key, r[h][:, halves[n]], r[h][:, halves[n]], y[h][:, halves[n]])
+                nc.sync.dma_start(out=o0[:, h, halves[n]], in_=r[h][:, halves[n]])
 
-        node_inverse(0)
-        node_inverse(1)
         node_y(0)
         st_c2(100)
         node_y(1)

@@ -14,16 +14,24 @@ AX = mybir.AxisListType
 
 P = 128
 C = 1024
+BANK = 512
 NODES = 16
 TILES = 32
+WORDS = 256
 EPS = 1e-5
-FLOPS = 2 * (4096 + 4 * 256) * 1024 * 1024
+SAMPLES = 16 * C
+FLOPS = 2 * (4096 + 4 * 256) * C * C
 
 W_E, W_A, W_B, W_V, W_U = 0, 1, 2, 3, 4
+PIECE = 256
+NODE_KEY = 100
 
-SEQ = [
-    ("C2", -1), ("A1", 2), ("XP", 0), ("C3", -1), ("XQ", 0), ("M1", 0), ("B0", 1), ("C4", -1), ("A2", 2), ("XS", 0), ("F1", -2), ("B1", 1), ("F2", -2), ("H", -4), ("VX", -3), ("M0", 1), ("GI", -4), ("A3", 2), ("D", -1), ("E", -1),
-]
+W_ROWS_BUFS = 4
+W_GROUPED_BUFS = 3
+E_GROUPED_BUFS = 3
+E_CODES_BUFS = 4
+EDGE_NEW_BUFS = 7
+EXPS_BUFS = 4
 
 
 def tile_gnn_s2_pa_t_kernel(
@@ -31,380 +39,426 @@ def tile_gnn_s2_pa_t_kernel(
 ):
     nc = tc.nc
     weights = [We, Wa, Wb, Wv, Wu]
-    ev = edge.rearrange("b (l h j) c -> (b l) h j c", h=2, j=NODES)
-    o1 = out_1.rearrange("b (l h j) c -> (b l) h j c", h=2, j=NODES)
-    xv = x.rearrange("b (l h) c -> (b l) h c", h=2)
-    o0 = out_0.rearrange("b (l h) c -> (b l) h c", h=2)
-    halves = [slice(0, 512), slice(512, 1024)]
+    edge_view = edge.rearrange("b (l h j) c -> (b l) h j c", h=2, j=NODES)
+    edge_new_view = out_1.rearrange("b (l h j) c -> (b l) h j c", h=2, j=NODES)
+    x_view = x.rearrange("b (l h) c -> (b l) h c", h=2)
+    x_new_view = out_0.rearrange("b (l h) c -> (b l) h c", h=2)
+    halves = [slice(0, BANK), slice(BANK, C)]
 
     with ExitStack() as ctx:
-        keep = ctx.enter_context(tc.tile_pool(name="keep", bufs=1))
-        stage = ctx.enter_context(tc.tile_pool(name="stage", bufs=2))
+        resident = ctx.enter_context(tc.tile_pool(name="resident", bufs=1))
+        staging = ctx.enter_context(tc.tile_pool(name="staging", bufs=2))
         work = ctx.enter_context(tc.tile_pool(name="work", bufs=2))
-        small = ctx.enter_context(tc.tile_pool(name="small", bufs=6))
+        columns = ctx.enter_context(tc.tile_pool(name="columns", bufs=8))
         psum = ctx.enter_context(tc.psum_pool(name="psum", bufs=1))
 
-        ident = keep.tile([P, P], F32, name="ident")
+        ident = resident.tile([P, P], F32, name="ident")
         make_identity(nc, ident[:])
-
-
-        same_l = keep.tile([P, 8], F32, name="same_l")
+        same_l = resident.tile([P, 8], F32, name="same_l")
         nc.vector.tensor_reduce(
             out=same_l[:], in_=ident[:].rearrange("p (b l) -> p l b", l=8), axis=AX.X, op=ALU.add
         )
-        avg_pos = keep.tile([P, P], F32, name="avg_pos")
-        avg_neg = keep.tile([P, P], F32, name="avg_neg")
+        avg_pos = resident.tile([P, P], F32, name="avg_pos")
+        avg_neg = resident.tile([P, P], F32, name="avg_neg")
         nc.vector.tensor_scalar(
             out=avg_pos[:].rearrange("p (b l) -> p b l", l=8),
             in0=same_l[:].unsqueeze(1).to_broadcast([P, 16, 8]),
-            scalar1=1.0 / 16384.0, scalar2=None, op0=ALU.mult,
+            scalar1=1.0 / SAMPLES, scalar2=None, op0=ALU.mult,
         )
         nc.vector.tensor_scalar(
             out=avg_neg[:].rearrange("p (b l) -> p b l", l=8),
             in0=same_l[:].unsqueeze(1).to_broadcast([P, 16, 8]),
-            scalar1=-1.0 / 16384.0, scalar2=None, op0=ALU.mult,
+            scalar1=-1.0 / SAMPLES, scalar2=None, op0=ALU.mult,
         )
-        eps_row = keep.tile([P, 4], F32, name="eps_row")
+        eps_row = resident.tile([P, 4], F32, name="eps_row")
         nc.vector.memset(eps_row[:], 0.0)
         nc.vector.memset(eps_row[:, 1:2], EPS)
-        minus_half = keep.tile([P, 1], F32, name="minus_half")
+        minus_half = resident.tile([P, 1], F32, name="minus_half")
         nc.vector.memset(minus_half[:], -0.5)
 
-        wc = [keep.tile([P, 2, C], U32, name="wc%d" % i, align_bytes=64) for i in range(5)]
-        ws = [keep.tile([P, 2, C], U8, name="ws%d" % i, align_bytes=64) for i in range(5)]
-        xnc = keep.tile([P, 2, 256], U32, name="xnc", align_bytes=64)
-        xns = keep.tile([P, 2, 256], U8, name="xns", align_bytes=64)
-        xrc = keep.tile([P, NODES, 256], U32, name="xrc", align_bytes=64)
-        xrs = keep.tile([P, NODES, 256], U8, name="xrs", align_bytes=64)
-        sums = [keep.tile([P, 2, C], F32, name="sums%d" % h) for h in range(2)]
-        accs = keep.tile([P, 8, 4], F32, name="accs")
-        nc.vector.memset(accs[:], 0.0)
+        w_codes = [resident.tile([P, 2, C], U32, name="w_codes%d" % w, align_bytes=64) for w in range(5)]
+        w_scales = [resident.tile([P, 2, C], U8, name="w_scales%d" % w, align_bytes=64) for w in range(5)]
+        x_codes = resident.tile([P, 2, WORDS], U32, name="x_codes", align_bytes=64)
+        x_scales = resident.tile([P, 2, WORDS], U8, name="x_scales", align_bytes=64)
+        xj_codes = resident.tile([P, NODES, WORDS], U32, name="xj_codes", align_bytes=64)
+        xj_scales = resident.tile([P, NODES, WORDS], U8, name="xj_scales", align_bytes=64)
+        sums = [resident.tile([P, 2, C], F32, name="sums%d" % h) for h in range(2)]
+        row_sums = resident.tile([P, 8, 4], F32, name="row_sums")
+        nc.vector.memset(row_sums[:], 0.0)
 
-        def transpose_words(bank, src_words):
+        def transpose_words(bank, rows_as_words):
             for k in range(4):
                 nc.tensor.transpose(
-                    bank[:, k * P:(k + 1) * P], src_words[:, k * P:(k + 1) * P], ident[:]
+                    bank[:, k * P:(k + 1) * P], rows_as_words[:, k * P:(k + 1) * P], ident[:]
                 )
 
-        def bank_view(bank):
+        def grouped_read(bank):
             return bank.rearrange("p (g u r) -> p g r u", g=2, u=2)
 
-        def load_piece(k):
-            w, part = k // 4, k % 4
-            wst = stage.tile([P, 2, C], BF16, name="wst", tag="wst", bufs=4)
-            nc.sync.dma_start(
-                out=wst[:],
-                in_=weights[w][part * 256:(part + 1) * 256, :].rearrange("(a p) k -> p a k", p=P),
-            )
-            return wst
-
-        def new_group_tile():
-            grp = stage.tile([P, 2048], BF16, name="grp", tag="grp", bufs=3, align_bytes=64)
-            return grp
-
-        def weight_rows(wst, grp, a, bank, on_scalar):
-            transpose_words(bank, wst[:].bitcast(F32)[:, a, :])
-            dst = grp[:].bitcast(F32).rearrange("p (g c u) -> p g c u", g=2, u=2)[:, :, a * P:(a + 1) * P, :]
-            if on_scalar:
-                nc.scalar.copy(out=dst, in_=bank_view(bank))
-            else:
-                nc.vector.tensor_copy(out=dst, in_=bank_view(bank))
-
-        def weight_quantise(k, grp):
-            w, part = k // 4, k % 4
-            for g in range(2):
-                nc.vector.quantize_mx(
-                    out=wc[w][:, g, part * 256:(part + 1) * 256].bitcast(FP8X4),
-                    scales=ws[w][:, g, part * 256:(part + 1) * 256],
-                    in_=grp[:, g * 1024:(g + 1) * 1024],
-                )
-
-        def mx_group(acc_ps, operands):
+        def mx_group(acc, operands):
             last = len(operands) - 1
-            for i, (lc, ls, rc, rs) in enumerate(operands):
+            for i, (l_codes, l_scales, r_codes, r_scales) in enumerate(operands):
                 nc.tensor.matmul_mx(
-                    out=acc_ps, lhsT=lc.bitcast(FP8X4), lhsT_scale=ls, rhs=rc.bitcast(FP8X4), rhs_scale=rs,
+                    out=acc, lhsT=l_codes.bitcast(FP8X4), lhsT_scale=l_scales,
+                    rhs=r_codes.bitcast(FP8X4), rhs_scale=r_scales,
                     start=(i == 0), stop=(i == last),
                 )
 
-        def pair(lc, ls, w, cols):
+        def passes(codes, scales, w, cols):
             return [
-                (lc[:, g * P:(g + 1) * P], ls[:, g * P:(g + 1) * P], wc[w][:, g, cols], ws[w][:, g, cols])
+                (codes[:, g * P:(g + 1) * P], scales[:, g * P:(g + 1) * P],
+                 w_codes[w][:, g, cols], w_scales[w][:, g, cols])
                 for g in range(2)
             ]
 
-        ed, tr, egrp, ecod, escl, m_ps, acc, ps4, sb, sc, rs, en, exx, vx = (
-            {}, {}, {}, {}, {}, {}, {}, {}, {}, {}, {}, {}, {}, {}
-        )
+        w_rows = {}
+        w_grouped = {}
+        w_banks = {}
 
-        def load_edges(h, q, lo, hi):
-            if lo == 0:
-                ed[(h, q)] = stage.tile([P, 4, C], BF16, name="ed", tag="ed%d" % h, bufs=2)
-            nc.sync.dma_start(out=ed[(h, q)][:, lo:hi, :], in_=ev[:, h, 4 * q + lo:4 * q + hi, :])
+        def load_piece(k):
+            w, part = k // 4, k % 4
+            w_rows[k] = staging.tile([P, 2, C], BF16, name="w_rows", tag="w_rows", bufs=W_ROWS_BUFS)
+            nc.sync.dma_start(
+                out=w_rows[k][:],
+                in_=weights[w][part * PIECE:(part + 1) * PIECE, :].rearrange("(a p) k -> p a k", p=P),
+            )
 
-        def edge_in(t):
-            j, h = t // 2, t % 2
-            return ed[(h, j // 4)][:, j % 4, :]
+        def new_grouped(k):
+            w_grouped[k] = staging.tile(
+                [P, 2048], BF16, name="w_grouped", tag="w_grouped", bufs=W_GROUPED_BUFS, align_bytes=64
+            )
 
+        def transpose_piece_rows(k, a, bank):
+            transpose_words(bank, w_rows[k][:].bitcast(F32)[:, a, :])
 
-        def st_c2(key):
-            ps4[key] = psum.tile([P, 4], F32, name="ps4", tag="st")
-            for i, mat in enumerate((avg_pos, avg_neg)):
+        def copy_piece_rows(k, a, bank):
+            dst = w_grouped[k][:].bitcast(F32).rearrange("p (g c u) -> p g c u", g=2, u=2)
+            nc.scalar.copy(out=dst[:, :, a * P:(a + 1) * P, :], in_=grouped_read(bank))
+
+        def quantise_piece(k):
+            w, part = k // 4, k % 4
+            cols = slice(part * PIECE, (part + 1) * PIECE)
+            for g in range(2):
+                nc.vector.quantize_mx(
+                    out=w_codes[w][:, g, cols].bitcast(FP8X4), scales=w_scales[w][:, g, cols],
+                    in_=w_grouped[k][:, g * 1024:(g + 1) * 1024],
+                )
+
+        sums_of, means_ps, moments, scale_bias, rstd = {}, {}, {}, {}, {}
+
+        def average_over_batches(key):
+            means_ps[key] = psum.tile([P, 4], F32, name="means_ps", tag="stats")
+            for i, avg in enumerate((avg_pos, avg_neg)):
                 for n in range(2):
                     nc.tensor.matmul(
-                        ps4[key][:, 2 * i:2 * i + 2], lhsT=mat[:], rhs=acc[key][:, 2 * n:2 * n + 2],
+                        means_ps[key][:, 2 * i:2 * i + 2], lhsT=avg[:], rhs=sums_of[key][:, 2 * n:2 * n + 2],
                         start=(n == 0), stop=(n == 1),
                     )
 
-        def st_c3(key):
-            sb[key] = small.tile([P, 8], F32, name="sb", tag="sb")
-            b = sb[key]
-            nc.vector.tensor_tensor(out=b[:, 0:4], in0=ps4[key][:], in1=eps_row[:], op=ALU.add)
+        def variance(key):
+            moments[key] = columns.tile([P, 8], F32, name="moments", tag="moments")
+            mo = moments[key]
+            nc.vector.tensor_tensor(out=mo[:, 0:4], in0=means_ps[key][:], in1=eps_row[:], op=ALU.add)
             nc.vector.scalar_tensor_tensor(
-                out=b[:, 4:5], in0=b[:, 0:1], scalar=b[:, 2:3], in1=b[:, 1:2], op0=ALU.mult, op1=ALU.add
+                out=mo[:, 4:5], in0=mo[:, 0:1], scalar=mo[:, 2:3], in1=mo[:, 1:2], op0=ALU.mult, op1=ALU.add
             )
 
-        def st_c4(key, w_col, o_col):
-            sc[key] = small.tile([P, 4], F32, name="sc", tag="sc")
-            a, b = sc[key], sb[key]
-            rs[key] = small.tile([P, 1], F32, name="rs", tag="rs")
-            nc.gpsimd.tensor_tensor(out=rs[key][:], in0=b[:, 4:5], in1=minus_half[:], op=ALU.pow)
-            nc.vector.tensor_tensor(out=a[:, 1:2], in0=rs[key][:], in1=w_col, op=ALU.mult)
+        def scale_and_bias(key, gain, offset):
+            scale_bias[key] = columns.tile([P, 4], F32, name="scale_bias", tag="scale_bias")
+            sb, mo = scale_bias[key], moments[key]
+            rstd[key] = columns.tile([P, 1], F32, name="rstd", tag="rstd")
+            nc.gpsimd.tensor_tensor(out=rstd[key][:], in0=mo[:, 4:5], in1=minus_half[:], op=ALU.pow)
+            nc.vector.tensor_tensor(out=sb[:, 1:2], in0=rstd[key][:], in1=gain, op=ALU.mult)
             nc.vector.tensor_scalar(
-                out=a[:, 2:3], in0=a[:, 1:2], scalar1=b[:, 0:1], scalar2=o_col, op0=ALU.mult, op1=ALU.subtract
+                out=sb[:, 2:3], in0=sb[:, 1:2], scalar1=mo[:, 0:1], scalar2=offset, op0=ALU.mult, op1=ALU.subtract
             )
 
-        def norm_relu(key, dst, src):
+        def scaled_max(key, dst, src):
             nc.vector.tensor_scalar(
-                out=dst, in0=src, scalar1=sc[key][:, 1:2], scalar2=sc[key][:, 2:3], op0=ALU.mult, op1=ALU.max
+                out=dst, in0=src, scalar1=scale_bias[key][:, 1:2], scalar2=scale_bias[key][:, 2:3],
+                op0=ALU.mult, op1=ALU.max,
             )
 
-        def add_back(key, dst, src, other):
+        def add_residual(key, dst, src, residual):
             nc.vector.scalar_tensor_tensor(
-                out=dst, in0=src, scalar=sc[key][:, 2:3], in1=other, op0=ALU.subtract, op1=ALU.add
+                out=dst, in0=src, scalar=scale_bias[key][:, 2:3], in1=residual, op0=ALU.subtract, op1=ALU.add
             )
 
-        def st_a1(t):
-            tr[t] = psum.tile([P, 512], F32, name="tr", tag="tr", bufs=2)
-            transpose_words(tr[t], edge_in(t).bitcast(F32))
+        edge_rows, transposed, e_grouped, e_codes, e_scales, m_ps, edge_new, exps, vx_ps = (
+            {}, {}, {}, {}, {}, {}, {}, {}, {}
+        )
 
-        def st_a2(t):
-            egrp[t] = work.tile([P, C], BF16, name="egrp", tag="egrp", bufs=3, align_bytes=64)
-            nc.scalar.copy(
-                out=egrp[t][:].bitcast(F32).rearrange("p (g r u) -> p g r u", g=2, u=2), in_=bank_view(tr[t])
-            )
+        def is_tile(t):
+            return 0 <= t < TILES
 
-        def st_a3(t):
-            ecod[t] = work.tile([P, 256], U32, name="ecod", tag="ecod", bufs=4, align_bytes=64)
-            escl[t] = work.tile([P, 256], U8, name="escl", tag="escl", bufs=4, align_bytes=64)
-            nc.vector.quantize_mx(out=ecod[t][:].bitcast(FP8X4), scales=escl[t][:], in_=egrp[t][:])
+        def load_edges(h, q, lo, hi):
+            if lo == 0:
+                edge_rows[(h, q)] = staging.tile([P, 4, C], BF16, name="edge_rows", tag="edge_rows%d" % h)
+            nc.sync.dma_start(out=edge_rows[(h, q)][:, lo:hi, :], in_=edge_view[:, h, 4 * q + lo:4 * q + hi, :])
 
-        def st_b(t, n):
+        def edge_of(t):
             j, h = t // 2, t % 2
-            m_ps[(t, n)] = psum.tile([P, 512], F32, name="m_ps", tag="m", bufs=3)
-            mx_group(
-                m_ps[(t, n)][:],
-                pair(ecod[t], escl[t], W_E, halves[n])
-                + pair(xnc[:, h, :], xns[:, h, :], W_A, halves[n])
-                + pair(xrc[:, j, :], xrs[:, j, :], W_B, halves[n]),
-            )
+            return edge_rows[(h, j // 4)][:, j % 4, :]
 
-        def st_m(t, n):
-            if n == 0:
-                en[t] = work.tile([P, C], F32, name="en", tag="en", bufs=6)
-                acc[t] = accs[:, t % 8, :]
-            nc.scalar.activation(
-                out=en[t][:, halves[n]], in_=m_ps[(t, n)][:], func=ACT.Identity,
-                accum_out=acc[t][:, 2 * n:2 * n + 1],
-            )
-            if n == 1:
-                junk = work.tile([P, C], BF16, name="junk", tag="junk", bufs=2)
-                nc.scalar.activation(out=junk[:], in_=en[t][:], func=ACT.Square, accum_out=acc[t][:, 1:2])
+        def transpose_edges(t):
+            if is_tile(t):
+                transposed[t] = psum.tile([P, BANK], F32, name="transposed", tag="transposed", bufs=2)
+                transpose_words(transposed[t], edge_of(t).bitcast(F32))
 
-        def st_d(t):
-            norm_relu(t, en[t][:], en[t][:])
-
-        def st_e(t):
-            j, h = t // 2, t % 2
-            add_back(t, en[t][:], en[t][:], edge_in(t))
-            nc.sync.dma_start(out=o1[:, h, j, :], in_=en[t][:])
-
-        def st_f1(t):
-            if t < 2:
-                exx[t] = sums[t]
-            else:
-                exx[t] = work.tile([P, 2, C], F32, name="exx", tag="exx", bufs=4, align_bytes=64)
-            nc.scalar.activation(out=exx[t][:, 0, :], in_=en[t][:], func=ACT.Tanh, scale=0.5)
-
-        def st_f2(t):
-            nc.scalar.activation(out=exx[t][:, 0, :], in_=exx[t][:, 0, :], func=ACT.Exp, scale=0.5)
-
-        def st_h(t):
-            if t >= TILES - 2:
-                nc.vector.tensor_tensor(
-                    out=sums[t % 2][:, 0, :], in0=sums[t % 2][:, 0, :], in1=exx[t][:, 0, :], op=ALU.add
+        def copy_transposed(t):
+            if is_tile(t):
+                e_grouped[t] = work.tile(
+                    [P, C], BF16, name="e_grouped", tag="e_grouped", bufs=E_GROUPED_BUFS, align_bytes=64
                 )
-                if t % 2 == 0:
-                    node_ln(0)
+                nc.scalar.copy(
+                    out=e_grouped[t][:].bitcast(F32).rearrange("p (g r u) -> p g r u", g=2, u=2),
+                    in_=grouped_read(transposed[t]),
+                )
+
+        def quantise_edges(t):
+            if is_tile(t):
+                e_codes[t] = work.tile(
+                    [P, WORDS], U32, name="e_codes", tag="e_codes", bufs=E_CODES_BUFS, align_bytes=64
+                )
+                e_scales[t] = work.tile(
+                    [P, WORDS], U8, name="e_scales", tag="e_scales", bufs=E_CODES_BUFS, align_bytes=64
+                )
+                nc.vector.quantize_mx(out=e_codes[t][:].bitcast(FP8X4), scales=e_scales[t][:], in_=e_grouped[t][:])
+
+        def fill_bank(t, n):
+            if is_tile(t):
+                j, h = t // 2, t % 2
+                m_ps[(t, n)] = psum.tile([P, BANK], F32, name="m_ps", tag="m", bufs=3)
+                mx_group(
+                    m_ps[(t, n)][:],
+                    passes(e_codes[t], e_scales[t], W_E, halves[n])
+                    + passes(x_codes[:, h, :], x_scales[:, h, :], W_A, halves[n])
+                    + passes(xj_codes[:, j, :], xj_scales[:, j, :], W_B, halves[n]),
+                )
+
+        def empty_bank(t, n):
+            if is_tile(t):
+                if n == 0:
+                    edge_new[t] = work.tile([P, C], F32, name="edge_new", tag="edge_new", bufs=EDGE_NEW_BUFS)
+                    sums_of[t] = row_sums[:, t % 8, :]
+                nc.scalar.activation(
+                    out=edge_new[t][:, halves[n]], in_=m_ps[(t, n)][:], func=ACT.Identity,
+                    accum_out=sums_of[t][:, 2 * n:2 * n + 1],
+                )
+                if n == 1:
+                    squares = work.tile([P, C], BF16, name="squares", tag="squares")
+                    nc.scalar.activation(
+                        out=squares[:], in_=edge_new[t][:], func=ACT.Square, accum_out=sums_of[t][:, 1:2]
+                    )
+
+        def edge_average(t):
+            if is_tile(t):
+                average_over_batches(t)
+
+        def edge_variance(t):
+            if is_tile(t):
+                variance(t)
+
+        def edge_scale_and_bias(t):
+            if is_tile(t):
+                col = (t % 2) * NODES + t // 2
+                scale_and_bias(t, params[:, col:col + 1], params[:, 32 + col:33 + col])
+
+        def normalise(t):
+            if is_tile(t):
+                scaled_max(t, edge_new[t][:], edge_new[t][:])
+
+        def finish_edge_new(t):
+            if is_tile(t):
+                j, h = t // 2, t % 2
+                add_residual(t, edge_new[t][:], edge_new[t][:], edge_of(t))
+                nc.sync.dma_start(out=edge_new_view[:, h, j, :], in_=edge_new[t][:])
+
+        def tanh_half(t):
+            if is_tile(t):
+                if t < 2:
+                    exps[t] = sums[t]
                 else:
-                    with tc.manual_schedule():
-                        node_ln(1)
-                        node_exp(1)
-                        node_exp(0)
-            for n in range(2):
-                nc.vector.tensor_tensor(
-                    out=exx[t][:, 1, halves[n]], in0=exx[t][:, 0, halves[n]], in1=vx[(t // 2, n)][:],
-                    op=ALU.mult,
-                )
+                    exps[t] = work.tile([P, 2, C], F32, name="exps", tag="exps", bufs=EXPS_BUFS, align_bytes=64)
+                nc.scalar.activation(out=exps[t][:, 0, :], in_=edge_new[t][:], func=ACT.Tanh, scale=0.5)
 
-        def st_gi(t):
-            if 2 <= t < TILES - 2:
-                nc.vector.tensor_tensor(out=sums[t % 2][:], in0=sums[t % 2][:], in1=exx[t][:], op=ALU.add)
-            elif t >= 2:
-                nc.vector.tensor_tensor(
-                    out=sums[t % 2][:, 1, :], in0=sums[t % 2][:, 1, :], in1=exx[t][:, 1, :], op=ALU.add
-                )
+        def exp_half(t):
+            if is_tile(t):
+                nc.scalar.activation(out=exps[t][:, 0, :], in_=exps[t][:, 0, :], func=ACT.Exp, scale=0.5)
 
-        def st_vx(j):
-            for n in range(2):
-                vx[(j, n)] = psum.tile([P, 512], F32, name="vx_ps", tag="vx", bufs=2)
-                mx_group(vx[(j, n)][:], pair(xrc[:, j, :], xrs[:, j, :], W_V, halves[n]))
+        def log_of_sum(h):
+            nc.scalar.activation(out=sums[h][:, 0, :], in_=sums[h][:, 0, :], func=ACT.Ln)
 
-        def st_c4_edge(t):
-            col = (t % 2) * NODES + t // 2
-            st_c4(t, prm[:, col:col + 1], prm[:, 32 + col:33 + col])
+        def inverse_of_sum(h):
+            nc.scalar.activation(out=sums[h][:, 0, :], in_=sums[h][:, 0, :], func=ACT.Exp, scale=-1.0)
 
-        stages = {
-            "A1": st_a1, "A2": st_a2, "A3": st_a3, "C2": st_c2, "C3": st_c3, "C4": st_c4_edge, "D": st_d,
-            "E": st_e, "F1": st_f1, "F2": st_f2, "H": st_h, "GI": st_gi,
-        }
+        def times_vx(t):
+            if is_tile(t):
+                h = t % 2
+                if t >= TILES - 2:
+                    nc.vector.tensor_tensor(
+                        out=sums[h][:, 0, :], in0=sums[h][:, 0, :], in1=exps[t][:, 0, :], op=ALU.add
+                    )
+                    if h == 0:
+                        log_of_sum(0)
+                    else:
+                        with tc.manual_schedule():
+                            log_of_sum(1)
+                            inverse_of_sum(1)
+                            inverse_of_sum(0)
+                for n in range(2):
+                    nc.vector.tensor_tensor(
+                        out=exps[t][:, 1, halves[n]], in0=exps[t][:, 0, halves[n]], in1=vx_ps[(t // 2, n)][:],
+                        op=ALU.mult,
+                    )
+
+        def add_to_sums(t):
+            if is_tile(t):
+                h = t % 2
+                if 2 <= t < TILES - 2:
+                    nc.vector.tensor_tensor(out=sums[h][:], in0=sums[h][:], in1=exps[t][:], op=ALU.add)
+                elif t >= 2:
+                    nc.vector.tensor_tensor(
+                        out=sums[h][:, 1, :], in0=sums[h][:, 1, :], in1=exps[t][:, 1, :], op=ALU.add
+                    )
+
+        def fill_vx(t):
+            if is_tile(t) and t % 2 == 0:
+                j = t // 2
+                for n in range(2):
+                    vx_ps[(j, n)] = psum.tile([P, BANK], F32, name="vx_ps", tag="vx", bufs=2)
+                    mx_group(vx_ps[(j, n)][:], passes(xj_codes[:, j, :], xj_scales[:, j, :], W_V, halves[n]))
+
+        def late_piece(t):
+            if -1 <= t <= 2:
+                return 13 + t, (0, 1)
+            if 4 <= t < 12:
+                return 16 + (t - 4) // 2, ((t - 4) % 2,)
+            return None, ()
+
+        def late_transposes(t):
+            k, row_tiles = late_piece(t)
+            tag = "vx" if len(row_tiles) == 2 else "transposed"
+            for a in row_tiles:
+                w_banks[(k, a)] = psum.tile([P, BANK], F32, name="w_bank", tag=tag, bufs=2)
+            for a in row_tiles:
+                transpose_piece_rows(k, a, w_banks[(k, a)][:])
+            if len(row_tiles) == 2:
+                load_piece(k + 4)
+
+        def late_copies(t):
+            k, row_tiles = late_piece(t)
+            for a in row_tiles:
+                if a == 0:
+                    new_grouped(k)
+                copy_piece_rows(k, a, w_banks[(k, a)][:])
+
+        def late_quantise(t):
+            k, row_tiles = late_piece(t - 1)
+            if 1 in row_tiles:
+                quantise_piece(k)
 
         def period(t):
-            for name, off in SEQ:
-                s = t + off
-                if name in ("XP", "XS", "XQ"):
-                    late_weights(name, t)
-                elif name == "VX":
-                    if s >= 0 and s % 2 == 0 and s // 2 < NODES:
-                        st_vx(s // 2)
-                elif 0 <= s < TILES:
-                    if name in ("B0", "B1"):
-                        st_b(s, int(name[1]))
-                    elif name in ("M0", "M1"):
-                        st_m(s, int(name[1]))
-                    else:
-                        stages[name](s)
+            edge_average(t - 1)
+            transpose_edges(t + 2)
+            late_transposes(t)
+            edge_variance(t - 1)
+            late_quantise(t)
+            empty_bank(t, 1)
+            fill_bank(t + 1, 0)
+            edge_scale_and_bias(t - 1)
+            copy_transposed(t + 2)
+            late_copies(t)
+            tanh_half(t - 2)
+            fill_bank(t + 1, 1)
+            exp_half(t - 2)
+            times_vx(t - 4)
+            fill_vx(t - 3)
+            empty_bank(t + 1, 0)
+            add_to_sums(t - 4)
+            quantise_edges(t + 2)
+            normalise(t - 1)
+            finish_edge_new(t - 1)
 
-        pst = keep.tile([P, 96], BF16, name="pst")
-        nc.vector.memset(pst[:], 0.0)
-        nc.sync.dma_start(out=pst[0:8, 0:32], in_=bne_w.rearrange("(l x) -> l x", l=8))
-        nc.sync.dma_start(out=pst[0:8, 32:64], in_=bne_b.rearrange("(l x) -> l x", l=8))
-        nc.sync.dma_start(out=pst[0:8, 64:66], in_=bnv_w.rearrange("(l x) -> l x", l=8))
-        nc.sync.dma_start(out=pst[0:8, 80:82], in_=bnv_b.rearrange("(l x) -> l x", l=8))
-        xs = work.tile([P, 2, C], BF16, name="xs", tag="en", bufs=6)
-        nc.sync.dma_start(out=xs[:], in_=xv)
-        loaded = [load_piece(k) for k in range(4)]
-        pf = keep.tile([P, 96], F32, name="pf")
-        nc.vector.tensor_scalar(out=pf[:], in0=pst[:], scalar1=16384.0, scalar2=None, op0=ALU.mult)
-        pp = psum.tile([P, 96], F32, name="pp", tag="st")
-        nc.tensor.matmul(pp[:], lhsT=avg_pos[:], rhs=pf[:], start=True, stop=True)
-        prm = keep.tile([P, 96], F32, name="prm")
-        nc.vector.tensor_copy(out=prm[:], in_=pp[:])
+        x_rows = work.tile([P, 2, C], BF16, name="x_rows", tag="edge_new", bufs=EDGE_NEW_BUFS)
+        nc.sync.dma_start(out=x_rows[:], in_=x_view)
+        for k in range(4):
+            load_piece(k)
+        params_rows = resident.tile([P, 96], BF16, name="params_rows")
+        nc.vector.memset(params_rows[:], 0.0)
+        nc.sync.dma_start(out=params_rows[0:8, 0:32], in_=bne_w.rearrange("(l x) -> l x", l=8))
+        nc.sync.dma_start(out=params_rows[0:8, 32:64], in_=bne_b.rearrange("(l x) -> l x", l=8))
+        nc.sync.dma_start(out=params_rows[0:8, 64:66], in_=bnv_w.rearrange("(l x) -> l x", l=8))
+        nc.sync.dma_start(out=params_rows[0:8, 80:82], in_=bnv_b.rearrange("(l x) -> l x", l=8))
 
-        rotation = [("m", 3), ("vx", 2), ("tr", 2), ("m", 3), ("vx", 2), ("tr", 2), ("m", 3)]
-        n_banks = [0]
+        rotation = [("m", 3), ("vx", 2), ("transposed", 2), ("m", 3), ("vx", 2), ("transposed", 2), ("m", 3)]
+        banks_taken = [0]
 
         def next_bank():
-            tag, bufs = rotation[n_banks[0] % 7]
-            n_banks[0] += 1
-            bank = psum.tile([P, 512], F32, name="bank", tag=tag, bufs=bufs)
+            tag, bufs = rotation[banks_taken[0] % len(rotation)]
+            banks_taken[0] += 1
+            bank = psum.tile([P, BANK], F32, name="bank", tag=tag, bufs=bufs)
             return bank
 
-        xg = []
+        x_grouped = []
         for h in range(2):
-            xbank = next_bank()
-            transpose_words(xbank[:], xs[:].bitcast(F32)[:, h, :])
-            g_t = keep.tile([P, C], BF16, name="xg%d" % h, align_bytes=64)
+            x_bank = next_bank()
+            transpose_words(x_bank[:], x_rows[:].bitcast(F32)[:, h, :])
+            grouped = resident.tile([P, C], BF16, name="x_grouped%d" % h, align_bytes=64)
             nc.scalar.copy(
-                out=g_t[:].bitcast(F32).rearrange("p (g r u) -> p g r u", g=2, u=2), in_=bank_view(xbank[:])
+                out=grouped[:].bitcast(F32).rearrange("p (g r u) -> p g r u", g=2, u=2),
+                in_=grouped_read(x_bank[:]),
             )
-            xg.append(g_t)
+            x_grouped.append(grouped)
         for h in range(2):
-            nc.vector.quantize_mx(out=xnc[:, h, :].bitcast(FP8X4), scales=xns[:, h, :], in_=xg[h][:])
+            nc.vector.quantize_mx(
+                out=x_codes[:, h, :].bitcast(FP8X4), scales=x_scales[:, h, :], in_=x_grouped[h][:]
+            )
 
         def repeat_x(q):
-            rep = work.tile([P, 2048], BF16, name="rep", tag="exx", bufs=4, align_bytes=64)
-            dst = rep[:].bitcast(F32).rearrange("p (jj g b l u) -> p jj g b l u", jj=2, g=2, b=16, l=8, u=2)
+            repeated = work.tile([P, 2048], BF16, name="repeated", tag="exps", bufs=EXPS_BUFS, align_bytes=64)
+            dst = repeated[:].bitcast(F32).rearrange(
+                "p (jj g b l u) -> p jj g b l u", jj=2, g=2, b=16, l=8, u=2
+            )
             for jj in range(2):
                 j = 2 * q + jj
-                src = xg[j % 2][:].bitcast(F32).rearrange("p (g b l u) -> p g b l u", g=2, b=16, l=8, u=2)
+                src = x_grouped[j % 2][:].bitcast(F32).rearrange("p (g b l u) -> p g b l u", g=2, b=16, l=8, u=2)
                 for g in range(2):
                     nc.vector.tensor_copy(
                         out=dst[:, jj, g, :, :, :],
                         in_=src[:, g, :, j // 2, :].unsqueeze(2).to_broadcast([P, 16, 8, 2]),
                     )
             nc.vector.quantize_mx(
-                out=xrc[:, 2 * q:2 * q + 2, :].rearrange("p j w -> p (j w)").bitcast(FP8X4),
-                scales=xrs[:, 2 * q:2 * q + 2, :].rearrange("p j w -> p (j w)"),
-                in_=rep[:],
+                out=xj_codes[:, 2 * q:2 * q + 2, :].rearrange("p j w -> p (j w)").bitcast(FP8X4),
+                scales=xj_scales[:, 2 * q:2 * q + 2, :].rearrange("p j w -> p (j w)"),
+                in_=repeated[:],
             )
 
-        def prep_piece(k, banks, on_scalar):
-            grp = new_group_tile()
-            for a in range(2):
-                weight_rows(loaded[k], grp, a, banks[a], on_scalar)
-            weight_quantise(k, grp)
-
-        def ring_banks():
-            b0 = next_bank()
-            b1 = next_bank()
-            return [b0[:], b1[:]]
-
-        late = {}
-        u_grp = {}
-
-        def late_weights(name, t):
-            if -1 <= t <= 2:
-                k = 13 + t
-                if name == "XP":
-                    late[k] = [psum.tile([P, 512], F32, name="wv_b", tag="vx", bufs=2) for a in range(2)]
-                    for a in range(2):
-                        transpose_words(late[k][a][:], loaded[k][:].bitcast(F32)[:, a, :])
-                    loaded.append(load_piece(k + 4))
-                elif name == "XS":
-                    u_grp[k] = new_group_tile()
-                    for a in range(2):
-                        evacuate_rows(u_grp[k], a, late[k][a][:])
-            if 4 <= t < 12:
-                k, a = 16 + (t - 4) // 2, (t - 4) % 2
-                if name == "XP":
-                    late[(k, a)] = psum.tile([P, 512], F32, name="wu_b", tag="tr", bufs=2)
-                    transpose_words(late[(k, a)][:], loaded[k][:].bitcast(F32)[:, a, :])
-                elif name == "XS":
-                    if a == 0:
-                        u_grp[k] = new_group_tile()
-                    evacuate_rows(u_grp[k], a, late[(k, a)][:])
-            if name == "XQ":
-                if 0 <= t <= 3:
-                    weight_quantise(12 + t, u_grp[12 + t])
-                if 6 <= t <= 12 and t % 2 == 0:
-                    weight_quantise(13 + t // 2, u_grp[13 + t // 2])
-
-        def evacuate_rows(grp, a, bank):
-            dst = grp[:].bitcast(F32).rearrange("p (g c u) -> p g c u", g=2, u=2)[:, :, a * P:(a + 1) * P, :]
-            nc.scalar.copy(out=dst, in_=bank_view(bank))
-
         for k in range(12):
+            if k == 6:
+                params_scaled = resident.tile([P, 96], F32, name="params_scaled")
+                nc.vector.tensor_scalar(
+                    out=params_scaled[:], in0=params_rows[:], scalar1=float(SAMPLES), scalar2=None, op0=ALU.mult
+                )
+                params_ps = psum.tile([P, 96], F32, name="params_ps", tag="stats")
+                nc.tensor.matmul(params_ps[:], lhsT=avg_pos[:], rhs=params_scaled[:], start=True, stop=True)
+                params = resident.tile([P, 96], F32, name="params")
+                nc.vector.tensor_copy(out=params[:], in_=params_ps[:])
             if k % 2 == 0:
                 repeat_x(k // 2)
-            prep_piece(k, ring_banks(), True)
+            new_grouped(k)
+            banks = [next_bank(), next_bank()]
+            for a in range(2):
+                transpose_piece_rows(k, a, banks[a][:])
+                copy_piece_rows(k, a, banks[a][:])
+            quantise_piece(k)
             if k == 4:
                 for h in range(2):
                     load_edges(h, 0, 0, 1)
             if k == 8:
                 for h in range(2):
                     load_edges(h, 0, 1, 2)
-            loaded.append(load_piece(k + 4))
+            load_piece(k + 4)
             if k == 7:
                 period(-2)
         for h in range(2):
@@ -412,15 +466,9 @@ def tile_gnn_s2_pa_t_kernel(
         for h in range(2):
             load_edges(h, 1, 0, 4)
 
-        def node_ln(h):
-            nc.scalar.activation(out=sums[h][:, 0, :], in_=sums[h][:, 0, :], func=ACT.Ln)
-
-        def node_exp(h):
-            nc.scalar.activation(out=sums[h][:, 0, :], in_=sums[h][:, 0, :], func=ACT.Exp, scale=-1.0)
-
+        ux_ps = {}
         period(-1)
-        u_ps = {}
-        for t in range(TILES + 5):
+        for t in range(TILES + 4):
             period(t)
             if t in (0, 1):
                 repeat_x(t + 6)
@@ -428,22 +476,21 @@ def tile_gnn_s2_pa_t_kernel(
                 for h in range(2):
                     load_edges(h, (t + 7) // 8, 0, 4)
             if t == TILES + 1:
-                warm = small.tile([P, 1], F32, name="warm", tag="warm")
-                nc.scalar.activation(out=warm[:], in_=exx[TILES - 1][:, 0, 0:1], func=ACT.Ln)
+                warm = columns.tile([P, 1], F32, name="warm", tag="warm")
+                nc.scalar.activation(out=warm[:], in_=exps[TILES - 1][:, 0, 0:1], func=ACT.Ln)
             if t == TILES:
+                free_banks = (("m", 3), ("m", 3), ("m", 3), ("transposed", 2))
                 for h in range(2):
                     for n in range(2):
-                        u_tag, u_bufs = (("m", 3), ("m", 3), ("m", 3), ("tr", 2))[2 * h + n]
-                        u_ps[(h, n)] = psum.tile([P, 512], F32, name="u_ps", tag=u_tag, bufs=u_bufs)
-                        mx_group(u_ps[(h, n)][:], pair(xnc[:, h, :], xns[:, h, :], W_U, halves[n]))
+                        tag, bufs = free_banks[2 * h + n]
+                        ux_ps[(h, n)] = psum.tile([P, BANK], F32, name="ux_ps", tag=tag, bufs=bufs)
+                        mx_group(ux_ps[(h, n)][:], passes(x_codes[:, h, :], x_scales[:, h, :], W_U, halves[n]))
 
-        y = {}
-        r = {}
-        st6 = {}
+        y, x_new, chunk_stats = {}, {}, {}
 
         def node_y(h):
-            y[h] = work.tile([P, C], F32, name="y", tag="en", bufs=6)
-            st6[h] = small.tile([P, 2, 6], F32, name="st6", tag="st6")
+            y[h] = work.tile([P, C], F32, name="y", tag="edge_new", bufs=EDGE_NEW_BUFS)
+            chunk_stats[h] = columns.tile([P, 2, 6], F32, name="chunk_stats", tag="chunk_stats")
             for n in range(2):
                 nc.vector.tensor_tensor(
                     out=sums[h][:, 1, halves[n]], in0=sums[h][:, 1, halves[n]], in1=sums[h][:, 0, halves[n]],
@@ -451,33 +498,35 @@ def tile_gnn_s2_pa_t_kernel(
                 )
                 nc.vector.scalar_tensor_tensor(
                     out=y[h][:, halves[n]], in0=sums[h][:, 1, halves[n]], scalar=1.0 / NODES,
-                    in1=u_ps[(h, n)][:], op0=ALU.mult, op1=ALU.add,
+                    in1=ux_ps[(h, n)][:], op0=ALU.mult, op1=ALU.add,
                 )
-                nc.vector.bn_stats(out=st6[h][:, n, :], in_=y[h][:, halves[n]])
-            mv = small.tile([P, 2], F32, name="mv", tag="mv")
-            nc.vector.bn_aggr(out=mv[:], in_=st6[h][:].rearrange("p a s -> p (a s)"))
+                nc.vector.bn_stats(out=chunk_stats[h][:, n, :], in_=y[h][:, halves[n]])
+            mean_var = columns.tile([P, 2], F32, name="mean_var", tag="mean_var")
+            nc.vector.bn_aggr(out=mean_var[:], in_=chunk_stats[h][:].rearrange("p a s -> p (a s)"))
             nc.vector.scalar_tensor_tensor(
-                out=mv[:, 1:2], in0=mv[:, 0:1], scalar=mv[:, 0:1], in1=mv[:, 1:2], op0=ALU.mult, op1=ALU.add
+                out=mean_var[:, 1:2], in0=mean_var[:, 0:1], scalar=mean_var[:, 0:1], in1=mean_var[:, 1:2],
+                op0=ALU.mult, op1=ALU.add,
             )
-            acc[100 + h] = small.tile([P, 4], F32, name="acc", tag="acc")
+            sums_of[NODE_KEY + h] = columns.tile([P, 4], F32, name="node_sums", tag="node_sums")
             for n in range(2):
                 nc.vector.tensor_scalar(
-                    out=acc[100 + h][:, 2 * n:2 * n + 2], in0=mv[:], scalar1=512.0, scalar2=None, op0=ALU.mult
+                    out=sums_of[NODE_KEY + h][:, 2 * n:2 * n + 2], in0=mean_var[:], scalar1=C / 2.0, scalar2=None,
+                    op0=ALU.mult,
                 )
 
         def node_out(h):
-            key = 100 + h
-            st_c3(key)
-            st_c4(key, prm[:, 64 + h:65 + h], prm[:, 80 + h:81 + h])
-            r[h] = work.tile([P, C], F32, name="r", tag="en", bufs=6)
+            key = NODE_KEY + h
+            variance(key)
+            scale_and_bias(key, params[:, 64 + h:65 + h], params[:, 80 + h:81 + h])
+            x_new[h] = work.tile([P, C], F32, name="x_new", tag="edge_new", bufs=EDGE_NEW_BUFS)
             for n in range(2):
-                norm_relu(key, r[h][:, halves[n]], y[h][:, halves[n]])
-                add_back(key, r[h][:, halves[n]], r[h][:, halves[n]], y[h][:, halves[n]])
-                nc.sync.dma_start(out=o0[:, h, halves[n]], in_=r[h][:, halves[n]])
+                scaled_max(key, x_new[h][:, halves[n]], y[h][:, halves[n]])
+                add_residual(key, x_new[h][:, halves[n]], x_new[h][:, halves[n]], y[h][:, halves[n]])
+                nc.sync.dma_start(out=x_new_view[:, h, halves[n]], in_=x_new[h][:, halves[n]])
 
         node_y(0)
-        st_c2(100)
+        average_over_batches(NODE_KEY)
         node_y(1)
         node_out(0)
-        st_c2(101)
+        average_over_batches(NODE_KEY + 1)
         node_out(1)

@@ -22,23 +22,27 @@ EPS = 1e-5
 SAMPLES = 16 * C
 FLOPS = 2 * (4096 + 4 * 256) * C * C
 
-W_E, W_A, W_B, W_V, W_U = 0, 1, 2, 3, 4
+W_E, W_B, W_A, W_V, W_U = 0, 1, 2, 3, 4
 PIECE = 256
 NODE_KEY = 100
 
 W_ROWS_BUFS = 4
-W_GROUPED_BUFS = 3
-E_GROUPED_BUFS = 3
+W_GROUPED_BUFS = 4
+E_GROUPED_BUFS = 2
 E_CODES_BUFS = 4
-EDGE_NEW_BUFS = 7
-EXPS_BUFS = 4
+EDGE_ROWS_BUFS = 3
+EDGE_NEW_BUFS = 6
+EXP_BUFS = 3
+EV_BUFS = 3
+VX_BUFS = 4
+VX_LAG = 4
 
 
 def tile_gnn_s2_pa_t_kernel(
     tc, x, edge, Wu, Wv, Wa, Wb, We, bnv_w, bnv_b, bne_w, bne_b, out_0, out_1
 ):
     nc = tc.nc
-    weights = [We, Wa, Wb, Wv, Wu]
+    weights = [We, Wb, Wa, Wv, Wu]
     edge_view = edge.rearrange("b (l h j) c -> (b l) h j c", h=2, j=NODES)
     edge_new_view = out_1.rearrange("b (l h j) c -> (b l) h j c", h=2, j=NODES)
     x_view = x.rearrange("b (l h) c -> (b l) h c", h=2)
@@ -51,6 +55,7 @@ def tile_gnn_s2_pa_t_kernel(
         work = ctx.enter_context(tc.tile_pool(name="work", bufs=2))
         columns = ctx.enter_context(tc.tile_pool(name="columns", bufs=8))
         psum = ctx.enter_context(tc.psum_pool(name="psum", bufs=1))
+        sum_tags = {"exp": ("sum_exp0", "sum_exp1"), "ev": ("sum_ev0", "sum_ev1")}
 
         ident = resident.tile([P, P], F32, name="ident")
         make_identity(nc, ident[:])
@@ -60,19 +65,12 @@ def tile_gnn_s2_pa_t_kernel(
         )
         avg_pos = resident.tile([P, P], F32, name="avg_pos")
         avg_neg = resident.tile([P, P], F32, name="avg_neg")
-        nc.vector.tensor_scalar(
-            out=avg_pos[:].rearrange("p (b l) -> p b l", l=8),
-            in0=same_l[:].unsqueeze(1).to_broadcast([P, 16, 8]),
-            scalar1=1.0 / SAMPLES, scalar2=None, op0=ALU.mult,
-        )
-        nc.vector.tensor_scalar(
-            out=avg_neg[:].rearrange("p (b l) -> p b l", l=8),
-            in0=same_l[:].unsqueeze(1).to_broadcast([P, 16, 8]),
-            scalar1=-1.0 / SAMPLES, scalar2=None, op0=ALU.mult,
-        )
-        eps_row = resident.tile([P, 4], F32, name="eps_row")
-        nc.vector.memset(eps_row[:], 0.0)
-        nc.vector.memset(eps_row[:, 1:2], EPS)
+        for avg, sign in ((avg_pos, 1.0), (avg_neg, -1.0)):
+            nc.vector.tensor_scalar(
+                out=avg[:].rearrange("p (b l) -> p b l", l=8),
+                in0=same_l[:].unsqueeze(1).to_broadcast([P, 16, 8]),
+                scalar1=sign / SAMPLES, scalar2=None, op0=ALU.mult,
+            )
         minus_half = resident.tile([P, 1], F32, name="minus_half")
         nc.vector.memset(minus_half[:], -0.5)
 
@@ -82,9 +80,13 @@ def tile_gnn_s2_pa_t_kernel(
         x_scales = resident.tile([P, 2, WORDS], U8, name="x_scales", align_bytes=64)
         xj_codes = resident.tile([P, NODES, WORDS], U32, name="xj_codes", align_bytes=64)
         xj_scales = resident.tile([P, NODES, WORDS], U8, name="xj_scales", align_bytes=64)
-        sums = [resident.tile([P, 2, C], F32, name="sums%d" % h) for h in range(2)]
+        ax = [resident.tile([P, C], F32, name="ax%d" % h) for h in range(2)]
+        sum_exp0 = resident.tile([P, C], F32, name="sum_exp0")
+        sum_ev0 = resident.tile([P, C], F32, name="sum_ev0")
+        ux = [resident.tile([P, C], F32, name="ux%d" % h) for h in range(2)]
         row_sums = resident.tile([P, 8, 4], F32, name="row_sums")
         nc.vector.memset(row_sums[:], 0.0)
+        nc.vector.memset(row_sums[:, :, 3:4], EPS * SAMPLES / 16)
 
         def transpose_words(bank, rows_as_words):
             for k in range(4):
@@ -113,7 +115,6 @@ def tile_gnn_s2_pa_t_kernel(
 
         w_rows = {}
         w_grouped = {}
-        w_banks = {}
 
         def load_piece(k):
             w, part = k // 4, k % 4
@@ -123,17 +124,17 @@ def tile_gnn_s2_pa_t_kernel(
                 in_=weights[w][part * PIECE:(part + 1) * PIECE, :].rearrange("(a p) k -> p a k", p=P),
             )
 
-        def new_grouped(k):
+        def prepare_piece(k, next_bank):
             w_grouped[k] = staging.tile(
                 [P, 2048], BF16, name="w_grouped", tag="w_grouped", bufs=W_GROUPED_BUFS, align_bytes=64
             )
-
-        def transpose_piece_rows(k, a, bank):
-            transpose_words(bank, w_rows[k][:].bitcast(F32)[:, a, :])
-
-        def copy_piece_rows(k, a, bank):
             dst = w_grouped[k][:].bitcast(F32).rearrange("p (g c u) -> p g c u", g=2, u=2)
-            nc.scalar.copy(out=dst[:, :, a * P:(a + 1) * P, :], in_=grouped_read(bank))
+            for a in range(2):
+                bank = next_bank()
+                transpose_words(bank[:], w_rows[k][:].bitcast(F32)[:, a, :])
+                nc.scalar.copy(out=dst[:, :, a * P:(a + 1) * P, :], in_=grouped_read(bank[:]))
+            if k + 4 < 20:
+                load_piece(k + 4)
 
         def quantise_piece(k):
             w, part = k // 4, k % 4
@@ -144,10 +145,10 @@ def tile_gnn_s2_pa_t_kernel(
                     in_=w_grouped[k][:, g * 1024:(g + 1) * 1024],
                 )
 
-        sums_of, means_ps, moments, scale_bias, rstd = {}, {}, {}, {}, {}
+        sums_of, means_ps, moments, scale_bias = {}, {}, {}, {}
 
         def average_over_batches(key):
-            means_ps[key] = psum.tile([P, 4], F32, name="means_ps", tag="stats")
+            means_ps[key] = psum.tile([P, 4], F32, name="means_ps", tag="stats", bufs=1)
             for i, avg in enumerate((avg_pos, avg_neg)):
                 for n in range(2):
                     nc.tensor.matmul(
@@ -158,51 +159,52 @@ def tile_gnn_s2_pa_t_kernel(
         def variance(key):
             moments[key] = columns.tile([P, 8], F32, name="moments", tag="moments")
             mo = moments[key]
-            nc.vector.tensor_tensor(out=mo[:, 0:4], in0=means_ps[key][:], in1=eps_row[:], op=ALU.add)
-            nc.vector.scalar_tensor_tensor(
-                out=mo[:, 4:5], in0=mo[:, 0:1], scalar=mo[:, 2:3], in1=mo[:, 1:2], op0=ALU.mult, op1=ALU.add
+            nc.scalar.copy(out=mo[:, 0:4], in_=means_ps[key][:])
+            nc.scalar.activation(
+                out=mo[:, 4:5], in_=means_ps[key][:, 0:1], func=ACT.Identity, scale=mo[:, 2:3], bias=mo[:, 1:2]
             )
 
         def scale_and_bias(key, gain, offset):
-            scale_bias[key] = columns.tile([P, 4], F32, name="scale_bias", tag="scale_bias")
+            scale_bias[key] = columns.tile([P, 2], F32, name="scale_bias", tag="scale_bias")
+            rstd = columns.tile([P, 1], F32, name="rstd", tag="rstd")
             sb, mo = scale_bias[key], moments[key]
-            rstd[key] = columns.tile([P, 1], F32, name="rstd", tag="rstd")
-            nc.gpsimd.tensor_tensor(out=rstd[key][:], in0=mo[:, 4:5], in1=minus_half[:], op=ALU.pow)
-            nc.vector.tensor_tensor(out=sb[:, 1:2], in0=rstd[key][:], in1=gain, op=ALU.mult)
-            nc.vector.tensor_scalar(
-                out=sb[:, 2:3], in0=sb[:, 1:2], scalar1=mo[:, 0:1], scalar2=offset, op0=ALU.mult, op1=ALU.subtract
+            nc.gpsimd.tensor_tensor(out=rstd[:], in0=mo[:, 4:5], in1=minus_half[:], op=ALU.pow)
+            nc.gpsimd.tensor_tensor(out=sb[:, 0:1], in0=rstd[:], in1=gain, op=ALU.mult)
+            nc.gpsimd.tensor_scalar(
+                out=sb[:, 1:2], in0=sb[:, 0:1], scalar1=mo[:, 0:1], scalar2=offset, op0=ALU.mult, op1=ALU.subtract
             )
 
         def scaled_max(key, dst, src):
             nc.vector.tensor_scalar(
-                out=dst, in0=src, scalar1=scale_bias[key][:, 1:2], scalar2=scale_bias[key][:, 2:3],
+                out=dst, in0=src, scalar1=scale_bias[key][:, 0:1], scalar2=scale_bias[key][:, 1:2],
                 op0=ALU.mult, op1=ALU.max,
             )
 
         def add_residual(key, dst, src, residual):
             nc.vector.scalar_tensor_tensor(
-                out=dst, in0=src, scalar=scale_bias[key][:, 2:3], in1=residual, op0=ALU.subtract, op1=ALU.add
+                out=dst, in0=src, scalar=scale_bias[key][:, 1:2], in1=residual, op0=ALU.subtract, op1=ALU.add
             )
 
-        edge_rows, transposed, e_grouped, e_codes, e_scales, m_ps, edge_new, exps, vx_ps = (
-            {}, {}, {}, {}, {}, {}, {}, {}, {}
+        edge_rows, transposed, e_grouped, e_codes, e_scales, m_ps, edge_new, exps, evs, vx = (
+            {}, {}, {}, {}, {}, {}, {}, {}, {}, {}
         )
+        sums_ps = {}
 
         def is_tile(t):
             return 0 <= t < TILES
 
-        def load_edges(h, q, lo, hi):
+        def load_edges(q, lo, hi):
             if lo == 0:
-                edge_rows[(h, q)] = staging.tile([P, 4, C], BF16, name="edge_rows", tag="edge_rows%d" % h)
-            nc.sync.dma_start(out=edge_rows[(h, q)][:, lo:hi, :], in_=edge_view[:, h, 4 * q + lo:4 * q + hi, :])
+                edge_rows[q] = staging.tile([P, 4, C], BF16, name="edge_rows", tag="edge_rows", bufs=EDGE_ROWS_BUFS)
+            h, j = q // 4, 4 * (q % 4)
+            nc.sync.dma_start(out=edge_rows[q][:, lo:hi, :], in_=edge_view[:, h, j + lo:j + hi, :])
 
         def edge_of(t):
-            j, h = t // 2, t % 2
-            return edge_rows[(h, j // 4)][:, j % 4, :]
+            return edge_rows[t // 4][:, t % 4, :]
 
         def transpose_edges(t):
             if is_tile(t):
-                transposed[t] = psum.tile([P, BANK], F32, name="transposed", tag="transposed", bufs=2)
+                transposed[t] = psum.tile([P, BANK], F32, name="transposed", tag="transposed", bufs=1)
                 transpose_words(transposed[t], edge_of(t).bitcast(F32))
 
         def copy_transposed(t):
@@ -227,12 +229,11 @@ def tile_gnn_s2_pa_t_kernel(
 
         def fill_bank(t, n):
             if is_tile(t):
-                j, h = t // 2, t % 2
-                m_ps[(t, n)] = psum.tile([P, BANK], F32, name="m_ps", tag="m", bufs=3)
+                j = t % NODES
+                m_ps[(t, n)] = psum.tile([P, BANK], F32, name="m_ps", tag="m", bufs=2)
                 mx_group(
                     m_ps[(t, n)][:],
                     passes(e_codes[t], e_scales[t], W_E, halves[n])
-                    + passes(x_codes[:, h, :], x_scales[:, h, :], W_A, halves[n])
                     + passes(xj_codes[:, j, :], xj_scales[:, j, :], W_B, halves[n]),
                 )
 
@@ -241,15 +242,18 @@ def tile_gnn_s2_pa_t_kernel(
                 if n == 0:
                     edge_new[t] = work.tile([P, C], F32, name="edge_new", tag="edge_new", bufs=EDGE_NEW_BUFS)
                     sums_of[t] = row_sums[:, t % 8, :]
-                nc.scalar.activation(
-                    out=edge_new[t][:, halves[n]], in_=m_ps[(t, n)][:], func=ACT.Identity,
-                    accum_out=sums_of[t][:, 2 * n:2 * n + 1],
+                nc.vector.scalar_tensor_tensor(
+                    out=edge_new[t][:, halves[n]], in0=m_ps[(t, n)][:], scalar=1.0, in1=ax[t // NODES][:, halves[n]],
+                    op0=ALU.mult, op1=ALU.add, accum_out=sums_of[t][:, 2 * n:2 * n + 1],
                 )
-                if n == 1:
-                    squares = work.tile([P, C], BF16, name="squares", tag="squares")
-                    nc.scalar.activation(
-                        out=squares[:], in_=edge_new[t][:], func=ACT.Square, accum_out=sums_of[t][:, 1:2]
-                    )
+
+        def sum_squares(key, src):
+            squares = work.tile([P, C], BF16, name="squares", tag="squares", bufs=1)
+            nc.scalar.activation(out=squares[:], in_=src, func=ACT.Square, accum_out=sums_of[key][:, 1:2])
+
+        def edge_squares(t):
+            if is_tile(t):
+                sum_squares(t, edge_new[t][:])
 
         def edge_average(t):
             if is_tile(t):
@@ -261,8 +265,7 @@ def tile_gnn_s2_pa_t_kernel(
 
         def edge_scale_and_bias(t):
             if is_tile(t):
-                col = (t % 2) * NODES + t // 2
-                scale_and_bias(t, params[:, col:col + 1], params[:, 32 + col:33 + col])
+                scale_and_bias(t, params[:, t:t + 1], params[:, 32 + t:33 + t])
 
         def normalise(t):
             if is_tile(t):
@@ -270,115 +273,153 @@ def tile_gnn_s2_pa_t_kernel(
 
         def finish_edge_new(t):
             if is_tile(t):
-                j, h = t // 2, t % 2
                 add_residual(t, edge_new[t][:], edge_new[t][:], edge_of(t))
-                nc.sync.dma_start(out=edge_new_view[:, h, j, :], in_=edge_new[t][:])
+                nc.sync.dma_start(out=edge_new_view[:, t // NODES, t % NODES, :], in_=edge_new[t][:])
 
         def tanh_half(t):
             if is_tile(t):
-                if t < 2:
-                    exps[t] = sums[t]
-                else:
-                    exps[t] = work.tile([P, 2, C], F32, name="exps", tag="exps", bufs=EXPS_BUFS, align_bytes=64)
-                nc.scalar.activation(out=exps[t][:, 0, :], in_=edge_new[t][:], func=ACT.Tanh, scale=0.5)
+                exps[t] = work.tile([P, C], F32, name="exps", tag="exps", bufs=EXP_BUFS)
+                nc.scalar.activation(out=exps[t][:], in_=edge_new[t][:], func=ACT.Tanh, scale=0.5)
 
         def exp_half(t):
             if is_tile(t):
-                nc.scalar.activation(out=exps[t][:, 0, :], in_=exps[t][:, 0, :], func=ACT.Exp, scale=0.5)
+                nc.scalar.activation(out=exps[t][:], in_=exps[t][:], func=ACT.Exp, scale=0.5)
 
-        def log_of_sum(h):
-            nc.scalar.activation(out=sums[h][:, 0, :], in_=sums[h][:, 0, :], func=ACT.Ln)
+        def new_ev():
+            ev = work.tile([P, C], F32, name="evs", tag="evs", bufs=EV_BUFS, align_bytes=64)
+            return ev
 
-        def inverse_of_sum(h):
-            nc.scalar.activation(out=sums[h][:, 0, :], in_=sums[h][:, 0, :], func=ACT.Exp, scale=-1.0)
+        def load_vx(t):
+            if is_tile(t):
+                vx[t] = work.tile([P, C], F32, name="vx", tag="vx", bufs=VX_BUFS)
+                nc.sync.dma_start(out=vx[t][:], in_=out_0[:, t % NODES, :].unsqueeze(1).to_broadcast([16, 8, C]))
 
         def times_vx(t):
             if is_tile(t):
-                h = t % 2
-                if t >= TILES - 2:
-                    nc.vector.tensor_tensor(
-                        out=sums[h][:, 0, :], in0=sums[h][:, 0, :], in1=exps[t][:, 0, :], op=ALU.add
-                    )
-                    if h == 0:
-                        log_of_sum(0)
-                    else:
-                        with tc.manual_schedule():
-                            log_of_sum(1)
-                            inverse_of_sum(1)
-                            inverse_of_sum(0)
-                for n in range(2):
-                    nc.vector.tensor_tensor(
-                        out=exps[t][:, 1, halves[n]], in0=exps[t][:, 0, halves[n]], in1=vx_ps[(t // 2, n)][:],
-                        op=ALU.mult,
+                evs[t] = new_ev()
+                nc.vector.tensor_tensor(out=evs[t][:], in0=exps[t][:], in1=vx[t][:], op=ALU.mult)
+
+        def add_to_sums(what, t, addend):
+            h, j = t // NODES, t % NODES
+            for n in range(2):
+                if j == 0:
+                    sums_ps[(what, h, n)] = psum.tile([P, BANK], F32, name="sums_ps", tag=sum_tags[what][n], bufs=1)
+                for k in range(4):
+                    col = n * BANK + k * P
+                    nc.tensor.matmul(
+                        sums_ps[(what, h, n)][:, k * P:(k + 1) * P], lhsT=addend[:, col:col + P], rhs=ident[:],
+                        start=(j == 0 and k == 0), stop=(j == NODES - 1 and k == 3), is_transpose=True,
                     )
 
-        def add_to_sums(t):
+        def sum_exp(t):
             if is_tile(t):
-                h = t % 2
-                if 2 <= t < TILES - 2:
-                    nc.vector.tensor_tensor(out=sums[h][:], in0=sums[h][:], in1=exps[t][:], op=ALU.add)
-                elif t >= 2:
-                    nc.vector.tensor_tensor(
-                        out=sums[h][:, 1, :], in0=sums[h][:, 1, :], in1=exps[t][:, 1, :], op=ALU.add
-                    )
+                add_to_sums("exp", t, exps[t])
 
-        def fill_vx(t):
-            if is_tile(t) and t % 2 == 0:
-                j = t // 2
+        def sum_ev(t):
+            if is_tile(t):
+                add_to_sums("ev", t, evs[t])
+
+        inverse, back, y = {}, {}, {}
+
+        def new_edge_new():
+            tile = work.tile([P, C], F32, name="edge_new", tag="edge_new", bufs=EDGE_NEW_BUFS)
+            return tile
+
+        def node_agg(h):
+            agg = new_ev()
+            for n in range(2):
+                nc.vector.tensor_tensor(
+                    out=agg[:, halves[n]], in0=sums_ps[("ev", 1, n)][:] if h == 1 else sum_ev0[:, halves[n]],
+                    in1=inverse[h][:, halves[n]], op=ALU.mult,
+                )
+                tag, bufs = ("m", 2) if h == 1 else (sum_tags["exp"][n], 1)
+                back[(h, n)] = psum.tile([P, BANK], F32, name="back", tag=tag, bufs=bufs)
+                transpose_words(back[(h, n)], agg[:, halves[n]])
+
+        def node_y(h):
+            y[h] = new_edge_new()
+            sums_of[NODE_KEY + h] = row_sums[:, h, :]
+            for n in range(2):
+                nc.vector.scalar_tensor_tensor(
+                    out=y[h][:, halves[n]], in0=back[(h, n)][:], scalar=1.0 / NODES, in1=ux[h][:, halves[n]],
+                    op0=ALU.mult, op1=ALU.add, accum_out=sums_of[NODE_KEY + h][:, 2 * n:2 * n + 1],
+                )
+            sum_squares(NODE_KEY + h, y[h][:])
+
+        def node_statistics(h):
+            key = NODE_KEY + h
+            average_over_batches(key)
+            variance(key)
+            scale_and_bias(key, params[:, 64 + h:65 + h], params[:, 80 + h:81 + h])
+
+        def node_out(h):
+            key = NODE_KEY + h
+            for n in range(2):
+                scaled_max(key, ux[h][:, halves[n]], y[h][:, halves[n]])
+                add_residual(key, ux[h][:, halves[n]], ux[h][:, halves[n]], y[h][:, halves[n]])
+                nc.sync.dma_start(out=x_new_view[:, h, halves[n]], in_=ux[h][:, halves[n]])
+
+        def product_half(w, h, n, tag, dst):
+            bank = psum.tile([P, BANK], F32, name="product", tag=tag, bufs=1)
+            mx_group(bank[:], passes(x_codes[:, h, :], x_scales[:, h, :], w, halves[n]))
+            nc.scalar.copy(out=dst[:, halves[n]], in_=bank[:])
+
+        def park_vx():
+            for h in range(2):
+                vx_rows = new_ev()
                 for n in range(2):
-                    vx_ps[(j, n)] = psum.tile([P, BANK], F32, name="vx_ps", tag="vx", bufs=2)
-                    mx_group(vx_ps[(j, n)][:], passes(xj_codes[:, j, :], xj_scales[:, j, :], W_V, halves[n]))
+                    product_half(W_V, h, n, sum_tags[("ev", "exp")[h]][n], vx_rows)
+                nc.sync.dma_start(out=x_new_view[:, h, :], in_=vx_rows[:])
 
-        def late_piece(t):
-            if -1 <= t <= 2:
-                return 13 + t, (0, 1)
-            if 4 <= t < 12:
-                return 16 + (t - 4) // 2, ((t - 4) % 2,)
-            return None, ()
+        free_tags = sum_tags["exp"] + sum_tags["ev"]
+        free_taken = [0]
 
-        def late_transposes(t):
-            k, row_tiles = late_piece(t)
-            tag = "vx" if len(row_tiles) == 2 else "transposed"
-            for a in row_tiles:
-                w_banks[(k, a)] = psum.tile([P, BANK], F32, name="w_bank", tag=tag, bufs=2)
-            for a in row_tiles:
-                transpose_piece_rows(k, a, w_banks[(k, a)][:])
-            if len(row_tiles) == 2:
-                load_piece(k + 4)
+        def free_bank():
+            tag = free_tags[free_taken[0] % 4]
+            free_taken[0] += 1
+            bank = psum.tile([P, BANK], F32, name="free_bank", tag=tag, bufs=1)
+            return bank
 
-        def late_copies(t):
-            k, row_tiles = late_piece(t)
-            for a in row_tiles:
-                if a == 0:
-                    new_grouped(k)
-                copy_piece_rows(k, a, w_banks[(k, a)][:])
+        late_pieces = {0: (12, 13, 14, 15), 1: (16, 17), 2: (18, 19)}
+
+        def late_prepare(t):
+            for k in late_pieces.get(t, ()):
+                prepare_piece(k, free_bank)
 
         def late_quantise(t):
-            k, row_tiles = late_piece(t - 1)
-            if 1 in row_tiles:
+            for k in late_pieces.get(t - 1, ()):
                 quantise_piece(k)
 
         def period(t):
-            edge_average(t - 1)
-            transpose_edges(t + 2)
-            late_transposes(t)
-            edge_variance(t - 1)
+            normalise(t - 2)
+            edge_squares(t - 1)
+            quantise_edges(t + 1)
             late_quantise(t)
-            empty_bank(t, 1)
-            fill_bank(t + 1, 0)
+            if t > 0:
+                fill_bank(t, 0)
+            times_vx(t - VX_LAG)
+            if is_tile(t - VX_LAG):
+                load_vx(t - VX_LAG + VX_BUFS)
+            tanh_half(t - 3)
+            sum_exp(t - 4)
+            edge_average(t - 1)
+            edge_variance(t - 1)
             edge_scale_and_bias(t - 1)
+            empty_bank(t, 0)
+            if t == NODES + VX_LAG:
+                for n in range(2):
+                    nc.vector.tensor_copy(out=sum_ev0[:, halves[n]], in_=sums_ps[("ev", 0, n)][:])
             copy_transposed(t + 2)
-            late_copies(t)
-            tanh_half(t - 2)
-            fill_bank(t + 1, 1)
-            exp_half(t - 2)
-            times_vx(t - 4)
-            fill_vx(t - 3)
-            empty_bank(t + 1, 0)
-            add_to_sums(t - 4)
-            quantise_edges(t + 2)
-            normalise(t - 1)
-            finish_edge_new(t - 1)
+            if t > 0:
+                fill_bank(t, 1)
+            finish_edge_new(t - 2)
+            exp_half(t - 3)
+            sum_ev(t - VX_LAG)
+            transpose_edges(t + 3)
+            if t == 1:
+                park_vx()
+            late_prepare(t)
+            empty_bank(t, 1)
 
         x_rows = work.tile([P, 2, C], BF16, name="x_rows", tag="edge_new", bufs=EDGE_NEW_BUFS)
         nc.sync.dma_start(out=x_rows[:], in_=x_view)
@@ -391,7 +432,7 @@ def tile_gnn_s2_pa_t_kernel(
         nc.sync.dma_start(out=params_rows[0:8, 64:66], in_=bnv_w.rearrange("(l x) -> l x", l=8))
         nc.sync.dma_start(out=params_rows[0:8, 80:82], in_=bnv_b.rearrange("(l x) -> l x", l=8))
 
-        rotation = [("m", 3), ("vx", 2), ("transposed", 2), ("m", 3), ("vx", 2), ("transposed", 2), ("m", 3)]
+        rotation = [("m", 2), ("m", 2), ("transposed", 1)] + [(tag, 1) for tag in free_tags]
         banks_taken = [0]
 
         def next_bank():
@@ -416,7 +457,7 @@ def tile_gnn_s2_pa_t_kernel(
             )
 
         def repeat_x(q):
-            repeated = work.tile([P, 2048], BF16, name="repeated", tag="exps", bufs=EXPS_BUFS, align_bytes=64)
+            repeated = work.tile([P, 2048], BF16, name="repeated", tag="evs", bufs=EV_BUFS, align_bytes=64)
             dst = repeated[:].bitcast(F32).rearrange(
                 "p (jj g b l u) -> p jj g b l u", jj=2, g=2, b=16, l=8, u=2
             )
@@ -440,93 +481,67 @@ def tile_gnn_s2_pa_t_kernel(
                 nc.vector.tensor_scalar(
                     out=params_scaled[:], in0=params_rows[:], scalar1=float(SAMPLES), scalar2=None, op0=ALU.mult
                 )
-                params_ps = psum.tile([P, 96], F32, name="params_ps", tag="stats")
+                params_ps = psum.tile([P, 96], F32, name="params_ps", tag="stats", bufs=1)
                 nc.tensor.matmul(params_ps[:], lhsT=avg_pos[:], rhs=params_scaled[:], start=True, stop=True)
                 params = resident.tile([P, 96], F32, name="params")
                 nc.vector.tensor_copy(out=params[:], in_=params_ps[:])
             if k % 2 == 0:
                 repeat_x(k // 2)
-            new_grouped(k)
-            banks = [next_bank(), next_bank()]
-            for a in range(2):
-                transpose_piece_rows(k, a, banks[a][:])
-                copy_piece_rows(k, a, banks[a][:])
+            prepare_piece(k, next_bank if k < 8 else free_bank)
             quantise_piece(k)
-            if k == 4:
-                for h in range(2):
-                    load_edges(h, 0, 0, 1)
-            if k == 8:
-                for h in range(2):
-                    load_edges(h, 0, 1, 2)
-            load_piece(k + 4)
+            if k == 0:
+                load_edges(0, 0, 1)
+            if k == 3:
+                load_edges(0, 1, 3)
+            if k == 5:
+                transpose_edges(0)
+                copy_transposed(0)
+            if k == 6:
+                quantise_edges(0)
+                transpose_edges(1)
+                copy_transposed(1)
             if k == 7:
-                period(-2)
-        for h in range(2):
-            load_edges(h, 0, 2, 4)
-        for h in range(2):
-            load_edges(h, 1, 0, 4)
+                fill_bank(0, 0)
+                fill_bank(0, 1)
+                transpose_edges(2)
+        load_edges(0, 3, 4)
+        load_edges(1, 0, 4)
+        for n in range(2):
+            product_half(W_A, 0, n, sum_tags["exp"][n], ax[0])
 
-        ux_ps = {}
-        period(-1)
-        for t in range(TILES + 4):
-            period(t)
-            if t in (0, 1):
-                repeat_x(t + 6)
-            if t in (9, 17):
-                for h in range(2):
-                    load_edges(h, (t + 7) // 8, 0, 4)
-            if t == TILES + 1:
-                warm = columns.tile([P, 1], F32, name="warm", tag="warm")
-                nc.scalar.activation(out=warm[:], in_=exps[TILES - 1][:, 0, 0:1], func=ACT.Ln)
-            if t == TILES:
-                free_banks = (("m", 3), ("m", 3), ("m", 3), ("transposed", 2))
-                for h in range(2):
+        with tc.manual_schedule():
+            for t in range(TILES + VX_LAG):
+                period(t)
+                if t in (0, 1):
+                    repeat_x(t + 6)
+                if t == 1:
+                    load_edges(2, 0, 4)
+                if t == 1:
+                    for u in range(VX_BUFS):
+                        load_vx(u)
+                if t % 4 == 1 and 5 <= t <= 21:
+                    load_edges((t + 7) // 4, 0, 4)
+                if t in (5, 6):
+                    product_half(W_A, 1, t - 5, "stats", ax[1])
+                if 7 <= t < 11:
+                    product_half(W_U, (t - 7) // 2, (t - 7) % 2, "stats", ux[(t - 7) // 2])
+                if t == NODES + 3:
                     for n in range(2):
-                        tag, bufs = free_banks[2 * h + n]
-                        ux_ps[(h, n)] = psum.tile([P, BANK], F32, name="ux_ps", tag=tag, bufs=bufs)
-                        mx_group(ux_ps[(h, n)][:], passes(x_codes[:, h, :], x_scales[:, h, :], W_U, halves[n]))
-
-        y, x_new, chunk_stats = {}, {}, {}
-
-        def node_y(h):
-            y[h] = work.tile([P, C], F32, name="y", tag="edge_new", bufs=EDGE_NEW_BUFS)
-            chunk_stats[h] = columns.tile([P, 2, 6], F32, name="chunk_stats", tag="chunk_stats")
+                        nc.scalar.copy(out=sum_exp0[:, halves[n]], in_=sums_ps[("exp", 0, n)][:])
+            for h in (1, 0):
+                inverse[h] = sum_exp0 if h == 0 else new_edge_new()
+            nc.scalar.activation(out=inverse[0][:], in_=sum_exp0[:], func=ACT.Ln)
             for n in range(2):
-                nc.vector.tensor_tensor(
-                    out=sums[h][:, 1, halves[n]], in0=sums[h][:, 1, halves[n]], in1=sums[h][:, 0, halves[n]],
-                    op=ALU.mult,
-                )
-                nc.vector.scalar_tensor_tensor(
-                    out=y[h][:, halves[n]], in0=sums[h][:, 1, halves[n]], scalar=1.0 / NODES,
-                    in1=ux_ps[(h, n)][:], op0=ALU.mult, op1=ALU.add,
-                )
-                nc.vector.bn_stats(out=chunk_stats[h][:, n, :], in_=y[h][:, halves[n]])
-            mean_var = columns.tile([P, 2], F32, name="mean_var", tag="mean_var")
-            nc.vector.bn_aggr(out=mean_var[:], in_=chunk_stats[h][:].rearrange("p a s -> p (a s)"))
-            nc.vector.scalar_tensor_tensor(
-                out=mean_var[:, 1:2], in0=mean_var[:, 0:1], scalar=mean_var[:, 0:1], in1=mean_var[:, 1:2],
-                op0=ALU.mult, op1=ALU.add,
-            )
-            sums_of[NODE_KEY + h] = columns.tile([P, 4], F32, name="node_sums", tag="node_sums")
-            for n in range(2):
-                nc.vector.tensor_scalar(
-                    out=sums_of[NODE_KEY + h][:, 2 * n:2 * n + 2], in0=mean_var[:], scalar1=C / 2.0, scalar2=None,
-                    op0=ALU.mult,
-                )
-
-        def node_out(h):
-            key = NODE_KEY + h
-            variance(key)
-            scale_and_bias(key, params[:, 64 + h:65 + h], params[:, 80 + h:81 + h])
-            x_new[h] = work.tile([P, C], F32, name="x_new", tag="edge_new", bufs=EDGE_NEW_BUFS)
-            for n in range(2):
-                scaled_max(key, x_new[h][:, halves[n]], y[h][:, halves[n]])
-                add_residual(key, x_new[h][:, halves[n]], x_new[h][:, halves[n]], y[h][:, halves[n]])
-                nc.sync.dma_start(out=x_new_view[:, h, halves[n]], in_=x_new[h][:, halves[n]])
-
-        node_y(0)
-        average_over_batches(NODE_KEY)
-        node_y(1)
-        node_out(0)
-        average_over_batches(NODE_KEY + 1)
-        node_out(1)
+                nc.scalar.activation(out=inverse[1][:, halves[n]], in_=sums_ps[("exp", 1, n)][:], func=ACT.Ln)
+            for h in (1, 0):
+                for n in range(2):
+                    nc.scalar.activation(
+                        out=inverse[h][:, halves[n]], in_=inverse[h][:, halves[n]], func=ACT.Exp, scale=-1.0
+                    )
+            for h in (1, 0):
+                node_agg(h)
+            for h in (1, 0):
+                node_y(h)
+                node_statistics(h)
+            for h in (1, 0):
+                node_out(h)

@@ -63,14 +63,12 @@ def tile_gnn_s2_pa_t_kernel(
         nc.vector.tensor_reduce(
             out=same_l[:], in_=ident[:].rearrange("p (b l) -> p l b", l=8), axis=AX.X, op=ALU.add
         )
-        avg_pos = resident.tile([P, P], F32, name="avg_pos")
-        avg_neg = resident.tile([P, P], F32, name="avg_neg")
-        for avg, sign in ((avg_pos, 1.0), (avg_neg, -1.0)):
-            nc.vector.tensor_scalar(
-                out=avg[:].rearrange("p (b l) -> p b l", l=8),
-                in0=same_l[:].unsqueeze(1).to_broadcast([P, 16, 8]),
-                scalar1=sign / SAMPLES, scalar2=None, op0=ALU.mult,
-            )
+        average = resident.tile([P, P], F32, name="average")
+        nc.vector.tensor_scalar(
+            out=average[:].rearrange("p (b l) -> p b l", l=8),
+            in0=same_l[:].unsqueeze(1).to_broadcast([P, 16, 8]),
+            scalar1=1.0 / SAMPLES, scalar2=None, op0=ALU.mult,
+        )
         minus_half = resident.tile([P, 1], F32, name="minus_half")
         nc.vector.memset(minus_half[:], -0.5)
 
@@ -148,27 +146,25 @@ def tile_gnn_s2_pa_t_kernel(
         sums_of, means_ps, moments, scale_bias = {}, {}, {}, {}
 
         def average_over_batches(key):
-            means_ps[key] = psum.tile([P, 4], F32, name="means_ps", tag="stats", bufs=1)
-            for i, avg in enumerate((avg_pos, avg_neg)):
-                for n in range(2):
-                    nc.tensor.matmul(
-                        means_ps[key][:, 2 * i:2 * i + 2], lhsT=avg[:], rhs=sums_of[key][:, 2 * n:2 * n + 2],
-                        start=(n == 0), stop=(n == 1),
-                    )
+            means_ps[key] = psum.tile([P, 2], F32, name="means_ps", tag="stats", bufs=1)
+            for n in range(2):
+                nc.tensor.matmul(
+                    means_ps[key][:], lhsT=average[:], rhs=sums_of[key][:, 2 * n:2 * n + 2],
+                    start=(n == 0), stop=(n == 1),
+                )
 
         def variance(key):
-            moments[key] = columns.tile([P, 8], F32, name="moments", tag="moments")
-            mo = moments[key]
-            nc.scalar.copy(out=mo[:, 0:4], in_=means_ps[key][:])
-            nc.scalar.activation(
-                out=mo[:, 4:5], in_=means_ps[key][:, 0:1], func=ACT.Identity, scale=mo[:, 2:3], bias=mo[:, 1:2]
-            )
+            moments[key] = columns.tile([P, 4], F32, name="moments", tag="moments")
+            mo, mean = moments[key], means_ps[key][:, 0:1]
+            nc.scalar.copy(out=mo[:, 0:2], in_=means_ps[key][:])
+            nc.scalar.activation(out=mo[:, 2:3], in_=mean, func=ACT.Identity, scale=-1.0)
+            nc.scalar.activation(out=mo[:, 3:4], in_=mean, func=ACT.Identity, scale=mo[:, 2:3], bias=mo[:, 1:2])
 
         def scale_and_bias(key, gain, offset):
             scale_bias[key] = columns.tile([P, 2], F32, name="scale_bias", tag="scale_bias")
             rstd = columns.tile([P, 1], F32, name="rstd", tag="rstd")
             sb, mo = scale_bias[key], moments[key]
-            nc.gpsimd.tensor_tensor(out=rstd[:], in0=mo[:, 4:5], in1=minus_half[:], op=ALU.pow)
+            nc.gpsimd.tensor_tensor(out=rstd[:], in0=mo[:, 3:4], in1=minus_half[:], op=ALU.pow)
             nc.gpsimd.tensor_tensor(out=sb[:, 0:1], in0=rstd[:], in1=gain, op=ALU.mult)
             nc.gpsimd.tensor_scalar(
                 out=sb[:, 1:2], in0=sb[:, 0:1], scalar1=mo[:, 0:1], scalar2=offset, op0=ALU.mult, op1=ALU.subtract
@@ -482,7 +478,7 @@ def tile_gnn_s2_pa_t_kernel(
                     out=params_scaled[:], in0=params_rows[:], scalar1=float(SAMPLES), scalar2=None, op0=ALU.mult
                 )
                 params_ps = psum.tile([P, 96], F32, name="params_ps", tag="stats", bufs=1)
-                nc.tensor.matmul(params_ps[:], lhsT=avg_pos[:], rhs=params_scaled[:], start=True, stop=True)
+                nc.tensor.matmul(params_ps[:], lhsT=average[:], rhs=params_scaled[:], start=True, stop=True)
                 params = resident.tile([P, 96], F32, name="params")
                 nc.vector.tensor_copy(out=params[:], in_=params_ps[:])
             if k % 2 == 0:

@@ -71,6 +71,8 @@ def tile_gnn_s2_pa_t_kernel(
         )
         minus_half = resident.tile([P, 1], F32, name="minus_half")
         nc.vector.memset(minus_half[:], -0.5)
+        eps = resident.tile([P, 1], F32, name="eps")
+        nc.vector.memset(eps[:], EPS)
 
         w_codes = [resident.tile([P, 2, C], U32, name="w_codes%d" % w, align_bytes=64) for w in range(5)]
         w_scales = [resident.tile([P, 2, C], U8, name="w_scales%d" % w, align_bytes=64) for w in range(5)]
@@ -83,8 +85,6 @@ def tile_gnn_s2_pa_t_kernel(
         sum_ev0 = resident.tile([P, C], F32, name="sum_ev0")
         ux = [resident.tile([P, C], F32, name="ux%d" % h) for h in range(2)]
         row_sums = resident.tile([P, 8, 4], F32, name="row_sums")
-        nc.vector.memset(row_sums[:], 0.0)
-        nc.vector.memset(row_sums[:, :, 3:4], EPS * SAMPLES / 16)
 
         def transpose_words(bank, rows_as_words):
             for k in range(4):
@@ -145,41 +145,41 @@ def tile_gnn_s2_pa_t_kernel(
 
         sums_of, means_ps, moments, scale_bias = {}, {}, {}, {}
 
+        def add_row_sums(key):
+            rs = sums_of[key]
+            nc.scalar.activation(out=rs[:, 2:3], in_=rs[:, 0:1], func=ACT.Identity, bias=rs[:, 1:2])
+
         def average_over_batches(key):
             means_ps[key] = psum.tile([P, 2], F32, name="means_ps", tag="stats", bufs=1)
-            for n in range(2):
-                nc.tensor.matmul(
-                    means_ps[key][:], lhsT=average[:], rhs=sums_of[key][:, 2 * n:2 * n + 2],
-                    start=(n == 0), stop=(n == 1),
-                )
+            nc.tensor.matmul(means_ps[key][:], lhsT=average[:], rhs=sums_of[key][:, 2:4], start=True, stop=True)
 
         def variance(key):
             moments[key] = columns.tile([P, 4], F32, name="moments", tag="moments")
-            mo, mean = moments[key], means_ps[key][:, 0:1]
-            nc.scalar.copy(out=mo[:, 0:2], in_=means_ps[key][:])
-            nc.scalar.activation(out=mo[:, 2:3], in_=mean, func=ACT.Identity, scale=-1.0)
-            nc.scalar.activation(out=mo[:, 3:4], in_=mean, func=ACT.Identity, scale=mo[:, 2:3], bias=mo[:, 1:2])
+            mo, ps = moments[key], means_ps[key]
+            nc.scalar.activation(out=mo[:, 0:1], in_=ps[:, 0:1], func=ACT.Identity, scale=-1.0)
+            nc.scalar.activation(out=mo[:, 1:2], in_=ps[:, 1:2], func=ACT.Identity, bias=eps[:])
+            nc.scalar.activation(
+                out=mo[:, 2:3], in_=ps[:, 0:1], func=ACT.Identity, scale=mo[:, 0:1], bias=mo[:, 1:2]
+            )
 
         def scale_and_bias(key, gain, offset):
             scale_bias[key] = columns.tile([P, 2], F32, name="scale_bias", tag="scale_bias")
             rstd = columns.tile([P, 1], F32, name="rstd", tag="rstd")
             sb, mo = scale_bias[key], moments[key]
-            nc.gpsimd.tensor_tensor(out=rstd[:], in0=mo[:, 3:4], in1=minus_half[:], op=ALU.pow)
+            nc.gpsimd.tensor_tensor(out=rstd[:], in0=mo[:, 2:3], in1=minus_half[:], op=ALU.pow)
             nc.gpsimd.tensor_tensor(out=sb[:, 0:1], in0=rstd[:], in1=gain, op=ALU.mult)
             nc.gpsimd.tensor_scalar(
-                out=sb[:, 1:2], in0=sb[:, 0:1], scalar1=mo[:, 0:1], scalar2=offset, op0=ALU.mult, op1=ALU.subtract
+                out=sb[:, 1:2], in0=sb[:, 0:1], scalar1=mo[:, 0:1], scalar2=offset, op0=ALU.mult, op1=ALU.add
             )
 
-        def scaled_max(key, dst, src):
+        def apply_norm(key, dst, src):
             nc.vector.tensor_scalar(
                 out=dst, in0=src, scalar1=scale_bias[key][:, 0:1], scalar2=scale_bias[key][:, 1:2],
-                op0=ALU.mult, op1=ALU.max,
+                op0=ALU.mult, op1=ALU.add,
             )
 
-        def add_residual(key, dst, src, residual):
-            nc.vector.scalar_tensor_tensor(
-                out=dst, in0=src, scalar=scale_bias[key][:, 1:2], in1=residual, op0=ALU.subtract, op1=ALU.add
-            )
+        def add_residual(dst, src, residual):
+            nc.vector.scalar_tensor_tensor(out=dst, in0=src, scalar=0.0, in1=residual, op0=ALU.max, op1=ALU.add)
 
         edge_rows, transposed, e_grouped, e_codes, e_scales, m_ps, edge_new, exps, evs, vx = (
             {}, {}, {}, {}, {}, {}, {}, {}, {}, {}
@@ -240,12 +240,13 @@ def tile_gnn_s2_pa_t_kernel(
                     sums_of[t] = row_sums[:, t % 8, :]
                 nc.vector.scalar_tensor_tensor(
                     out=edge_new[t][:, halves[n]], in0=m_ps[(t, n)][:], scalar=1.0, in1=ax[t // NODES][:, halves[n]],
-                    op0=ALU.mult, op1=ALU.add, accum_out=sums_of[t][:, 2 * n:2 * n + 1],
+                    op0=ALU.mult, op1=ALU.add, accum_out=sums_of[t][:, n:n + 1],
                 )
 
         def sum_squares(key, src):
             squares = work.tile([P, C], BF16, name="squares", tag="squares", bufs=1)
-            nc.scalar.activation(out=squares[:], in_=src, func=ACT.Square, accum_out=sums_of[key][:, 1:2])
+            nc.scalar.activation(out=squares[:], in_=src, func=ACT.Square, accum_out=sums_of[key][:, 3:4])
+            add_row_sums(key)
 
         def edge_squares(t):
             if is_tile(t):
@@ -265,11 +266,11 @@ def tile_gnn_s2_pa_t_kernel(
 
         def normalise(t):
             if is_tile(t):
-                scaled_max(t, edge_new[t][:], edge_new[t][:])
+                apply_norm(t, edge_new[t][:], edge_new[t][:])
 
         def finish_edge_new(t):
             if is_tile(t):
-                add_residual(t, edge_new[t][:], edge_new[t][:], edge_of(t))
+                add_residual(edge_new[t][:], edge_new[t][:], edge_of(t))
                 nc.sync.dma_start(out=edge_new_view[:, t // NODES, t % NODES, :], in_=edge_new[t][:])
 
         def tanh_half(t):
@@ -338,7 +339,7 @@ def tile_gnn_s2_pa_t_kernel(
             for n in range(2):
                 nc.vector.scalar_tensor_tensor(
                     out=y[h][:, halves[n]], in0=back[(h, n)][:], scalar=1.0 / NODES, in1=ux[h][:, halves[n]],
-                    op0=ALU.mult, op1=ALU.add, accum_out=sums_of[NODE_KEY + h][:, 2 * n:2 * n + 1],
+                    op0=ALU.mult, op1=ALU.add, accum_out=sums_of[NODE_KEY + h][:, n:n + 1],
                 )
             sum_squares(NODE_KEY + h, y[h][:])
 
@@ -351,8 +352,8 @@ def tile_gnn_s2_pa_t_kernel(
         def node_out(h):
             key = NODE_KEY + h
             for n in range(2):
-                scaled_max(key, ux[h][:, halves[n]], y[h][:, halves[n]])
-                add_residual(key, ux[h][:, halves[n]], ux[h][:, halves[n]], y[h][:, halves[n]])
+                apply_norm(key, ux[h][:, halves[n]], y[h][:, halves[n]])
+                add_residual(ux[h][:, halves[n]], ux[h][:, halves[n]], y[h][:, halves[n]])
                 nc.sync.dma_start(out=x_new_view[:, h, halves[n]], in_=ux[h][:, halves[n]])
 
         def product_half(w, h, n, tag, dst):

@@ -26,7 +26,9 @@ W_E, W_B, W_A, W_V, W_U = 0, 1, 2, 3, 4
 PIECE = 256
 NODE_KEY = 100
 
+RECIPROCAL_PARTS = 16
 W_ROWS_BUFS = 4
+EARLY_PIECES = 11
 W_GROUPED_BUFS = 4
 E_GROUPED_BUFS = 2
 E_CODES_BUFS = 4
@@ -36,6 +38,7 @@ EXP_BUFS = 3
 EV_BUFS = 3
 VX_BUFS = 4
 VX_LAG = 4
+FIRST_RECIPROCAL = 20
 
 
 def tile_gnn_s2_pa_t_kernel(
@@ -48,6 +51,7 @@ def tile_gnn_s2_pa_t_kernel(
     x_view = x.rearrange("b (l h) c -> (b l) h c", h=2)
     x_new_view = out_0.rearrange("b (l h) c -> (b l) h c", h=2)
     halves = [slice(0, BANK), slice(BANK, C)]
+    whole = [slice(0, C)]
 
     with ExitStack() as ctx:
         resident = ctx.enter_context(tc.tile_pool(name="resident", bufs=1))
@@ -116,13 +120,24 @@ def tile_gnn_s2_pa_t_kernel(
 
         def load_piece(k):
             w, part = k // 4, k % 4
-            w_rows[k] = staging.tile([P, 2, C], BF16, name="w_rows", tag="w_rows", bufs=W_ROWS_BUFS)
+            if 4 <= k < 8:
+                w_rows[k] = work.tile([P, 2, C], BF16, name="w_rows", tag="vx", bufs=VX_BUFS)
+            elif 8 <= k < EARLY_PIECES:
+                w_rows[k] = work.tile([P, 2, C], BF16, name="w_rows", tag="exps", bufs=EXP_BUFS)
+            else:
+                w_rows[k] = staging.tile([P, 2, C], BF16, name="w_rows", tag="w_rows", bufs=W_ROWS_BUFS)
             nc.sync.dma_start(
                 out=w_rows[k][:],
                 in_=weights[w][part * PIECE:(part + 1) * PIECE, :].rearrange("(a p) k -> p a k", p=P),
             )
 
-        def prepare_piece(k, next_bank):
+        def copy_on(vector, out, in_):
+            if vector:
+                nc.vector.tensor_copy(out=out, in_=in_)
+            else:
+                nc.scalar.copy(out=out, in_=in_)
+
+        def prepare_piece(k, next_bank, vector_copies):
             w_grouped[k] = staging.tile(
                 [P, 2048], BF16, name="w_grouped", tag="w_grouped", bufs=W_GROUPED_BUFS, align_bytes=64
             )
@@ -130,9 +145,10 @@ def tile_gnn_s2_pa_t_kernel(
             for a in range(2):
                 bank = next_bank()
                 transpose_words(bank[:], w_rows[k][:].bitcast(F32)[:, a, :])
-                nc.scalar.copy(out=dst[:, :, a * P:(a + 1) * P, :], in_=grouped_read(bank[:]))
-            if k + 4 < 20:
-                load_piece(k + 4)
+                copy_on(vector_copies[a], dst[:, :, a * P:(a + 1) * P, :], grouped_read(bank[:]))
+            following = k + EARLY_PIECES if k < 4 else k + 4
+            if (k < 4 or k >= EARLY_PIECES) and following < 20:
+                load_piece(following)
 
         def quantise_piece(k):
             w, part = k // 4, k % 4
@@ -145,13 +161,12 @@ def tile_gnn_s2_pa_t_kernel(
 
         sums_of, means_ps, moments, scale_bias = {}, {}, {}, {}
 
-        def add_row_sums(key):
-            rs = sums_of[key]
-            nc.scalar.activation(out=rs[:, 2:3], in_=rs[:, 0:1], func=ACT.Identity, bias=rs[:, 1:2])
+        def add_columns(dst, one, other):
+            nc.scalar.activation(out=dst, in_=one, func=ACT.Identity, bias=other)
 
         def average_over_batches(key):
             means_ps[key] = psum.tile([P, 2], F32, name="means_ps", tag="stats", bufs=1)
-            nc.tensor.matmul(means_ps[key][:], lhsT=average[:], rhs=sums_of[key][:, 2:4], start=True, stop=True)
+            nc.tensor.matmul(means_ps[key][:], lhsT=average[:], rhs=sums_of[key], start=True, stop=True)
 
         def variance(key):
             moments[key] = columns.tile([P, 4], F32, name="moments", tag="moments")
@@ -237,20 +252,21 @@ def tile_gnn_s2_pa_t_kernel(
             if is_tile(t):
                 if n == 0:
                     edge_new[t] = work.tile([P, C], F32, name="edge_new", tag="edge_new", bufs=EDGE_NEW_BUFS)
-                    sums_of[t] = row_sums[:, t % 8, :]
                 nc.vector.scalar_tensor_tensor(
                     out=edge_new[t][:, halves[n]], in0=m_ps[(t, n)][:], scalar=1.0, in1=ax[t // NODES][:, halves[n]],
-                    op0=ALU.mult, op1=ALU.add, accum_out=sums_of[t][:, n:n + 1],
+                    op0=ALU.mult, op1=ALU.add, accum_out=row_sums[:, t % 8, n:n + 1],
                 )
 
-        def sum_squares(key, src):
+        def sum_squares(src, cols, dst):
             squares = work.tile([P, C], BF16, name="squares", tag="squares", bufs=1)
-            nc.scalar.activation(out=squares[:], in_=src, func=ACT.Square, accum_out=sums_of[key][:, 3:4])
-            add_row_sums(key)
+            nc.scalar.activation(out=squares[:, cols], in_=src, func=ACT.Square, accum_out=dst)
 
         def edge_squares(t):
             if is_tile(t):
-                sum_squares(t, edge_new[t][:])
+                rs = row_sums[:, t % 8, :]
+                sum_squares(edge_new[t][:], slice(0, C), rs[:, 3:4])
+                add_columns(rs[:, 2:3], rs[:, 0:1], rs[:, 1:2])
+                sums_of[t] = rs[:, 2:4]
 
         def edge_average(t):
             if is_tile(t):
@@ -268,19 +284,22 @@ def tile_gnn_s2_pa_t_kernel(
             if is_tile(t):
                 apply_norm(t, edge_new[t][:], edge_new[t][:])
 
-        def finish_edge_new(t):
+        def finish_edge_new(t, parts=whole):
             if is_tile(t):
-                add_residual(edge_new[t][:], edge_new[t][:], edge_of(t))
+                for cols in parts:
+                    add_residual(edge_new[t][:, cols], edge_new[t][:, cols], edge_of(t)[:, cols])
                 nc.sync.dma_start(out=edge_new_view[:, t // NODES, t % NODES, :], in_=edge_new[t][:])
 
-        def tanh_half(t):
+        def tanh_half(t, parts=whole):
             if is_tile(t):
                 exps[t] = work.tile([P, C], F32, name="exps", tag="exps", bufs=EXP_BUFS)
-                nc.scalar.activation(out=exps[t][:], in_=edge_new[t][:], func=ACT.Tanh, scale=0.5)
+                for cols in parts:
+                    nc.scalar.activation(out=exps[t][:, cols], in_=edge_new[t][:, cols], func=ACT.Tanh, scale=0.5)
 
-        def exp_half(t):
+        def exp_half(t, parts=whole):
             if is_tile(t):
-                nc.scalar.activation(out=exps[t][:], in_=exps[t][:], func=ACT.Exp, scale=0.5)
+                for cols in parts:
+                    nc.scalar.activation(out=exps[t][:, cols], in_=exps[t][:, cols], func=ACT.Exp, scale=0.5)
 
         def new_ev():
             ev = work.tile([P, C], F32, name="evs", tag="evs", bufs=EV_BUFS, align_bytes=64)
@@ -291,10 +310,11 @@ def tile_gnn_s2_pa_t_kernel(
                 vx[t] = work.tile([P, C], F32, name="vx", tag="vx", bufs=VX_BUFS)
                 nc.sync.dma_start(out=vx[t][:], in_=out_0[:, t % NODES, :].unsqueeze(1).to_broadcast([16, 8, C]))
 
-        def times_vx(t):
+        def times_vx(t, parts=whole):
             if is_tile(t):
                 evs[t] = new_ev()
-                nc.vector.tensor_tensor(out=evs[t][:], in0=exps[t][:], in1=vx[t][:], op=ALU.mult)
+                for cols in parts:
+                    nc.vector.tensor_tensor(out=evs[t][:, cols], in0=exps[t][:, cols], in1=vx[t][:, cols], op=ALU.mult)
 
         def add_to_sums(what, t, addend):
             h, j = t // NODES, t % NODES
@@ -316,11 +336,16 @@ def tile_gnn_s2_pa_t_kernel(
             if is_tile(t):
                 add_to_sums("ev", t, evs[t])
 
-        inverse, back, y = {}, {}, {}
+        inverse, back, y, node_sums = {}, {}, {}, {}
 
         def new_edge_new():
             tile = work.tile([P, C], F32, name="edge_new", tag="edge_new", bufs=EDGE_NEW_BUFS)
             return tile
+
+        def invert_sum_exp0(part):
+            width = C // RECIPROCAL_PARTS
+            cols = slice(part * width, (part + 1) * width)
+            nc.vector.reciprocal(out=sum_exp0[:, cols], in_=sum_exp0[:, cols])
 
         def node_agg(h):
             agg = new_ev()
@@ -329,37 +354,43 @@ def tile_gnn_s2_pa_t_kernel(
                     out=agg[:, halves[n]], in0=sums_ps[("ev", 1, n)][:] if h == 1 else sum_ev0[:, halves[n]],
                     in1=inverse[h][:, halves[n]], op=ALU.mult,
                 )
-                tag, bufs = ("m", 2) if h == 1 else (sum_tags["exp"][n], 1)
+                tag, bufs = ("m", 2) if h == 0 else (sum_tags["exp"][n], 1)
                 back[(h, n)] = psum.tile([P, BANK], F32, name="back", tag=tag, bufs=bufs)
                 transpose_words(back[(h, n)], agg[:, halves[n]])
 
         def node_y(h):
             y[h] = new_edge_new()
-            sums_of[NODE_KEY + h] = row_sums[:, h, :]
+            node_sums[h] = columns.tile([P, 8], F32, name="node_sums", tag="node_sums", bufs=2)
             for n in range(2):
                 nc.vector.scalar_tensor_tensor(
                     out=y[h][:, halves[n]], in0=back[(h, n)][:], scalar=1.0 / NODES, in1=ux[h][:, halves[n]],
-                    op0=ALU.mult, op1=ALU.add, accum_out=sums_of[NODE_KEY + h][:, n:n + 1],
+                    op0=ALU.mult, op1=ALU.add, accum_out=node_sums[h][:, n:n + 1],
                 )
-            sum_squares(NODE_KEY + h, y[h][:])
 
-        def node_statistics(h):
-            key = NODE_KEY + h
-            average_over_batches(key)
-            variance(key)
-            scale_and_bias(key, params[:, 64 + h:65 + h], params[:, 80 + h:81 + h])
+        def node_squares(h, n):
+            ns = node_sums[h]
+            sum_squares(y[h][:, halves[n]], halves[n], ns[:, 2 + n:3 + n])
+            if n == 1:
+                add_columns(ns[:, 4:5], ns[:, 0:1], ns[:, 1:2])
+                add_columns(ns[:, 5:6], ns[:, 2:3], ns[:, 3:4])
+                sums_of[NODE_KEY + h] = ns[:, 4:6]
+                average_over_batches(NODE_KEY + h)
+
+        def node_scale_and_bias(h):
+            variance(NODE_KEY + h)
+            scale_and_bias(NODE_KEY + h, params[:, 64 + h:65 + h], params[:, 80 + h:81 + h])
 
         def node_out(h):
-            key = NODE_KEY + h
             for n in range(2):
-                apply_norm(key, ux[h][:, halves[n]], y[h][:, halves[n]])
+                apply_norm(NODE_KEY + h, ux[h][:, halves[n]], y[h][:, halves[n]])
+            for n in range(2):
                 add_residual(ux[h][:, halves[n]], ux[h][:, halves[n]], y[h][:, halves[n]])
                 nc.sync.dma_start(out=x_new_view[:, h, halves[n]], in_=ux[h][:, halves[n]])
 
-        def product_half(w, h, n, tag, dst):
+        def product_half(w, h, n, tag, dst, vector=False):
             bank = psum.tile([P, BANK], F32, name="product", tag=tag, bufs=1)
             mx_group(bank[:], passes(x_codes[:, h, :], x_scales[:, h, :], w, halves[n]))
-            nc.scalar.copy(out=dst[:, halves[n]], in_=bank[:])
+            copy_on(vector, dst[:, halves[n]], bank[:])
 
         def park_vx():
             for h in range(2):
@@ -377,11 +408,11 @@ def tile_gnn_s2_pa_t_kernel(
             bank = psum.tile([P, BANK], F32, name="free_bank", tag=tag, bufs=1)
             return bank
 
-        late_pieces = {0: (12, 13, 14, 15), 1: (16, 17), 2: (18, 19)}
+        late_pieces = {0: (12, 13), 1: (14, 15), 2: (16, 17), 3: (18, 19)}
 
         def late_prepare(t):
             for k in late_pieces.get(t, ()):
-                prepare_piece(k, free_bank)
+                prepare_piece(k, free_bank, (False, True))
 
         def late_quantise(t):
             for k in late_pieces.get(t - 1, ()):
@@ -394,6 +425,7 @@ def tile_gnn_s2_pa_t_kernel(
             late_quantise(t)
             if t > 0:
                 fill_bank(t, 0)
+            finish_edge_new(t - 2)
             times_vx(t - VX_LAG)
             if is_tile(t - VX_LAG):
                 load_vx(t - VX_LAG + VX_BUFS)
@@ -409,19 +441,22 @@ def tile_gnn_s2_pa_t_kernel(
             copy_transposed(t + 2)
             if t > 0:
                 fill_bank(t, 1)
-            finish_edge_new(t - 2)
             exp_half(t - 3)
             sum_ev(t - VX_LAG)
             transpose_edges(t + 3)
-            if t == 1:
+            empty_bank(t, 1)
+            if t == 2:
                 park_vx()
             late_prepare(t)
-            empty_bank(t, 1)
 
         x_rows = work.tile([P, 2, C], BF16, name="x_rows", tag="edge_new", bufs=EDGE_NEW_BUFS)
         nc.sync.dma_start(out=x_rows[:], in_=x_view)
-        for k in range(4):
+        for k in range(EARLY_PIECES):
             load_piece(k)
+            if k == 3:
+                load_edges(0, 0, 1)
+            if k == 7:
+                load_edges(0, 1, 3)
         params_rows = resident.tile([P, 96], BF16, name="params_rows")
         nc.vector.memset(params_rows[:], 0.0)
         nc.sync.dma_start(out=params_rows[0:8, 0:32], in_=bne_w.rearrange("(l x) -> l x", l=8))
@@ -429,7 +464,7 @@ def tile_gnn_s2_pa_t_kernel(
         nc.sync.dma_start(out=params_rows[0:8, 64:66], in_=bnv_w.rearrange("(l x) -> l x", l=8))
         nc.sync.dma_start(out=params_rows[0:8, 80:82], in_=bnv_b.rearrange("(l x) -> l x", l=8))
 
-        rotation = [("m", 2), ("m", 2), ("transposed", 1)] + [(tag, 1) for tag in free_tags]
+        rotation = [("m", 2), ("m", 2)] + [(tag, 1) for tag in free_tags]
         banks_taken = [0]
 
         def next_bank():
@@ -443,9 +478,8 @@ def tile_gnn_s2_pa_t_kernel(
             x_bank = next_bank()
             transpose_words(x_bank[:], x_rows[:].bitcast(F32)[:, h, :])
             grouped = resident.tile([P, C], BF16, name="x_grouped%d" % h, align_bytes=64)
-            nc.scalar.copy(
-                out=grouped[:].bitcast(F32).rearrange("p (g r u) -> p g r u", g=2, u=2),
-                in_=grouped_read(x_bank[:]),
+            copy_on(
+                h == 1, grouped[:].bitcast(F32).rearrange("p (g r u) -> p g r u", g=2, u=2), grouped_read(x_bank[:])
             )
             x_grouped.append(grouped)
         for h in range(2):
@@ -472,8 +506,9 @@ def tile_gnn_s2_pa_t_kernel(
                 in_=repeated[:],
             )
 
+        repeat_x(0)
         for k in range(12):
-            if k == 6:
+            if k == 9:
                 params_scaled = resident.tile([P, 96], F32, name="params_scaled")
                 nc.vector.tensor_scalar(
                     out=params_scaled[:], in0=params_rows[:], scalar1=float(SAMPLES), scalar2=None, op0=ALU.mult
@@ -482,14 +517,10 @@ def tile_gnn_s2_pa_t_kernel(
                 nc.tensor.matmul(params_ps[:], lhsT=average[:], rhs=params_scaled[:], start=True, stop=True)
                 params = resident.tile([P, 96], F32, name="params")
                 nc.vector.tensor_copy(out=params[:], in_=params_ps[:])
-            if k % 2 == 0:
-                repeat_x(k // 2)
-            prepare_piece(k, next_bank if k < 8 else free_bank)
+            if k in (2, 5):
+                repeat_x((k + 1) // 3)
+            prepare_piece(k, next_bank if k < 8 else free_bank, (False, k % 2 == 1))
             quantise_piece(k)
-            if k == 0:
-                load_edges(0, 0, 1)
-            if k == 3:
-                load_edges(0, 1, 3)
             if k == 5:
                 transpose_edges(0)
                 copy_transposed(0)
@@ -498,22 +529,22 @@ def tile_gnn_s2_pa_t_kernel(
                 transpose_edges(1)
                 copy_transposed(1)
             if k == 7:
-                fill_bank(0, 0)
-                fill_bank(0, 1)
                 transpose_edges(2)
+            if k in (9, 11):
+                fill_bank(0, (k - 9) // 2)
         load_edges(0, 3, 4)
         load_edges(1, 0, 4)
         for n in range(2):
-            product_half(W_A, 0, n, sum_tags["exp"][n], ax[0])
+            product_half(W_A, 0, n, sum_tags["exp"][n], ax[0], vector=(n == 1))
 
         with tc.manual_schedule():
-            for t in range(TILES + VX_LAG):
+            for t in range(TILES):
                 period(t)
-                if t in (0, 1):
-                    repeat_x(t + 6)
+                if t in (1, 3, 5, 7, 9):
+                    repeat_x((t + 5) // 2)
                 if t == 1:
                     load_edges(2, 0, 4)
-                if t == 1:
+                if t == 2:
                     for u in range(VX_BUFS):
                         load_vx(u)
                 if t % 4 == 1 and 5 <= t <= 21:
@@ -525,20 +556,60 @@ def tile_gnn_s2_pa_t_kernel(
                 if t == NODES + 3:
                     for n in range(2):
                         nc.scalar.copy(out=sum_exp0[:, halves[n]], in_=sums_ps[("exp", 0, n)][:])
-            for h in (1, 0):
-                inverse[h] = sum_exp0 if h == 0 else new_edge_new()
-            nc.scalar.activation(out=inverse[0][:], in_=sum_exp0[:], func=ACT.Ln)
+                if t >= FIRST_RECIPROCAL:
+                    invert_sum_exp0(t - FIRST_RECIPROCAL)
+
+            part = TILES - FIRST_RECIPROCAL
+            last = TILES - 1
+            edge_squares(last)
+            sum_exp(last - 3)
+            edge_average(last)
+            edge_variance(last)
+            edge_scale_and_bias(last)
+            normalise(last - 1)
+            times_vx(last - 3)
+            sum_ev(last - 3)
+            finish_edge_new(last - 1)
+            invert_sum_exp0(part)
+            normalise(last)
+            invert_sum_exp0(part + 1)
+            tanh_half(last - 2)
+            exp_half(last - 2)
+            tanh_half(last - 1)
+            exp_half(last - 1)
+            finish_edge_new(last, halves)
+            times_vx(last - 2)
+            sum_exp(last - 2)
+            sum_ev(last - 2)
+            tanh_half(last, halves)
+            exp_half(last, halves)
+            warm = columns.tile([P, 1], F32, name="warm", tag="warm", bufs=1)
+            nc.scalar.activation(out=warm[:], in_=exps[last][:, C - 1:C], func=ACT.Ln)
+            times_vx(last - 1)
+            sum_exp(last - 1)
+            sum_ev(last - 1)
+            for p in range(part + 2, RECIPROCAL_PARTS):
+                invert_sum_exp0(p)
+            sum_exp(last)
+            times_vx(last, halves)
+            sum_ev(last)
+
+            inverse[0] = sum_exp0
+            inverse[1] = new_edge_new()
             for n in range(2):
                 nc.scalar.activation(out=inverse[1][:, halves[n]], in_=sums_ps[("exp", 1, n)][:], func=ACT.Ln)
-            for h in (1, 0):
-                for n in range(2):
-                    nc.scalar.activation(
-                        out=inverse[h][:, halves[n]], in_=inverse[h][:, halves[n]], func=ACT.Exp, scale=-1.0
-                    )
-            for h in (1, 0):
+            for n in range(2):
+                nc.scalar.activation(
+                    out=inverse[1][:, halves[n]], in_=inverse[1][:, halves[n]], func=ACT.Exp, scale=-1.0
+                )
+            for h in range(2):
                 node_agg(h)
-            for h in (1, 0):
                 node_y(h)
-                node_statistics(h)
-            for h in (1, 0):
+            node_squares(0, 0)
+            node_squares(0, 1)
+            node_squares(1, 0)
+            node_scale_and_bias(0)
+            node_squares(1, 1)
+            node_scale_and_bias(1)
+            for h in range(2):
                 node_out(h)

@@ -6,6 +6,7 @@ from concourse.masks import make_identity
 F32 = mybir.dt.float32
 BF16 = mybir.dt.bfloat16
 U32 = mybir.dt.uint32
+I32 = mybir.dt.int32
 U8 = mybir.dt.uint8
 FP8X4 = mybir.dt.float8_e4m3fn_x4
 ACT = mybir.ActivationFunctionType
@@ -26,9 +27,9 @@ W_E, W_B, W_A, W_V, W_U = 0, 1, 2, 3, 4
 PIECE = 256
 NODE_KEY = 100
 
-RECIPROCAL_PARTS = 16
 W_ROWS_BUFS = 4
 EARLY_PIECES = 11
+LOAD_BEHIND = {0: 11, 1: 12, 2: 13, 3: 14, 4: 15, 5: 16, 6: 17, 7: 18, 8: 19}
 W_GROUPED_BUFS = 4
 E_GROUPED_BUFS = 2
 E_CODES_BUFS = 4
@@ -37,8 +38,9 @@ EDGE_NEW_BUFS = 6
 EXP_BUFS = 3
 EV_BUFS = 3
 VX_BUFS = 4
+CATCH_UP = 30
+INVERTED = 256
 VX_LAG = 4
-FIRST_RECIPROCAL = 20
 
 
 def tile_gnn_s2_pa_t_kernel(
@@ -60,6 +62,7 @@ def tile_gnn_s2_pa_t_kernel(
         columns = ctx.enter_context(tc.tile_pool(name="columns", bufs=8))
         psum = ctx.enter_context(tc.psum_pool(name="psum", bufs=1))
         sum_tags = {"exp": ("sum_exp0", "sum_exp1"), "ev": ("sum_ev0", "sum_ev1")}
+        ctx.enter_context(tc.manual_schedule())
 
         ident = resident.tile([P, P], F32, name="ident")
         make_identity(nc, ident[:])
@@ -82,13 +85,15 @@ def tile_gnn_s2_pa_t_kernel(
         w_scales = [resident.tile([P, 2, C], U8, name="w_scales%d" % w, align_bytes=64) for w in range(5)]
         x_codes = resident.tile([P, 2, WORDS], U32, name="x_codes", align_bytes=64)
         x_scales = resident.tile([P, 2, WORDS], U8, name="x_scales", align_bytes=64)
+        x_scales4 = resident.tile([P, 8 * WORDS], U8, name="x_scales4", align_bytes=64)
+        nc.vector.memset(x_scales[:].rearrange("p h w -> p (h w)").bitcast(I32), 0)
         xj_codes = resident.tile([P, NODES, WORDS], U32, name="xj_codes", align_bytes=64)
         xj_scales = resident.tile([P, NODES, WORDS], U8, name="xj_scales", align_bytes=64)
         ax = [resident.tile([P, C], F32, name="ax%d" % h) for h in range(2)]
         sum_exp0 = resident.tile([P, C], F32, name="sum_exp0")
         sum_ev0 = resident.tile([P, C], F32, name="sum_ev0")
         ux = [resident.tile([P, C], F32, name="ux%d" % h) for h in range(2)]
-        row_sums = resident.tile([P, 8, 4], F32, name="row_sums")
+        row_sums = resident.tile([P, 8, 8], F32, name="row_sums")
 
         def transpose_words(bank, rows_as_words):
             for k in range(4):
@@ -120,9 +125,9 @@ def tile_gnn_s2_pa_t_kernel(
 
         def load_piece(k):
             w, part = k // 4, k % 4
-            if 4 <= k < 8:
+            if 4 <= k < 8 or 15 <= k < 19:
                 w_rows[k] = work.tile([P, 2, C], BF16, name="w_rows", tag="vx", bufs=VX_BUFS)
-            elif 8 <= k < EARLY_PIECES:
+            elif 8 <= k < EARLY_PIECES or k == 19:
                 w_rows[k] = work.tile([P, 2, C], BF16, name="w_rows", tag="exps", bufs=EXP_BUFS)
             else:
                 w_rows[k] = staging.tile([P, 2, C], BF16, name="w_rows", tag="w_rows", bufs=W_ROWS_BUFS)
@@ -137,18 +142,28 @@ def tile_gnn_s2_pa_t_kernel(
             else:
                 nc.scalar.copy(out=out, in_=in_)
 
-        def prepare_piece(k, next_bank, vector_copies):
-            w_grouped[k] = staging.tile(
-                [P, 2048], BF16, name="w_grouped", tag="w_grouped", bufs=W_GROUPED_BUFS, align_bytes=64
-            )
-            dst = w_grouped[k][:].bitcast(F32).rearrange("p (g c u) -> p g c u", g=2, u=2)
+        piece_banks = {}
+
+        def transpose_piece(k, next_bank):
+            piece_banks[k] = []
             for a in range(2):
                 bank = next_bank()
                 transpose_words(bank[:], w_rows[k][:].bitcast(F32)[:, a, :])
-                copy_on(vector_copies[a], dst[:, :, a * P:(a + 1) * P, :], grouped_read(bank[:]))
-            following = k + EARLY_PIECES if k < 4 else k + 4
-            if (k < 4 or k >= EARLY_PIECES) and following < 20:
-                load_piece(following)
+                piece_banks[k].append(bank)
+            if k in LOAD_BEHIND:
+                load_piece(LOAD_BEHIND[k])
+
+        def copy_half(k, a, vector):
+            if k not in w_grouped:
+                w_grouped[k] = staging.tile(
+                    [P, 2048], BF16, name="w_grouped", tag="w_grouped", bufs=W_GROUPED_BUFS, align_bytes=64
+                )
+            dst = w_grouped[k][:].bitcast(F32).rearrange("p (g c u) -> p g c u", g=2, u=2)
+            copy_on(vector, dst[:, :, a * P:(a + 1) * P, :], grouped_read(piece_banks[k][a][:]))
+
+        def copy_piece(k, vector):
+            copy_half(k, 0, False)
+            copy_half(k, 1, vector)
 
         def quantise_piece(k):
             w, part = k // 4, k % 4
@@ -215,7 +230,10 @@ def tile_gnn_s2_pa_t_kernel(
 
         def transpose_edges(t):
             if is_tile(t):
-                transposed[t] = psum.tile([P, BANK], F32, name="transposed", tag="transposed", bufs=1)
+                if t < 4:
+                    transposed[t] = (next_bank if t == 0 else free_bank)()[:]
+                else:
+                    transposed[t] = psum.tile([P, BANK], F32, name="transposed", tag="transposed", bufs=1)
                 transpose_words(transposed[t], edge_of(t).bitcast(F32))
 
         def copy_transposed(t):
@@ -261,12 +279,17 @@ def tile_gnn_s2_pa_t_kernel(
             squares = work.tile([P, C], BF16, name="squares", tag="squares", bufs=1)
             nc.scalar.activation(out=squares[:, cols], in_=src, func=ACT.Square, accum_out=dst)
 
-        def edge_squares(t):
+        def complete_row_sums(key, src, rs, parts):
+            for n, cols in enumerate(parts):
+                sum_squares(src[:, cols], cols, rs[:, 2 + n:3 + n] if len(parts) == 2 else rs[:, 5:6])
+            add_columns(rs[:, 4:5], rs[:, 0:1], rs[:, 1:2])
+            if len(parts) == 2:
+                add_columns(rs[:, 5:6], rs[:, 2:3], rs[:, 3:4])
+            sums_of[key] = rs[:, 4:6]
+
+        def edge_squares(t, parts=whole):
             if is_tile(t):
-                rs = row_sums[:, t % 8, :]
-                sum_squares(edge_new[t][:], slice(0, C), rs[:, 3:4])
-                add_columns(rs[:, 2:3], rs[:, 0:1], rs[:, 1:2])
-                sums_of[t] = rs[:, 2:4]
+                complete_row_sums(t, edge_new[t], row_sums[:, t % 8, :], parts)
 
         def edge_average(t):
             if is_tile(t):
@@ -336,49 +359,49 @@ def tile_gnn_s2_pa_t_kernel(
             if is_tile(t):
                 add_to_sums("ev", t, evs[t])
 
-        inverse, back, y, node_sums = {}, {}, {}, {}
+        inverse, agg, back, y, node_sums = {}, {}, {}, {}, {}
 
         def new_edge_new():
             tile = work.tile([P, C], F32, name="edge_new", tag="edge_new", bufs=EDGE_NEW_BUFS)
             return tile
 
-        def invert_sum_exp0(part):
-            width = C // RECIPROCAL_PARTS
-            cols = slice(part * width, (part + 1) * width)
-            nc.vector.reciprocal(out=sum_exp0[:, cols], in_=sum_exp0[:, cols])
+        def node_agg(h, n):
+            if n == 0:
+                agg[h] = new_ev()
+            nc.vector.tensor_tensor(
+                out=agg[h][:, halves[n]], in0=sums_ps[("ev", 1, n)][:] if h == 1 else sum_ev0[:, halves[n]],
+                in1=inverse[h][:, halves[n]], op=ALU.mult,
+            )
+            tag, bufs = ("m", 2) if h == 0 else (sum_tags["exp"][n], 1)
+            back[(h, n)] = psum.tile([P, BANK], F32, name="back", tag=tag, bufs=bufs)
+            transpose_words(back[(h, n)], agg[h][:, halves[n]])
 
-        def node_agg(h):
-            agg = new_ev()
-            for n in range(2):
-                nc.vector.tensor_tensor(
-                    out=agg[:, halves[n]], in0=sums_ps[("ev", 1, n)][:] if h == 1 else sum_ev0[:, halves[n]],
-                    in1=inverse[h][:, halves[n]], op=ALU.mult,
-                )
-                tag, bufs = ("m", 2) if h == 0 else (sum_tags["exp"][n], 1)
-                back[(h, n)] = psum.tile([P, BANK], F32, name="back", tag=tag, bufs=bufs)
-                transpose_words(back[(h, n)], agg[:, halves[n]])
+        def node_y(h, n):
+            if n == 0:
+                y[h] = new_edge_new()
+                node_sums[h] = columns.tile([P, 8], F32, name="node_sums", tag="node_sums", bufs=2)
+            nc.vector.scalar_tensor_tensor(
+                out=y[h][:, halves[n]], in0=back[(h, n)][:], scalar=1.0 / NODES, in1=ux[h][:, halves[n]],
+                op0=ALU.mult, op1=ALU.add, accum_out=node_sums[h][:, n:n + 1],
+            )
 
-        def node_y(h):
-            y[h] = new_edge_new()
-            node_sums[h] = columns.tile([P, 8], F32, name="node_sums", tag="node_sums", bufs=2)
-            for n in range(2):
-                nc.vector.scalar_tensor_tensor(
-                    out=y[h][:, halves[n]], in0=back[(h, n)][:], scalar=1.0 / NODES, in1=ux[h][:, halves[n]],
-                    op0=ALU.mult, op1=ALU.add, accum_out=node_sums[h][:, n:n + 1],
-                )
-
-        def node_squares(h, n):
-            ns = node_sums[h]
-            sum_squares(y[h][:, halves[n]], halves[n], ns[:, 2 + n:3 + n])
-            if n == 1:
-                add_columns(ns[:, 4:5], ns[:, 0:1], ns[:, 1:2])
-                add_columns(ns[:, 5:6], ns[:, 2:3], ns[:, 3:4])
-                sums_of[NODE_KEY + h] = ns[:, 4:6]
-                average_over_batches(NODE_KEY + h)
+        def node_row_sums(h):
+            complete_row_sums(NODE_KEY + h, y[h], node_sums[h], halves)
 
         def node_scale_and_bias(h):
-            variance(NODE_KEY + h)
-            scale_and_bias(NODE_KEY + h, params[:, 64 + h:65 + h], params[:, 80 + h:81 + h])
+            key = NODE_KEY + h
+            average_over_batches(key)
+            scale_bias[key] = columns.tile([P, 2], F32, name="scale_bias", tag="scale_bias")
+            mo = columns.tile([P, 4], F32, name="moments", tag="moments")
+            sb, ps = scale_bias[key], means_ps[key]
+            nc.scalar.activation(out=mo[:, 0:1], in_=ps[:, 0:1], func=ACT.Identity, scale=-1.0)
+            nc.scalar.activation(out=mo[:, 1:2], in_=ps[:, 1:2], func=ACT.Identity, bias=eps[:])
+            nc.scalar.activation(out=mo[:, 2:3], in_=ps[:, 0:1], func=ACT.Ln, scale=mo[:, 0:1], bias=mo[:, 1:2])
+            nc.scalar.activation(out=mo[:, 3:4], in_=mo[:, 2:3], func=ACT.Exp, scale=-0.5)
+            nc.scalar.activation(out=sb[:, 0:1], in_=mo[:, 3:4], func=ACT.Identity, scale=params[:, 64 + h:65 + h])
+            nc.scalar.activation(
+                out=sb[:, 1:2], in_=sb[:, 0:1], func=ACT.Identity, scale=mo[:, 0:1], bias=params[:, 80 + h:81 + h]
+            )
 
         def node_out(h):
             for n in range(2):
@@ -387,17 +410,9 @@ def tile_gnn_s2_pa_t_kernel(
                 add_residual(ux[h][:, halves[n]], ux[h][:, halves[n]], y[h][:, halves[n]])
                 nc.sync.dma_start(out=x_new_view[:, h, halves[n]], in_=ux[h][:, halves[n]])
 
-        def product_half(w, h, n, tag, dst, vector=False):
-            bank = psum.tile([P, BANK], F32, name="product", tag=tag, bufs=1)
+        def product_half(w, h, n, bank):
             mx_group(bank[:], passes(x_codes[:, h, :], x_scales[:, h, :], w, halves[n]))
-            copy_on(vector, dst[:, halves[n]], bank[:])
-
-        def park_vx():
-            for h in range(2):
-                vx_rows = new_ev()
-                for n in range(2):
-                    product_half(W_V, h, n, sum_tags[("ev", "exp")[h]][n], vx_rows)
-                nc.sync.dma_start(out=x_new_view[:, h, :], in_=vx_rows[:])
+            return bank
 
         free_tags = sum_tags["exp"] + sum_tags["ev"]
         free_taken = [0]
@@ -408,46 +423,142 @@ def tile_gnn_s2_pa_t_kernel(
             bank = psum.tile([P, BANK], F32, name="free_bank", tag=tag, bufs=1)
             return bank
 
-        late_pieces = {0: (12, 13), 1: (14, 15), 2: (16, 17), 3: (18, 19)}
+        def stats_bank():
+            bank = psum.tile([P, BANK], F32, name="stats_bank", tag="stats", bufs=1)
+            return bank
 
-        def late_prepare(t):
-            for k in late_pieces.get(t, ()):
-                prepare_piece(k, free_bank, (False, True))
+        params = resident.tile([P, 96], F32, name="params")
 
-        def late_quantise(t):
-            for k in late_pieces.get(t - 1, ()):
+        def spread_parameters():
+            params_scaled = resident.tile([P, 96], F32, name="params_scaled")
+            nc.vector.tensor_scalar(
+                out=params_scaled[:], in0=params_rows[:], scalar1=float(SAMPLES), scalar2=None, op0=ALU.mult
+            )
+            params_ps = psum.tile([P, 96], F32, name="params_ps", tag="stats", bufs=1)
+            nc.tensor.matmul(params_ps[:], lhsT=average[:], rhs=params_scaled[:], start=True, stop=True)
+            nc.vector.tensor_copy(out=params[:], in_=params_ps[:])
+
+        products = {}
+        vx_rows = {}
+
+        def multiply_x(w, h, n, next_bank):
+            products[(w, h, n)] = product_half(w, h, n, next_bank())
+
+        def copy_product(w, h, n, vector):
+            if w == W_V and n == 0:
+                vx_rows[h] = new_ev()
+            dst = {W_A: ax, W_U: ux, W_V: vx_rows}[w][h]
+            copy_on(vector, dst[:, halves[n]], products[(w, h, n)][:])
+            if w == W_V and n == 1:
+                nc.sync.dma_start(out=x_new_view[:, h, :], in_=vx_rows[h][:])
+
+        REPEATS = {0: 4, 5: 5, 6: 6, 7: 7}
+
+        def T(*ks):
+            for k in ks:
+                transpose_piece(k, free_bank)
+
+        def Q(*ks):
+            for k in ks:
                 quantise_piece(k)
 
+        def CS(k, a):
+            copy_half(k, a, False)
+
+        def CV(k, a):
+            copy_half(k, a, True)
+
+        def M(w, h, n):
+            multiply_x(w, h, n, free_bank)
+
+        def MS(w, h, n):
+            multiply_x(w, h, n, stats_bank)
+
+        def PS(w, h, n):
+            copy_product(w, h, n, False)
+
+        def PV(w, h, n):
+            copy_product(w, h, n, True)
+
+        EXTRA = {
+            (1, "P1"): [(T, 13), (transpose_edges, 3), (spread_parameters,)],
+            (1, "S1"): [(CS, 13, 0)],
+            (1, "V1"): [(Q, 12), (CV, 13, 1)],
+            (1, "P2"): [(T, 14, 15)],
+            (1, "V2"): [(Q, 13)],
+            (2, "S0"): [(CS, 14, 0), (CS, 14, 1), (CS, 15, 0)],
+            (2, "V0"): [(CV, 15, 1), (Q, 14), (Q, 15)],
+            (2, "P1"): [(T, 16)],
+            (2, "V1"): [(CV, 16, 1)],
+            (2, "S1"): [(CS, 16, 0)],
+            (2, "P2"): [(M, W_V, 0, 0), (M, W_V, 1, 0), (M, W_V, 0, 1), (M, W_V, 1, 1), (T, 17)],
+            (2, "S2"): [(PS, W_V, 0, 0), (PS, W_V, 1, 0), (CS, 17, 0)],
+            (2, "V2"): [(PV, W_V, 0, 1), (PV, W_V, 1, 1), (CV, 17, 1), (Q, 16)],
+            (3, "P1"): [(T, 18)],
+            (3, "S1"): [(CS, 18, 0)],
+            (3, "V1"): [(CV, 18, 1)],
+            (3, "P2"): [(T, 19), (M, W_A, 1, 0), (M, W_A, 1, 1)],
+            (3, "V2"): [(Q, 17), (Q, 18)],
+            (3, "S2"): [(CS, 19, 0), (PS, W_A, 1, 0)],
+            (4, "V0"): [(CV, 19, 1), (PV, W_A, 1, 1)],
+            (4, "V2"): [(Q, 19)],
+            (4, "P2"): [(MS, W_U, 0, 0)],
+            (5, "S0"): [(PS, W_U, 0, 0)],
+            (5, "P2"): [(MS, W_U, 0, 1)],
+            (6, "S0"): [(PS, W_U, 0, 1)],
+            (6, "P2"): [(MS, W_U, 1, 0)],
+            (7, "S0"): [(PS, W_U, 1, 0)],
+            (7, "P2"): [(MS, W_U, 1, 1)],
+            (8, "S0"): [(PS, W_U, 1, 1)],
+        }
+
+        def extra(t, slot):
+            for f, *args in EXTRA.get((t, slot), ()):
+                f(*args)
+
         def period(t):
-            normalise(t - 2)
             edge_squares(t - 1)
-            quantise_edges(t + 1)
-            late_quantise(t)
+            extra(t, "S0")
+            normalise(t - 2)
+            extra(t, "V0")
             if t > 0:
+                quantise_edges(t + 1)
                 fill_bank(t, 0)
+            extra(t, "P1")
             finish_edge_new(t - 2)
             times_vx(t - VX_LAG)
             if is_tile(t - VX_LAG):
                 load_vx(t - VX_LAG + VX_BUFS)
-            tanh_half(t - 3)
+            if t <= CATCH_UP:
+                tanh_half(t - 3)
+            else:
+                exp_half(t - 3)
             sum_exp(t - 4)
             edge_average(t - 1)
             edge_variance(t - 1)
             edge_scale_and_bias(t - 1)
-            empty_bank(t, 0)
+            extra(t, "V1")
+            if t > 0:
+                empty_bank(t, 0)
             if t == NODES + VX_LAG:
                 for n in range(2):
-                    nc.vector.tensor_copy(out=sum_ev0[:, halves[n]], in_=sums_ps[("ev", 0, n)][:])
-            copy_transposed(t + 2)
+                    copy_on(n == 1, sum_ev0[:, halves[n]], sums_ps[("ev", 0, n)][:])
+            if t > 0:
+                copy_transposed(t + 2)
+            extra(t, "S1")
             if t > 0:
                 fill_bank(t, 1)
-            exp_half(t - 3)
+            if t <= CATCH_UP:
+                exp_half(t - 3)
+            if t >= CATCH_UP:
+                tanh_half(t - 2)
             sum_ev(t - VX_LAG)
-            transpose_edges(t + 3)
-            empty_bank(t, 1)
-            if t == 2:
-                park_vx()
-            late_prepare(t)
+            if t > 0:
+                transpose_edges(t + 3)
+                empty_bank(t, 1)
+            extra(t, "P2")
+            extra(t, "S2")
+            extra(t, "V2")
 
         x_rows = work.tile([P, 2, C], BF16, name="x_rows", tag="edge_new", bufs=EDGE_NEW_BUFS)
         nc.sync.dma_start(out=x_rows[:], in_=x_view)
@@ -456,7 +567,7 @@ def tile_gnn_s2_pa_t_kernel(
             if k == 3:
                 load_edges(0, 0, 1)
             if k == 7:
-                load_edges(0, 1, 3)
+                load_edges(0, 1, 4)
         params_rows = resident.tile([P, 96], BF16, name="params_rows")
         nc.vector.memset(params_rows[:], 0.0)
         nc.sync.dma_start(out=params_rows[0:8, 0:32], in_=bne_w.rearrange("(l x) -> l x", l=8))
@@ -487,129 +598,130 @@ def tile_gnn_s2_pa_t_kernel(
                 out=x_codes[:, h, :].bitcast(FP8X4), scales=x_scales[:, h, :], in_=x_grouped[h][:]
             )
 
+        def quadruple_scales():
+            for i in range(4):
+                nc.vector.tensor_copy(
+                    out=x_scales4[:].rearrange("p (n i) -> p n i", i=4)[:, :, i],
+                    in_=x_scales[:].rearrange("p h w -> p (h w)"),
+                )
+
         def repeat_x(q):
-            repeated = work.tile([P, 2048], BF16, name="repeated", tag="evs", bufs=EV_BUFS, align_bytes=64)
-            dst = repeated[:].bitcast(F32).rearrange(
-                "p (jj g b l u) -> p jj g b l u", jj=2, g=2, b=16, l=8, u=2
+            def repeated(words, times):
+                per_node = words.rearrange("p (hg b l) -> p hg b l", hg=4, b=16, l=8)[:, :, :, q]
+                return per_node.unsqueeze(3).to_broadcast([P, 4, 16, times])
+
+            nc.vector.tensor_copy(
+                out=xj_codes[:, 2 * q:2 * q + 2, :].rearrange("p j w -> p (j w)").bitcast(I32).rearrange(
+                    "p (jg b l) -> p jg b l", jg=4, b=16, l=8
+                ),
+                in_=repeated(x_codes[:].rearrange("p h w -> p (h w)").bitcast(I32), 8),
             )
-            for jj in range(2):
-                j = 2 * q + jj
-                src = x_grouped[j % 2][:].bitcast(F32).rearrange("p (g b l u) -> p g b l u", g=2, b=16, l=8, u=2)
-                for g in range(2):
-                    nc.vector.tensor_copy(
-                        out=dst[:, jj, g, :, :, :],
-                        in_=src[:, g, :, j // 2, :].unsqueeze(2).to_broadcast([P, 16, 8, 2]),
-                    )
-            nc.vector.quantize_mx(
-                out=xj_codes[:, 2 * q:2 * q + 2, :].rearrange("p j w -> p (j w)").bitcast(FP8X4),
-                scales=xj_scales[:, 2 * q:2 * q + 2, :].rearrange("p j w -> p (j w)"),
-                in_=repeated[:],
+            nc.vector.tensor_copy(
+                out=xj_scales[:, 2 * q:2 * q + 2, :].rearrange("p j w -> p (j w)").bitcast(I32).rearrange(
+                    "p (jg b l) -> p jg b l", jg=4, b=16, l=2
+                ),
+                in_=repeated(x_scales4[:].bitcast(I32), 2),
             )
 
-        repeat_x(0)
         for k in range(12):
-            if k == 9:
-                params_scaled = resident.tile([P, 96], F32, name="params_scaled")
-                nc.vector.tensor_scalar(
-                    out=params_scaled[:], in0=params_rows[:], scalar1=float(SAMPLES), scalar2=None, op0=ALU.mult
-                )
-                params_ps = psum.tile([P, 96], F32, name="params_ps", tag="stats", bufs=1)
-                nc.tensor.matmul(params_ps[:], lhsT=average[:], rhs=params_scaled[:], start=True, stop=True)
-                params = resident.tile([P, 96], F32, name="params")
-                nc.vector.tensor_copy(out=params[:], in_=params_ps[:])
-            if k in (2, 5):
-                repeat_x((k + 1) // 3)
-            prepare_piece(k, next_bank if k < 8 else free_bank, (False, k % 2 == 1))
-            quantise_piece(k)
-            if k == 5:
+            if k in (8, 9):
+                quantise_piece(k - 1)
+                fill_bank(0, k - 8)
+                repeat_x(k - 7)
+                if k == 8:
+                    repeat_x(3)
+            transpose_piece(k, next_bank if k < 8 else free_bank)
+            if k == 0:
+                quadruple_scales()
+                repeat_x(0)
+            elif k not in (8, 9):
+                quantise_piece(k - 1)
+            copy_piece(k, k >= 8 or k % 2 == 1)
+            if k == 4:
                 transpose_edges(0)
                 copy_transposed(0)
             if k == 6:
                 quantise_edges(0)
+            if k == 9:
                 transpose_edges(1)
                 copy_transposed(1)
-            if k == 7:
-                transpose_edges(2)
-            if k in (9, 11):
-                fill_bank(0, (k - 9) // 2)
-        load_edges(0, 3, 4)
+            if k == 10:
+                bank = product_half(W_A, 0, 0, free_bank())
+                nc.scalar.copy(out=ax[0][:, halves[0]], in_=bank[:])
+        transpose_edges(2)
+        quantise_piece(11)
+        empty_bank(0, 0)
+        transpose_piece(12, free_bank)
+        bank = product_half(W_A, 0, 1, free_bank())
+        nc.scalar.copy(out=ax[0][:, halves[1]], in_=bank[:])
+        quantise_edges(1)
+        copy_transposed(2)
+        copy_piece(12, True)
+        empty_bank(0, 1)
         load_edges(1, 0, 4)
+
+        for t in range(TILES):
+            period(t)
+            if t in REPEATS:
+                repeat_x(REPEATS[t])
+            if t == 1:
+                load_edges(2, 0, 4)
+            if t == 2:
+                for u in range(VX_BUFS):
+                    load_vx(u)
+            if t % 4 == 1 and 5 <= t <= 21:
+                load_edges((t + 7) // 4, 0, 4)
+            if t == NODES + 3:
+                for n in range(2):
+                    nc.scalar.copy(out=sum_exp0[:, halves[n]], in_=sums_ps[("exp", 0, n)][:])
+
+        last = TILES - 1
+        edge_squares(last, halves)
+        sum_exp(last - 3)
+        edge_average(last)
+        exp_half(last - 2)
+        edge_variance(last)
+        edge_scale_and_bias(last)
+        normalise(last - 1)
+        times_vx(last - 3)
+        sum_ev(last - 3)
+        finish_edge_new(last - 1)
+        tanh_half(last - 1)
+        sum_exp(last - 2)
+        exp_half(last - 1)
+        normalise(last)
+        finish_edge_new(last, halves)
+        sum_exp(last - 1)
+        tanh_half(last, halves)
+        times_vx(last - 2)
+        sum_ev(last - 2)
+        exp_half(last, halves)
+        sum_exp(last)
+        times_vx(last - 1)
+        sum_ev(last - 1)
+        times_vx(last, halves)
+        sum_ev(last)
+
+        inverse[0], inverse[1] = sum_exp0, new_edge_new()
+        inverted, rest = inverse[0][:, :INVERTED], inverse[0][:, INVERTED:]
+        nc.vector.reciprocal(out=inverted, in_=inverted)
         for n in range(2):
-            product_half(W_A, 0, n, sum_tags["exp"][n], ax[0], vector=(n == 1))
-
-        with tc.manual_schedule():
-            for t in range(TILES):
-                period(t)
-                if t in (1, 3, 5, 7, 9):
-                    repeat_x((t + 5) // 2)
-                if t == 1:
-                    load_edges(2, 0, 4)
-                if t == 2:
-                    for u in range(VX_BUFS):
-                        load_vx(u)
-                if t % 4 == 1 and 5 <= t <= 21:
-                    load_edges((t + 7) // 4, 0, 4)
-                if t in (5, 6):
-                    product_half(W_A, 1, t - 5, "stats", ax[1])
-                if 7 <= t < 11:
-                    product_half(W_U, (t - 7) // 2, (t - 7) % 2, "stats", ux[(t - 7) // 2])
-                if t == NODES + 3:
-                    for n in range(2):
-                        nc.scalar.copy(out=sum_exp0[:, halves[n]], in_=sums_ps[("exp", 0, n)][:])
-                if t >= FIRST_RECIPROCAL:
-                    invert_sum_exp0(t - FIRST_RECIPROCAL)
-
-            part = TILES - FIRST_RECIPROCAL
-            last = TILES - 1
-            edge_squares(last)
-            sum_exp(last - 3)
-            edge_average(last)
-            edge_variance(last)
-            edge_scale_and_bias(last)
-            normalise(last - 1)
-            times_vx(last - 3)
-            sum_ev(last - 3)
-            finish_edge_new(last - 1)
-            invert_sum_exp0(part)
-            normalise(last)
-            invert_sum_exp0(part + 1)
-            tanh_half(last - 2)
-            exp_half(last - 2)
-            tanh_half(last - 1)
-            exp_half(last - 1)
-            finish_edge_new(last, halves)
-            times_vx(last - 2)
-            sum_exp(last - 2)
-            sum_ev(last - 2)
-            tanh_half(last, halves)
-            exp_half(last, halves)
-            warm = columns.tile([P, 1], F32, name="warm", tag="warm", bufs=1)
-            nc.scalar.activation(out=warm[:], in_=exps[last][:, C - 1:C], func=ACT.Ln)
-            times_vx(last - 1)
-            sum_exp(last - 1)
-            sum_ev(last - 1)
-            for p in range(part + 2, RECIPROCAL_PARTS):
-                invert_sum_exp0(p)
-            sum_exp(last)
-            times_vx(last, halves)
-            sum_ev(last)
-
-            inverse[0] = sum_exp0
-            inverse[1] = new_edge_new()
-            for n in range(2):
-                nc.scalar.activation(out=inverse[1][:, halves[n]], in_=sums_ps[("exp", 1, n)][:], func=ACT.Ln)
-            for n in range(2):
-                nc.scalar.activation(
-                    out=inverse[1][:, halves[n]], in_=inverse[1][:, halves[n]], func=ACT.Exp, scale=-1.0
-                )
-            for h in range(2):
-                node_agg(h)
-                node_y(h)
-            node_squares(0, 0)
-            node_squares(0, 1)
-            node_squares(1, 0)
-            node_scale_and_bias(0)
-            node_squares(1, 1)
-            node_scale_and_bias(1)
-            for h in range(2):
-                node_out(h)
+            cols = inverse[1][:, halves[n]]
+            nc.scalar.activation(out=cols, in_=sums_ps[("exp", 1, n)][:], func=ACT.Ln)
+            nc.scalar.activation(out=cols, in_=cols, func=ACT.Exp, scale=-1.0)
+        nc.scalar.activation(out=rest, in_=rest, func=ACT.Ln)
+        nc.scalar.activation(out=rest, in_=rest, func=ACT.Exp, scale=-1.0)
+        node_agg(1, 0)
+        node_agg(1, 1)
+        node_y(1, 0)
+        node_y(1, 1)
+        node_row_sums(1)
+        node_scale_and_bias(1)
+        node_agg(0, 0)
+        node_agg(0, 1)
+        node_y(0, 0)
+        node_y(0, 1)
+        node_row_sums(0)
+        node_scale_and_bias(0)
+        node_out(1)
+        node_out(0)

@@ -39,7 +39,6 @@ EXP_BUFS = 3
 EV_BUFS = 3
 VX_BUFS = 4
 CATCH_UP = 30
-INVERTED = 256
 VX_LAG = 4
 
 
@@ -389,19 +388,9 @@ def tile_gnn_s2_pa_t_kernel(
             complete_row_sums(NODE_KEY + h, y[h], node_sums[h], halves)
 
         def node_scale_and_bias(h):
-            key = NODE_KEY + h
-            average_over_batches(key)
-            scale_bias[key] = columns.tile([P, 2], F32, name="scale_bias", tag="scale_bias")
-            mo = columns.tile([P, 4], F32, name="moments", tag="moments")
-            sb, ps = scale_bias[key], means_ps[key]
-            nc.scalar.activation(out=mo[:, 0:1], in_=ps[:, 0:1], func=ACT.Identity, scale=-1.0)
-            nc.scalar.activation(out=mo[:, 1:2], in_=ps[:, 1:2], func=ACT.Identity, bias=eps[:])
-            nc.scalar.activation(out=mo[:, 2:3], in_=ps[:, 0:1], func=ACT.Ln, scale=mo[:, 0:1], bias=mo[:, 1:2])
-            nc.scalar.activation(out=mo[:, 3:4], in_=mo[:, 2:3], func=ACT.Exp, scale=-0.5)
-            nc.scalar.activation(out=sb[:, 0:1], in_=mo[:, 3:4], func=ACT.Identity, scale=params[:, 64 + h:65 + h])
-            nc.scalar.activation(
-                out=sb[:, 1:2], in_=sb[:, 0:1], func=ACT.Identity, scale=mo[:, 0:1], bias=params[:, 80 + h:81 + h]
-            )
+            average_over_batches(NODE_KEY + h)
+            variance(NODE_KEY + h)
+            scale_and_bias(NODE_KEY + h, params[:, 64 + h:65 + h], params[:, 80 + h:81 + h])
 
         def node_out(h):
             for n in range(2):
@@ -637,6 +626,8 @@ def tile_gnn_s2_pa_t_kernel(
             elif k not in (8, 9):
                 quantise_piece(k - 1)
             copy_piece(k, k >= 8 or k % 2 == 1)
+            if k == 5:
+                load_edges(1, 0, 2)
             if k == 4:
                 transpose_edges(0)
                 copy_transposed(0)
@@ -658,7 +649,7 @@ def tile_gnn_s2_pa_t_kernel(
         copy_transposed(2)
         copy_piece(12, True)
         empty_bank(0, 1)
-        load_edges(1, 0, 4)
+        load_edges(1, 2, 4)
 
         for t in range(TILES):
             period(t)
@@ -689,6 +680,7 @@ def tile_gnn_s2_pa_t_kernel(
         tanh_half(last - 1)
         sum_exp(last - 2)
         exp_half(last - 1)
+        nc.vector.reciprocal(out=sum_exp0[:, :128], in_=sum_exp0[:, :128])
         normalise(last)
         finish_edge_new(last, halves)
         sum_exp(last - 1)
@@ -703,13 +695,14 @@ def tile_gnn_s2_pa_t_kernel(
         sum_ev(last)
 
         inverse[0], inverse[1] = sum_exp0, new_edge_new()
-        inverted, rest = inverse[0][:, :INVERTED], inverse[0][:, INVERTED:]
+        inverted, rest = inverse[0][:, 128:640], inverse[0][:, 640:]
         nc.vector.reciprocal(out=inverted, in_=inverted)
+        nc.scalar.activation(out=rest, in_=rest, func=ACT.Ln)
+        for n in range(2):
+            nc.scalar.activation(out=inverse[1][:, halves[n]], in_=sums_ps[("exp", 1, n)][:], func=ACT.Ln)
         for n in range(2):
             cols = inverse[1][:, halves[n]]
-            nc.scalar.activation(out=cols, in_=sums_ps[("exp", 1, n)][:], func=ACT.Ln)
             nc.scalar.activation(out=cols, in_=cols, func=ACT.Exp, scale=-1.0)
-        nc.scalar.activation(out=rest, in_=rest, func=ACT.Ln)
         nc.scalar.activation(out=rest, in_=rest, func=ACT.Exp, scale=-1.0)
         node_agg(1, 0)
         node_agg(1, 1)

@@ -388,9 +388,20 @@ def tile_gnn_s2_pa_t_kernel(
             complete_row_sums(NODE_KEY + h, y[h], node_sums[h], halves)
 
         def node_scale_and_bias(h):
-            average_over_batches(NODE_KEY + h)
-            variance(NODE_KEY + h)
-            scale_and_bias(NODE_KEY + h, params[:, 64 + h:65 + h], params[:, 80 + h:81 + h])
+            key = NODE_KEY + h
+            average_over_batches(key)
+            scale_bias[key] = columns.tile([P, 2], F32, name="scale_bias", tag="scale_bias")
+            mo = columns.tile([P, 4], F32, name="moments", tag="moments")
+            sb, ps = scale_bias[key], means_ps[key]
+            nc.scalar.activation(out=mo[:, 0:1], in_=ps[:, 0:1], func=ACT.Identity, scale=-1.0)
+            nc.scalar.activation(out=mo[:, 1:2], in_=ps[:, 1:2], func=ACT.Identity, bias=eps[:])
+            nc.scalar.activation(
+                out=mo[:, 2:3], in_=ps[:, 0:1], func=ACT.Abs_reciprocal_sqrt, scale=mo[:, 0:1], bias=mo[:, 1:2]
+            )
+            nc.scalar.activation(out=sb[:, 0:1], in_=mo[:, 2:3], func=ACT.Identity, scale=params[:, 64 + h:65 + h])
+            nc.scalar.activation(
+                out=sb[:, 1:2], in_=sb[:, 0:1], func=ACT.Identity, scale=mo[:, 0:1], bias=params[:, 80 + h:81 + h]
+            )
 
         def node_out(h):
             for n in range(2):
@@ -477,12 +488,9 @@ def tile_gnn_s2_pa_t_kernel(
             (1, "V2"): [(Q, 13)],
             (2, "S0"): [(CS, 14, 0), (CS, 14, 1), (CS, 15, 0)],
             (2, "V0"): [(CV, 15, 1), (Q, 14), (Q, 15)],
-            (2, "P1"): [(T, 16)],
-            (2, "V1"): [(CV, 16, 1)],
-            (2, "S1"): [(CS, 16, 0)],
-            (2, "P2"): [(M, W_V, 0, 0), (M, W_V, 1, 0), (M, W_V, 0, 1), (M, W_V, 1, 1), (T, 17)],
-            (2, "S2"): [(PS, W_V, 0, 0), (PS, W_V, 1, 0), (CS, 17, 0)],
-            (2, "V2"): [(PV, W_V, 0, 1), (PV, W_V, 1, 1), (CV, 17, 1), (Q, 16)],
+            (2, "P2"): [(M, W_V, 0, 0), (M, W_V, 1, 0), (M, W_V, 0, 1), (M, W_V, 1, 1), (T, 16, 17)],
+            (2, "S2"): [(PS, W_V, 0, 0), (PS, W_V, 1, 0), (CS, 16, 0), (CS, 17, 0)],
+            (2, "V2"): [(PV, W_V, 0, 1), (PV, W_V, 1, 1), (CV, 16, 1), (CV, 17, 1), (Q, 16)],
             (3, "P1"): [(T, 18)],
             (3, "S1"): [(CS, 18, 0)],
             (3, "V1"): [(CV, 18, 1)],
@@ -612,6 +620,11 @@ def tile_gnn_s2_pa_t_kernel(
                 in_=repeated(x_scales4[:].bitcast(I32), 2),
             )
 
+        def keep_clock_up(times):
+            for i in range(times):
+                idle = psum.tile([P, BANK], F32, name="idle", tag="transposed", bufs=1)
+                nc.tensor.matmul(idle[:], lhsT=x_grouped[0][:, :P], rhs=x_grouped[0][:, BANK:], start=True, stop=True)
+
         for k in range(12):
             if k in (8, 9):
                 quantise_piece(k - 1)
@@ -620,6 +633,7 @@ def tile_gnn_s2_pa_t_kernel(
                 if k == 8:
                     repeat_x(3)
             transpose_piece(k, next_bank if k < 8 else free_bank)
+            keep_clock_up({9: 1, 10: 1, 11: 1}.get(k, 0))
             if k == 0:
                 quadruple_scales()
                 repeat_x(0)
@@ -669,6 +683,7 @@ def tile_gnn_s2_pa_t_kernel(
         last = TILES - 1
         edge_squares(last, halves)
         sum_exp(last - 3)
+        keep_clock_up(3)
         edge_average(last)
         exp_half(last - 2)
         edge_variance(last)
@@ -676,34 +691,35 @@ def tile_gnn_s2_pa_t_kernel(
         normalise(last - 1)
         times_vx(last - 3)
         sum_ev(last - 3)
+        keep_clock_up(2)
         finish_edge_new(last - 1)
         tanh_half(last - 1)
         sum_exp(last - 2)
+        keep_clock_up(2)
         exp_half(last - 1)
-        nc.vector.reciprocal(out=sum_exp0[:, :128], in_=sum_exp0[:, :128])
         normalise(last)
         finish_edge_new(last, halves)
         sum_exp(last - 1)
+        keep_clock_up(2)
         tanh_half(last, halves)
         times_vx(last - 2)
         sum_ev(last - 2)
+        keep_clock_up(1)
         exp_half(last, halves)
         sum_exp(last)
+        keep_clock_up(1)
         times_vx(last - 1)
         sum_ev(last - 1)
         times_vx(last, halves)
         sum_ev(last)
 
         inverse[0], inverse[1] = sum_exp0, new_edge_new()
-        inverted, rest = inverse[0][:, 128:640], inverse[0][:, 640:]
-        nc.vector.reciprocal(out=inverted, in_=inverted)
-        nc.scalar.activation(out=rest, in_=rest, func=ACT.Ln)
-        for n in range(2):
-            nc.scalar.activation(out=inverse[1][:, halves[n]], in_=sums_ps[("exp", 1, n)][:], func=ACT.Ln)
         for n in range(2):
             cols = inverse[1][:, halves[n]]
-            nc.scalar.activation(out=cols, in_=cols, func=ACT.Exp, scale=-1.0)
-        nc.scalar.activation(out=rest, in_=rest, func=ACT.Exp, scale=-1.0)
+            nc.scalar.activation(out=cols, in_=sums_ps[("exp", 1, n)][:], func=ACT.Abs_reciprocal_sqrt)
+            nc.scalar.activation(out=cols, in_=cols, func=ACT.Square)
+        nc.scalar.activation(out=inverse[0][:], in_=inverse[0][:], func=ACT.Abs_reciprocal_sqrt)
+        nc.scalar.activation(out=inverse[0][:], in_=inverse[0][:], func=ACT.Square)
         node_agg(1, 0)
         node_agg(1, 1)
         node_y(1, 0)

@@ -180,15 +180,22 @@ def tile_gnn_s2_pa_t_kernel(
 
         def average_over_batches(key):
             means_ps[key] = psum.tile([P, 2], F32, name="means_ps", tag="stats", bufs=1)
-            nc.tensor.matmul(means_ps[key][:], lhsT=average[:], rhs=sums_of[key], start=True, stop=True)
+            last_part = len(sums_of[key]) - 1
+            for i, sums in enumerate(sums_of[key]):
+                nc.tensor.matmul(
+                    means_ps[key][:], lhsT=average[:], rhs=sums, start=(i == 0), stop=(i == last_part)
+                )
 
-        def variance(key):
+        def minus_mean_and_squares(key):
             moments[key] = columns.tile([P, 4], F32, name="moments", tag="moments")
             mo, ps = moments[key], means_ps[key]
             nc.scalar.activation(out=mo[:, 0:1], in_=ps[:, 0:1], func=ACT.Identity, scale=-1.0)
             nc.scalar.activation(out=mo[:, 1:2], in_=ps[:, 1:2], func=ACT.Identity, bias=eps[:])
+
+        def variance(key):
+            mo = moments[key]
             nc.scalar.activation(
-                out=mo[:, 2:3], in_=ps[:, 0:1], func=ACT.Identity, scale=mo[:, 0:1], bias=mo[:, 1:2]
+                out=mo[:, 2:3], in_=means_ps[key][:, 0:1], func=ACT.Identity, scale=mo[:, 0:1], bias=mo[:, 1:2]
             )
 
         def scale_and_bias(key, gain, offset):
@@ -275,24 +282,34 @@ def tile_gnn_s2_pa_t_kernel(
                 )
 
         def sum_squares(src, cols, dst):
-            squares = work.tile([P, C], BF16, name="squares", tag="squares", bufs=1)
+            squares = work.tile([P, C], BF16, name="squares", tag="squares", bufs=2)
             nc.scalar.activation(out=squares[:, cols], in_=src, func=ACT.Square, accum_out=dst)
 
-        def complete_row_sums(key, src, rs, parts):
-            for n, cols in enumerate(parts):
-                sum_squares(src[:, cols], cols, rs[:, 2 + n:3 + n] if len(parts) == 2 else rs[:, 5:6])
+        def complete_row_sums(key, src, rs):
+            sum_squares(src, whole[0], rs[:, 5:6])
             add_columns(rs[:, 4:5], rs[:, 0:1], rs[:, 1:2])
-            if len(parts) == 2:
-                add_columns(rs[:, 5:6], rs[:, 2:3], rs[:, 3:4])
-            sums_of[key] = rs[:, 4:6]
+            sums_of[key] = [rs[:, 4:6]]
 
-        def edge_squares(t, parts=whole):
+        def half_sums(rs):
+            return [rs[:, n:n + 3:2] for n in range(2)]
+
+        def half_squares(t, n):
+            sum_squares(edge_new[t][:, halves[n]], halves[n], row_sums[:, t % 8, 2 + n:3 + n])
+
+        def add_half_sums(t):
+            sums_of[t] = half_sums(row_sums[:, t % 8, :])
+
+        def edge_squares(t):
             if is_tile(t):
-                complete_row_sums(t, edge_new[t], row_sums[:, t % 8, :], parts)
+                complete_row_sums(t, edge_new[t][:], row_sums[:, t % 8, :])
 
         def edge_average(t):
             if is_tile(t):
                 average_over_batches(t)
+
+        def edge_moments(t):
+            if is_tile(t):
+                minus_mean_and_squares(t)
 
         def edge_variance(t):
             if is_tile(t):
@@ -302,9 +319,10 @@ def tile_gnn_s2_pa_t_kernel(
             if is_tile(t):
                 scale_and_bias(t, params[:, t:t + 1], params[:, 32 + t:33 + t])
 
-        def normalise(t):
+        def normalise(t, parts=whole):
             if is_tile(t):
-                apply_norm(t, edge_new[t][:], edge_new[t][:])
+                for cols in parts:
+                    apply_norm(t, edge_new[t][:, cols], edge_new[t][:, cols])
 
         def finish_edge_new(t, parts=whole):
             if is_tile(t):
@@ -318,10 +336,13 @@ def tile_gnn_s2_pa_t_kernel(
                 for cols in parts:
                     nc.scalar.activation(out=exps[t][:, cols], in_=edge_new[t][:, cols], func=ACT.Tanh, scale=0.5)
 
+        def exp_of(t, cols):
+            nc.scalar.activation(out=exps[t][:, cols], in_=exps[t][:, cols], func=ACT.Exp, scale=0.5)
+
         def exp_half(t, parts=whole):
             if is_tile(t):
                 for cols in parts:
-                    nc.scalar.activation(out=exps[t][:, cols], in_=exps[t][:, cols], func=ACT.Exp, scale=0.5)
+                    exp_of(t, cols)
 
         def new_ev():
             ev = work.tile([P, C], F32, name="evs", tag="evs", bufs=EV_BUFS, align_bytes=64)
@@ -385,7 +406,17 @@ def tile_gnn_s2_pa_t_kernel(
             )
 
         def node_row_sums(h):
-            complete_row_sums(NODE_KEY + h, y[h], node_sums[h], halves)
+            for n in range(2):
+                dst = node_sums[h][:, 2 + n:3 + n]
+                if h == 1:
+                    sum_squares(y[h][:, halves[n]], halves[n], dst)
+                else:
+                    squares = work.tile([P, C], BF16, name="squares", tag="squares", bufs=2)
+                    nc.vector.scalar_tensor_tensor(
+                        out=squares[:, halves[n]], in0=y[h][:, halves[n]], scalar=1.0, in1=y[h][:, halves[n]],
+                        op0=ALU.mult, op1=ALU.mult, accum_out=dst,
+                    )
+            sums_of[NODE_KEY + h] = half_sums(node_sums[h])
 
         def node_scale_and_bias(h):
             key = NODE_KEY + h
@@ -395,13 +426,13 @@ def tile_gnn_s2_pa_t_kernel(
             sb, ps = scale_bias[key], means_ps[key]
             nc.scalar.activation(out=mo[:, 0:1], in_=ps[:, 0:1], func=ACT.Identity, scale=-1.0)
             nc.scalar.activation(out=mo[:, 1:2], in_=ps[:, 1:2], func=ACT.Identity, bias=eps[:])
+            gain, offset = params[:, 64 + h:65 + h], params[:, 80 + h:81 + h]
+            nc.scalar.activation(out=mo[:, 3:4], in_=mo[:, 0:1], func=ACT.Identity, scale=gain)
             nc.scalar.activation(
                 out=mo[:, 2:3], in_=ps[:, 0:1], func=ACT.Abs_reciprocal_sqrt, scale=mo[:, 0:1], bias=mo[:, 1:2]
             )
-            nc.scalar.activation(out=sb[:, 0:1], in_=mo[:, 2:3], func=ACT.Identity, scale=params[:, 64 + h:65 + h])
-            nc.scalar.activation(
-                out=sb[:, 1:2], in_=sb[:, 0:1], func=ACT.Identity, scale=mo[:, 0:1], bias=params[:, 80 + h:81 + h]
-            )
+            nc.scalar.activation(out=sb[:, 0:1], in_=mo[:, 2:3], func=ACT.Identity, scale=gain)
+            nc.scalar.activation(out=sb[:, 1:2], in_=mo[:, 2:3], func=ACT.Identity, scale=mo[:, 3:4], bias=offset)
 
         def node_out(h):
             for n in range(2):
@@ -516,43 +547,52 @@ def tile_gnn_s2_pa_t_kernel(
         def period(t):
             edge_squares(t - 1)
             extra(t, "S0")
-            normalise(t - 2)
-            extra(t, "V0")
             if t > 0:
                 quantise_edges(t + 1)
-                fill_bank(t, 0)
-            extra(t, "P1")
-            finish_edge_new(t - 2)
+            extra(t, "V0")
             times_vx(t - VX_LAG)
             if is_tile(t - VX_LAG):
                 load_vx(t - VX_LAG + VX_BUFS)
+            normalise(t - 2)
+            if t > 0:
+                fill_bank(t, 0)
+            extra(t, "P1")
             if t <= CATCH_UP:
                 tanh_half(t - 3)
             else:
                 exp_half(t - 3)
             sum_exp(t - 4)
             edge_average(t - 1)
-            edge_variance(t - 1)
-            edge_scale_and_bias(t - 1)
-            extra(t, "V1")
-            if t > 0:
-                empty_bank(t, 0)
             if t == NODES + VX_LAG:
                 for n in range(2):
                     copy_on(n == 1, sum_ev0[:, halves[n]], sums_ps[("ev", 0, n)][:])
+            edge_moments(t - 1)
+            extra(t, "V1")
+            if t > 0:
+                empty_bank(t, 0)
+            finish_edge_new(t - 2)
             if t > 0:
                 copy_transposed(t + 2)
+            if t == TILES - 1:
+                half_squares(t, 0)
+            edge_variance(t - 1)
+            edge_scale_and_bias(t - 1)
             extra(t, "S1")
+            if t == NODES + 3:
+                for n in range(2):
+                    copy_on(n == 1, sum_exp0[:, halves[n]], sums_ps[("exp", 0, n)][:])
             if t > 0:
                 fill_bank(t, 1)
             if t <= CATCH_UP:
                 exp_half(t - 3)
-            if t >= CATCH_UP:
+            if t >= CATCH_UP and t < TILES - 1:
                 tanh_half(t - 2)
             sum_ev(t - VX_LAG)
             if t > 0:
                 transpose_edges(t + 3)
                 empty_bank(t, 1)
+            if t == TILES - 1:
+                half_squares(t, 1)
             extra(t, "P2")
             extra(t, "S2")
             extra(t, "V2")
@@ -676,58 +716,61 @@ def tile_gnn_s2_pa_t_kernel(
                     load_vx(u)
             if t % 4 == 1 and 5 <= t <= 21:
                 load_edges((t + 7) // 4, 0, 4)
-            if t == NODES + 3:
-                for n in range(2):
-                    nc.scalar.copy(out=sum_exp0[:, halves[n]], in_=sums_ps[("exp", 0, n)][:])
 
         last = TILES - 1
-        edge_squares(last, halves)
-        sum_exp(last - 3)
-        keep_clock_up(3)
-        edge_average(last)
-        exp_half(last - 2)
-        edge_variance(last)
-        edge_scale_and_bias(last)
-        normalise(last - 1)
+        add_half_sums(last)
         times_vx(last - 3)
+        normalise(last - 1)
+        keep_clock_up(2)
+        sum_exp(last - 3)
+        edge_average(last)
+        keep_clock_up(2)
         sum_ev(last - 3)
         keep_clock_up(2)
+        tanh_half(last - 2)
+        edge_moments(last)
+        exp_of(last - 2, halves[0])
+        edge_variance(last)
+        edge_scale_and_bias(last)
+        exp_of(last - 2, halves[1])
         finish_edge_new(last - 1)
-        tanh_half(last - 1)
         sum_exp(last - 2)
         keep_clock_up(2)
-        exp_half(last - 1)
-        normalise(last)
+        tanh_half(last - 1, halves)
+        exp_half(last - 1, halves)
+        times_vx(last - 2)
+        sum_ev(last - 2)
+        keep_clock_up(2)
+        normalise(last, halves)
         finish_edge_new(last, halves)
         sum_exp(last - 1)
         keep_clock_up(2)
         tanh_half(last, halves)
-        times_vx(last - 2)
-        sum_ev(last - 2)
-        keep_clock_up(1)
-        exp_half(last, halves)
-        sum_exp(last)
-        keep_clock_up(1)
         times_vx(last - 1)
+        exp_half(last, halves)
         sum_ev(last - 1)
+        keep_clock_up(2)
+        sum_exp(last)
         times_vx(last, halves)
         sum_ev(last)
+        keep_clock_up(6)
 
         inverse[0], inverse[1] = sum_exp0, new_edge_new()
-        for n in range(2):
-            cols = inverse[1][:, halves[n]]
-            nc.scalar.activation(out=cols, in_=sums_ps[("exp", 1, n)][:], func=ACT.Abs_reciprocal_sqrt)
-            nc.scalar.activation(out=cols, in_=cols, func=ACT.Square)
-        nc.scalar.activation(out=inverse[0][:], in_=inverse[0][:], func=ACT.Abs_reciprocal_sqrt)
-        nc.scalar.activation(out=inverse[0][:], in_=inverse[0][:], func=ACT.Square)
+        for h in (1, 0):
+            for func in (ACT.Abs_reciprocal_sqrt, ACT.Square):
+                for n in range(2):
+                    cols = inverse[h][:, halves[n]]
+                    src = sums_ps[("exp", 1, n)][:] if h == 1 and func == ACT.Abs_reciprocal_sqrt else cols
+                    nc.scalar.activation(out=cols, in_=src, func=func)
         node_agg(1, 0)
         node_agg(1, 1)
+        keep_clock_up(4)
         node_y(1, 0)
         node_y(1, 1)
-        node_row_sums(1)
-        node_scale_and_bias(1)
         node_agg(0, 0)
         node_agg(0, 1)
+        node_row_sums(1)
+        node_scale_and_bias(1)
         node_y(0, 0)
         node_y(0, 1)
         node_row_sums(0)

@@ -38,7 +38,6 @@ EDGE_NEW_BUFS = 6
 EXP_BUFS = 3
 EV_BUFS = 3
 VX_BUFS = 4
-CATCH_UP = 30
 VX_LAG = 4
 
 
@@ -196,6 +195,22 @@ def tile_gnn_s2_pa_t_kernel(
             mo = moments[key]
             nc.scalar.activation(
                 out=mo[:, 2:3], in_=means_ps[key][:, 0:1], func=ACT.Identity, scale=mo[:, 0:1], bias=mo[:, 1:2]
+            )
+
+        def inverse_deviation(t):
+            mo = moments[t]
+            nc.gpsimd.tensor_tensor(out=mo[:, 2:3], in0=mo[:, 2:3], in1=minus_half[:], op=ALU.pow)
+
+        def minus_mean_times_gain(t):
+            mo = moments[t]
+            nc.scalar.activation(out=mo[:, 3:4], in_=mo[:, 0:1], func=ACT.Identity, scale=params[:, t:t + 1])
+
+        def scale_and_bias_on_scalar(t):
+            scale_bias[t] = columns.tile([P, 2], F32, name="scale_bias", tag="scale_bias")
+            sb, mo = scale_bias[t], moments[t]
+            nc.scalar.activation(out=sb[:, 0:1], in_=mo[:, 2:3], func=ACT.Identity, scale=params[:, t:t + 1])
+            nc.scalar.activation(
+                out=sb[:, 1:2], in_=mo[:, 2:3], func=ACT.Identity, scale=mo[:, 3:4], bias=params[:, 32 + t:33 + t]
             )
 
         def scale_and_bias(key, gain, offset):
@@ -547,20 +562,18 @@ def tile_gnn_s2_pa_t_kernel(
         def period(t):
             edge_squares(t - 1)
             extra(t, "S0")
+            finish_edge_new(t - 3)
             if t > 0:
                 quantise_edges(t + 1)
             extra(t, "V0")
+            if t > 0:
+                fill_bank(t, 0)
+            extra(t, "P1")
             times_vx(t - VX_LAG)
             if is_tile(t - VX_LAG):
                 load_vx(t - VX_LAG + VX_BUFS)
             normalise(t - 2)
-            if t > 0:
-                fill_bank(t, 0)
-            extra(t, "P1")
-            if t <= CATCH_UP:
-                tanh_half(t - 3)
-            else:
-                exp_half(t - 3)
+            tanh_half(t - 3)
             sum_exp(t - 4)
             edge_average(t - 1)
             if t == NODES + VX_LAG:
@@ -570,29 +583,30 @@ def tile_gnn_s2_pa_t_kernel(
             extra(t, "V1")
             if t > 0:
                 empty_bank(t, 0)
-            finish_edge_new(t - 2)
-            if t > 0:
                 copy_transposed(t + 2)
-            if t == TILES - 1:
-                half_squares(t, 0)
             edge_variance(t - 1)
-            edge_scale_and_bias(t - 1)
+            if t < TILES - 1:
+                edge_scale_and_bias(t - 1)
+            else:
+                minus_mean_times_gain(t - 1)
+                inverse_deviation(t - 1)
+                scale_and_bias_on_scalar(t - 1)
+                half_squares(t, 0)
             extra(t, "S1")
             if t == NODES + 3:
                 for n in range(2):
-                    copy_on(n == 1, sum_exp0[:, halves[n]], sums_ps[("exp", 0, n)][:])
+                    copy_on(False, sum_exp0[:, halves[n]], sums_ps[("exp", 0, n)][:])
             if t > 0:
                 fill_bank(t, 1)
-            if t <= CATCH_UP:
+            if t < TILES - 1:
                 exp_half(t - 3)
-            if t >= CATCH_UP and t < TILES - 1:
-                tanh_half(t - 2)
             sum_ev(t - VX_LAG)
             if t > 0:
                 transpose_edges(t + 3)
                 empty_bank(t, 1)
             if t == TILES - 1:
                 half_squares(t, 1)
+                exp_half(t - 3)
             extra(t, "P2")
             extra(t, "S2")
             extra(t, "V2")
@@ -714,42 +728,41 @@ def tile_gnn_s2_pa_t_kernel(
             if t == 2:
                 for u in range(VX_BUFS):
                     load_vx(u)
-            if t % 4 == 1 and 5 <= t <= 21:
-                load_edges((t + 7) // 4, 0, 4)
+            if t % 4 == 2 and 6 <= t <= 22:
+                load_edges((t + 6) // 4, 0, 4)
 
         last = TILES - 1
         add_half_sums(last)
-        times_vx(last - 3)
-        normalise(last - 1)
-        keep_clock_up(2)
-        sum_exp(last - 3)
         edge_average(last)
-        keep_clock_up(2)
+        sum_exp(last - 3)
+        finish_edge_new(last - 2)
+        normalise(last - 1)
+        times_vx(last - 3)
         sum_ev(last - 3)
-        keep_clock_up(2)
         tanh_half(last - 2)
         edge_moments(last)
         exp_of(last - 2, halves[0])
         edge_variance(last)
-        edge_scale_and_bias(last)
+        minus_mean_times_gain(last)
+        inverse_deviation(last)
         exp_of(last - 2, halves[1])
-        finish_edge_new(last - 1)
+        scale_and_bias_on_scalar(last)
+        finish_edge_new(last - 1, halves)
         sum_exp(last - 2)
-        keep_clock_up(2)
+        keep_clock_up(4)
         tanh_half(last - 1, halves)
         exp_half(last - 1, halves)
-        times_vx(last - 2)
-        sum_ev(last - 2)
-        keep_clock_up(2)
         normalise(last, halves)
+        times_vx(last - 2)
         finish_edge_new(last, halves)
+        sum_ev(last - 2)
+        keep_clock_up(1)
         sum_exp(last - 1)
-        keep_clock_up(2)
+        keep_clock_up(1)
         tanh_half(last, halves)
         times_vx(last - 1)
         exp_half(last, halves)
         sum_ev(last - 1)
-        keep_clock_up(2)
         sum_exp(last)
         times_vx(last, halves)
         sum_ev(last)
@@ -764,7 +777,6 @@ def tile_gnn_s2_pa_t_kernel(
                     nc.scalar.activation(out=cols, in_=src, func=func)
         node_agg(1, 0)
         node_agg(1, 1)
-        keep_clock_up(4)
         node_y(1, 0)
         node_y(1, 1)
         node_agg(0, 0)

@@ -62,6 +62,8 @@ def tile_gnn_s2_pa_t_kernel(
         sum_tags = {"exp": ("sum_exp0", "sum_exp1"), "ev": ("sum_ev0", "sum_ev1")}
         ctx.enter_context(tc.manual_schedule())
 
+        warm = resident.tile([P, BANK], BF16, name="warm")
+        nc.vector.memset(warm[:], 0.0)
         ident = resident.tile([P, P], F32, name="ident")
         make_identity(nc, ident[:])
         same_l = resident.tile([P, 8], F32, name="same_l")
@@ -78,6 +80,8 @@ def tile_gnn_s2_pa_t_kernel(
         nc.vector.memset(minus_half[:], -0.5)
         eps = resident.tile([P, 1], F32, name="eps")
         nc.vector.memset(eps[:], EPS)
+        first_tanh = resident.tile([P, 1], F32, name="first_tanh")
+        nc.scalar.activation(out=first_tanh[:], in_=minus_half[:], func=ACT.Tanh)
 
         w_codes = [resident.tile([P, 2, C], U32, name="w_codes%d" % w, align_bytes=64) for w in range(5)]
         w_scales = [resident.tile([P, 2, C], U8, name="w_scales%d" % w, align_bytes=64) for w in range(5)]
@@ -475,14 +479,17 @@ def tile_gnn_s2_pa_t_kernel(
 
         params = resident.tile([P, 96], F32, name="params")
 
-        def spread_parameters():
-            params_scaled = resident.tile([P, 96], F32, name="params_scaled")
+        params_scaled = resident.tile([P, 96], F32, name="params_scaled")
+
+        def scale_parameters():
             nc.vector.tensor_scalar(
                 out=params_scaled[:], in0=params_rows[:], scalar1=float(SAMPLES), scalar2=None, op0=ALU.mult
             )
+
+        def spread_parameters():
             params_ps = psum.tile([P, 96], F32, name="params_ps", tag="stats", bufs=1)
             nc.tensor.matmul(params_ps[:], lhsT=average[:], rhs=params_scaled[:], start=True, stop=True)
-            nc.vector.tensor_copy(out=params[:], in_=params_ps[:])
+            return params_ps
 
         products = {}
         vx_rows = {}
@@ -527,7 +534,7 @@ def tile_gnn_s2_pa_t_kernel(
             copy_product(w, h, n, True)
 
         EXTRA = {
-            (1, "P1"): [(T, 13), (transpose_edges, 3), (spread_parameters,)],
+            (1, "P1"): [(T, 13), (transpose_edges, 3)],
             (1, "S1"): [(CS, 13, 0)],
             (1, "V1"): [(Q, 12), (CV, 13, 1)],
             (1, "P2"): [(T, 14, 15)],
@@ -538,12 +545,11 @@ def tile_gnn_s2_pa_t_kernel(
             (2, "S2"): [(PS, W_V, 0, 0), (PS, W_V, 1, 0), (CS, 16, 0), (CS, 17, 0)],
             (2, "V2"): [(PV, W_V, 0, 1), (PV, W_V, 1, 1), (CV, 16, 1), (CV, 17, 1), (Q, 16)],
             (3, "P1"): [(T, 18)],
-            (3, "S1"): [(CS, 18, 0)],
+            (3, "SA"): [(CS, 18, 0)],
             (3, "V1"): [(CV, 18, 1)],
             (3, "P2"): [(T, 19), (M, W_A, 1, 0), (M, W_A, 1, 1)],
-            (3, "V2"): [(Q, 17), (Q, 18)],
+            (3, "V2"): [(CV, 19, 1), (PV, W_A, 1, 1), (Q, 17), (Q, 18)],
             (3, "S2"): [(CS, 19, 0), (PS, W_A, 1, 0)],
-            (4, "V0"): [(CV, 19, 1), (PV, W_A, 1, 1)],
             (4, "V2"): [(Q, 19)],
             (4, "P2"): [(MS, W_U, 0, 0)],
             (5, "S0"): [(PS, W_U, 0, 0)],
@@ -573,6 +579,9 @@ def tile_gnn_s2_pa_t_kernel(
             if is_tile(t - VX_LAG):
                 load_vx(t - VX_LAG + VX_BUFS)
             normalise(t - 2)
+            if 0 < t < 4:
+                copy_transposed(t + 2)
+            extra(t, "SA")
             tanh_half(t - 3)
             sum_exp(t - 4)
             edge_average(t - 1)
@@ -583,6 +592,7 @@ def tile_gnn_s2_pa_t_kernel(
             extra(t, "V1")
             if t > 0:
                 empty_bank(t, 0)
+            if t >= 4:
                 copy_transposed(t + 2)
             edge_variance(t - 1)
             if t < TILES - 1:
@@ -617,7 +627,7 @@ def tile_gnn_s2_pa_t_kernel(
             load_piece(k)
             if k == 3:
                 load_edges(0, 0, 1)
-            if k == 7:
+            if k == 9:
                 load_edges(0, 1, 4)
         params_rows = resident.tile([P, 96], BF16, name="params_rows")
         nc.vector.memset(params_rows[:], 0.0)
@@ -635,26 +645,35 @@ def tile_gnn_s2_pa_t_kernel(
             bank = psum.tile([P, BANK], F32, name="bank", tag=tag, bufs=bufs)
             return bank
 
+        def keep_clock_up(times):
+            for i in range(times):
+                idle = psum.tile([P, BANK], F32, name="idle", tag="transposed", bufs=1)
+                nc.tensor.matmul(idle[:], lhsT=warm[:, :P], rhs=warm[:], start=True, stop=True)
+
+        keep_clock_up(6)
+
         x_grouped = []
         for h in range(2):
             x_bank = next_bank()
             transpose_words(x_bank[:], x_rows[:].bitcast(F32)[:, h, :])
-            grouped = resident.tile([P, C], BF16, name="x_grouped%d" % h, align_bytes=64)
+            grouped = work.tile(
+                [P, C], BF16, name="e_grouped", tag="e_grouped", bufs=E_GROUPED_BUFS, align_bytes=64
+            )
             copy_on(
                 h == 1, grouped[:].bitcast(F32).rearrange("p (g r u) -> p g r u", g=2, u=2), grouped_read(x_bank[:])
             )
             x_grouped.append(grouped)
+        keep_clock_up(2)
         for h in range(2):
             nc.vector.quantize_mx(
                 out=x_codes[:, h, :].bitcast(FP8X4), scales=x_scales[:, h, :], in_=x_grouped[h][:]
             )
 
-        def quadruple_scales():
-            for i in range(4):
-                nc.vector.tensor_copy(
-                    out=x_scales4[:].rearrange("p (n i) -> p n i", i=4)[:, :, i],
-                    in_=x_scales[:].rearrange("p h w -> p (h w)"),
-                )
+        def quadruple_scales(i):
+            nc.vector.tensor_copy(
+                out=x_scales4[:].rearrange("p (n i) -> p n i", i=4)[:, :, i],
+                in_=x_scales[:].rearrange("p h w -> p (h w)"),
+            )
 
         def repeat_x(q):
             def repeated(words, times):
@@ -674,26 +693,19 @@ def tile_gnn_s2_pa_t_kernel(
                 in_=repeated(x_scales4[:].bitcast(I32), 2),
             )
 
-        def keep_clock_up(times):
-            for i in range(times):
-                idle = psum.tile([P, BANK], F32, name="idle", tag="transposed", bufs=1)
-                nc.tensor.matmul(idle[:], lhsT=x_grouped[0][:, :P], rhs=x_grouped[0][:, BANK:], start=True, stop=True)
-
         for k in range(12):
-            if k in (8, 9):
+            transpose_piece(k, next_bank if k < 8 else free_bank)
+            keep_clock_up([2,2,2,2,2,2,2,2,0,1,1,1][k])
+            copy_piece(k, k in [3,7,9,11])
+            if k > 0:
                 quantise_piece(k - 1)
+            if 1 <= k <= 4:
+                quadruple_scales(k - 1)
+            if k == 5:
+                repeat_x(0)
+            if k in (8, 9):
                 fill_bank(0, k - 8)
                 repeat_x(k - 7)
-                if k == 8:
-                    repeat_x(3)
-            transpose_piece(k, next_bank if k < 8 else free_bank)
-            keep_clock_up({9: 1, 10: 1, 11: 1}.get(k, 0))
-            if k == 0:
-                quadruple_scales()
-                repeat_x(0)
-            elif k not in (8, 9):
-                quantise_piece(k - 1)
-            copy_piece(k, k >= 8 or k % 2 == 1)
             if k == 5:
                 load_edges(1, 0, 2)
             if k == 4:
@@ -705,10 +717,14 @@ def tile_gnn_s2_pa_t_kernel(
                 transpose_edges(1)
                 copy_transposed(1)
             if k == 10:
+                scale_parameters()
                 bank = product_half(W_A, 0, 0, free_bank())
                 nc.scalar.copy(out=ax[0][:, halves[0]], in_=bank[:])
+                repeat_x(3)
         transpose_edges(2)
+        params_ps = spread_parameters()
         quantise_piece(11)
+        nc.vector.tensor_copy(out=params[:], in_=params_ps[:])
         empty_bank(0, 0)
         transpose_piece(12, free_bank)
         bank = product_half(W_A, 0, 1, free_bank())

@@ -583,7 +583,6 @@ def tile_gnn_s2_pa_t_kernel(
                 copy_transposed(t + 2)
             extra(t, "SA")
             tanh_half(t - 3)
-            sum_exp(t - 4)
             edge_average(t - 1)
             if t == NODES + VX_LAG:
                 for n in range(2):
@@ -603,13 +602,14 @@ def tile_gnn_s2_pa_t_kernel(
                 scale_and_bias_on_scalar(t - 1)
                 half_squares(t, 0)
             extra(t, "S1")
-            if t == NODES + 3:
-                for n in range(2):
-                    copy_on(False, sum_exp0[:, halves[n]], sums_ps[("exp", 0, n)][:])
             if t > 0:
                 fill_bank(t, 1)
             if t < TILES - 1:
                 exp_half(t - 3)
+            sum_exp(t - 4)
+            if t == NODES + 3:
+                for n in range(2):
+                    copy_on(False, sum_exp0[:, halves[n]], sums_ps[("exp", 0, n)][:])
             sum_ev(t - VX_LAG)
             if t > 0:
                 transpose_edges(t + 3)

@@ -206,25 +206,15 @@ def tile_gnn_s2_pa_t_kernel(
             nc.gpsimd.tensor_tensor(out=mo[:, 2:3], in0=mo[:, 2:3], in1=minus_half[:], op=ALU.pow)
 
         def minus_mean_times_gain(t):
-            mo = moments[t]
-            nc.scalar.activation(out=mo[:, 3:4], in_=mo[:, 0:1], func=ACT.Identity, scale=params[:, t:t + 1])
-
-        def scale_and_bias_on_scalar(t):
-            scale_bias[t] = columns.tile([P, 2], F32, name="scale_bias", tag="scale_bias")
-            sb, mo = scale_bias[t], moments[t]
-            nc.scalar.activation(out=sb[:, 0:1], in_=mo[:, 2:3], func=ACT.Identity, scale=params[:, t:t + 1])
             nc.scalar.activation(
-                out=sb[:, 1:2], in_=mo[:, 2:3], func=ACT.Identity, scale=mo[:, 3:4], bias=params[:, 32 + t:33 + t]
+                out=gain_pairs[:, t, 1:2], in_=moments[t][:, 0:1], func=ACT.Identity, scale=params[:, t:t + 1]
             )
 
-        def scale_and_bias(key, gain, offset):
-            scale_bias[key] = columns.tile([P, 2], F32, name="scale_bias", tag="scale_bias")
-            rstd = columns.tile([P, 1], F32, name="rstd", tag="rstd")
-            sb, mo = scale_bias[key], moments[key]
-            nc.gpsimd.tensor_tensor(out=rstd[:], in0=mo[:, 2:3], in1=minus_half[:], op=ALU.pow)
-            nc.gpsimd.tensor_tensor(out=sb[:, 0:1], in0=rstd[:], in1=gain, op=ALU.mult)
-            nc.gpsimd.tensor_scalar(
-                out=sb[:, 1:2], in0=sb[:, 0:1], scalar1=mo[:, 0:1], scalar2=offset, op0=ALU.mult, op1=ALU.add
+        def scale_and_bias(t):
+            scale_bias[t] = columns.tile([P, 2], F32, name="scale_bias", tag="scale_bias")
+            nc.vector.scalar_tensor_tensor(
+                out=scale_bias[t][:], in0=gain_pairs[:, t, :], scalar=moments[t][:, 2:3], in1=offset_pairs[:, t, :],
+                op0=ALU.mult, op1=ALU.add,
             )
 
         def apply_norm(key, dst, src):
@@ -334,9 +324,14 @@ def tile_gnn_s2_pa_t_kernel(
             if is_tile(t):
                 variance(t)
 
+        def edge_inverse_deviation(t):
+            if is_tile(t):
+                minus_mean_times_gain(t)
+                inverse_deviation(t)
+
         def edge_scale_and_bias(t):
             if is_tile(t):
-                scale_and_bias(t, params[:, t:t + 1], params[:, 32 + t:33 + t])
+                scale_and_bias(t)
 
         def normalise(t, parts=whole):
             if is_tile(t):
@@ -491,6 +486,10 @@ def tile_gnn_s2_pa_t_kernel(
             nc.tensor.matmul(params_ps[:], lhsT=average[:], rhs=params_scaled[:], start=True, stop=True)
             return params_ps
 
+        gain_pairs = resident.tile([P, TILES, 2], F32, name="gain_pairs")
+        offset_pairs = resident.tile([P, TILES, 2], F32, name="offset_pairs")
+        nc.vector.memset(offset_pairs[:], 0.0)
+
         products = {}
         vx_rows = {}
 
@@ -575,6 +574,7 @@ def tile_gnn_s2_pa_t_kernel(
             if t > 0:
                 fill_bank(t, 0)
             extra(t, "P1")
+            edge_scale_and_bias(t - 2)
             times_vx(t - VX_LAG)
             if is_tile(t - VX_LAG):
                 load_vx(t - VX_LAG + VX_BUFS)
@@ -594,12 +594,8 @@ def tile_gnn_s2_pa_t_kernel(
             if t >= 4:
                 copy_transposed(t + 2)
             edge_variance(t - 1)
-            if t < TILES - 1:
-                edge_scale_and_bias(t - 1)
-            else:
-                minus_mean_times_gain(t - 1)
-                inverse_deviation(t - 1)
-                scale_and_bias_on_scalar(t - 1)
+            edge_inverse_deviation(t - 1)
+            if t == TILES - 1:
                 half_squares(t, 0)
             extra(t, "S1")
             if t > 0:
@@ -725,6 +721,8 @@ def tile_gnn_s2_pa_t_kernel(
         params_ps = spread_parameters()
         quantise_piece(11)
         nc.vector.tensor_copy(out=params[:], in_=params_ps[:])
+        nc.vector.tensor_copy(out=gain_pairs[:, :, 0], in_=params_ps[:, 0:32])
+        nc.vector.tensor_copy(out=offset_pairs[:, :, 1], in_=params_ps[:, 32:64])
         empty_bank(0, 0)
         transpose_piece(12, free_bank)
         bank = product_half(W_A, 0, 1, free_bank())
@@ -752,6 +750,7 @@ def tile_gnn_s2_pa_t_kernel(
         edge_average(last)
         sum_exp(last - 3)
         finish_edge_new(last - 2)
+        scale_and_bias(last - 1)
         normalise(last - 1)
         times_vx(last - 3)
         sum_ev(last - 3)
@@ -762,12 +761,12 @@ def tile_gnn_s2_pa_t_kernel(
         minus_mean_times_gain(last)
         inverse_deviation(last)
         exp_of(last - 2, halves[1])
-        scale_and_bias_on_scalar(last)
         finish_edge_new(last - 1, halves)
         sum_exp(last - 2)
         keep_clock_up(4)
         tanh_half(last - 1, halves)
         exp_half(last - 1, halves)
+        scale_and_bias(last)
         normalise(last, halves)
         times_vx(last - 2)
         finish_edge_new(last, halves)

@@ -135,7 +135,7 @@ def tile_gnn_s2_pa_t_kernel(
                 w_rows[k] = staging.tile([P, 2, C], BF16, name="w_rows", tag="w_rows", bufs=W_ROWS_BUFS)
             nc.sync.dma_start(
                 out=w_rows[k][:],
-                in_=weights[w][part * PIECE:(part + 1) * PIECE, :].rearrange("(a p) k -> p a k", p=P),
+                in_=weights[w][part * PIECE:(part + 1) * PIECE, :].rearrange("(p a) k -> p a k", a=2),
             )
 
         def copy_on(vector, out, in_):
@@ -148,20 +148,26 @@ def tile_gnn_s2_pa_t_kernel(
 
         def transpose_piece(k, next_bank):
             piece_banks[k] = []
-            for a in range(2):
+            for g in range(2):
                 bank = next_bank()
-                transpose_words(bank[:], w_rows[k][:].bitcast(F32)[:, a, :])
+                for a in range(2):
+                    words = w_rows[k][:].bitcast(F32)[:, a, g * WORDS:(g + 1) * WORDS]
+                    for u in range(2):
+                        slot = 2 * a + u
+                        nc.tensor.transpose(
+                            bank[:, slot * P:(slot + 1) * P], words[:, u * P:(u + 1) * P], ident[:]
+                        )
                 piece_banks[k].append(bank)
             if k in LOAD_BEHIND:
                 load_piece(LOAD_BEHIND[k])
 
-        def copy_half(k, a, vector):
+        def copy_half(k, g, vector):
             if k not in w_grouped:
                 w_grouped[k] = staging.tile(
                     [P, 2048], BF16, name="w_grouped", tag="w_grouped", bufs=W_GROUPED_BUFS, align_bytes=64
                 )
-            dst = w_grouped[k][:].bitcast(F32).rearrange("p (g c u) -> p g c u", g=2, u=2)
-            copy_on(vector, dst[:, :, a * P:(a + 1) * P, :], grouped_read(piece_banks[k][a][:]))
+            dst = w_grouped[k][:].bitcast(F32).rearrange("p (g r a u) -> p g r a u", g=2, a=2, u=2)
+            copy_on(vector, dst[:, g, :, :, :], piece_banks[k][g][:].rearrange("p (a u r) -> p r a u", a=2, u=2))
 
         def copy_piece(k, vector):
             copy_half(k, 0, False)
@@ -468,6 +474,14 @@ def tile_gnn_s2_pa_t_kernel(
             bank = psum.tile([P, BANK], F32, name="free_bank", tag=tag, bufs=1)
             return bank
 
+        def m_bank():
+            bank = psum.tile([P, BANK], F32, name="m_bank", tag="m", bufs=2)
+            return bank
+
+        def transposed_bank():
+            bank = psum.tile([P, BANK], F32, name="transposed_bank", tag="transposed", bufs=1)
+            return bank
+
         def stats_bank():
             bank = psum.tile([P, BANK], F32, name="stats_bank", tag="stats", bufs=1)
             return bank
@@ -503,8 +517,6 @@ def tile_gnn_s2_pa_t_kernel(
             copy_on(vector, dst[:, halves[n]], products[(w, h, n)][:])
             if w == W_V and n == 1:
                 nc.sync.dma_start(out=x_new_view[:, h, :], in_=vx_rows[h][:])
-
-        REPEATS = {0: 4, 5: 5, 6: 6, 7: 7}
 
         def T(*ks):
             for k in ks:
@@ -550,14 +562,6 @@ def tile_gnn_s2_pa_t_kernel(
             (3, "V2"): [(CV, 19, 1), (PV, W_A, 1, 1), (Q, 17), (Q, 18)],
             (3, "S2"): [(CS, 19, 0), (PS, W_A, 1, 0)],
             (4, "V2"): [(Q, 19)],
-            (4, "P2"): [(MS, W_U, 0, 0)],
-            (5, "S0"): [(PS, W_U, 0, 0)],
-            (5, "P2"): [(MS, W_U, 0, 1)],
-            (6, "S0"): [(PS, W_U, 0, 1)],
-            (6, "P2"): [(MS, W_U, 1, 0)],
-            (7, "S0"): [(PS, W_U, 1, 0)],
-            (7, "P2"): [(MS, W_U, 1, 1)],
-            (8, "S0"): [(PS, W_U, 1, 1)],
         }
 
         def extra(t, slot):
@@ -624,7 +628,7 @@ def tile_gnn_s2_pa_t_kernel(
             if k == 3:
                 load_edges(0, 0, 1)
             if k == 9:
-                load_edges(0, 1, 4)
+                load_edges(0, 1, 2)
         params_rows = resident.tile([P, 96], BF16, name="params_rows")
         nc.vector.memset(params_rows[:], 0.0)
         nc.sync.dma_start(out=params_rows[0:8, 0:32], in_=bne_w.rearrange("(l x) -> l x", l=8))
@@ -690,6 +694,10 @@ def tile_gnn_s2_pa_t_kernel(
             )
 
         for k in range(12):
+            if k == 1:
+                load_edges(0, 2, 4)
+            if k == 4:
+                load_edges(1, 0, 2)
             transpose_piece(k, next_bank if k < 8 else free_bank)
             keep_clock_up([2,2,2,2,2,2,2,2,0,1,1,1][k])
             copy_piece(k, k in [3,7,9,11])
@@ -697,13 +705,12 @@ def tile_gnn_s2_pa_t_kernel(
                 quantise_piece(k - 1)
             if 1 <= k <= 4:
                 quadruple_scales(k - 1)
-            if k == 5:
-                repeat_x(0)
+            if k >= 5:
+                repeat_x(k - 5)
+            if k == 11:
+                repeat_x(7)
             if k in (8, 9):
                 fill_bank(0, k - 8)
-                repeat_x(k - 7)
-            if k == 5:
-                load_edges(1, 0, 2)
             if k == 4:
                 transpose_edges(0)
                 copy_transposed(0)
@@ -716,7 +723,6 @@ def tile_gnn_s2_pa_t_kernel(
                 scale_parameters()
                 bank = product_half(W_A, 0, 0, free_bank())
                 nc.scalar.copy(out=ax[0][:, halves[0]], in_=bank[:])
-                repeat_x(3)
         transpose_edges(2)
         params_ps = spread_parameters()
         quantise_piece(11)
@@ -735,8 +741,6 @@ def tile_gnn_s2_pa_t_kernel(
 
         for t in range(TILES):
             period(t)
-            if t in REPEATS:
-                repeat_x(REPEATS[t])
             if t == 1:
                 load_edges(2, 0, 4)
             if t == 2:
@@ -754,34 +758,35 @@ def tile_gnn_s2_pa_t_kernel(
         normalise(last - 1)
         times_vx(last - 3)
         sum_ev(last - 3)
-        tanh_half(last - 2)
         edge_moments(last)
-        exp_of(last - 2, halves[0])
+        tanh_half(last - 2)
         edge_variance(last)
-        minus_mean_times_gain(last)
-        inverse_deviation(last)
-        exp_of(last - 2, halves[1])
+        edge_inverse_deviation(last)
+        exp_half(last - 2)
         finish_edge_new(last - 1, halves)
         sum_exp(last - 2)
-        keep_clock_up(4)
+        multiply_x(W_U, 1, 0, m_bank)
+        multiply_x(W_U, 1, 1, m_bank)
+        multiply_x(W_U, 0, 0, transposed_bank)
+        multiply_x(W_U, 0, 1, stats_bank)
         tanh_half(last - 1, halves)
         exp_half(last - 1, halves)
         scale_and_bias(last)
         normalise(last, halves)
-        times_vx(last - 2)
         finish_edge_new(last, halves)
-        sum_ev(last - 2)
-        keep_clock_up(1)
         sum_exp(last - 1)
-        keep_clock_up(1)
+        times_vx(last - 2)
+        sum_ev(last - 2)
         tanh_half(last, halves)
         times_vx(last - 1)
         exp_half(last, halves)
-        sum_ev(last - 1)
         sum_exp(last)
+        sum_ev(last - 1)
         times_vx(last, halves)
         sum_ev(last)
-        keep_clock_up(6)
+        for h in (1, 0):
+            for n in range(2):
+                copy_product(W_U, h, n, True)
 
         inverse[0], inverse[1] = sum_exp0, new_edge_new()
         for h in (1, 0):

@@ -38,6 +38,7 @@ EDGE_NEW_BUFS = 6
 EXP_BUFS = 3
 EV_BUFS = 3
 VX_BUFS = 4
+NORM_SHARE = 128
 VX_LAG = 4
 
 
@@ -344,6 +345,14 @@ def tile_gnn_s2_pa_t_kernel(
                 for cols in parts:
                     apply_norm(t, edge_new[t][:, cols], edge_new[t][:, cols])
 
+        def normalise_on_scalar(t):
+            if is_tile(t):
+                cols, sb = slice(C - NORM_SHARE, C), scale_bias[t]
+                nc.scalar.activation(
+                    out=edge_new[t][:, cols], in_=edge_new[t][:, cols], func=ACT.Identity,
+                    scale=sb[:, 0:1], bias=sb[:, 1:2],
+                )
+
         def finish_edge_new(t, parts=whole):
             if is_tile(t):
                 for cols in parts:
@@ -557,7 +566,7 @@ def tile_gnn_s2_pa_t_kernel(
             (2, "V2"): [(PV, W_V, 0, 1), (PV, W_V, 1, 1), (CV, 16, 1), (CV, 17, 1), (Q, 16)],
             (3, "P1"): [(T, 18)],
             (3, "SA"): [(CS, 18, 0)],
-            (3, "V1"): [(CV, 18, 1)],
+            (3, "S1"): [(CS, 18, 1)],
             (3, "P2"): [(T, 19), (M, W_A, 1, 0), (M, W_A, 1, 1)],
             (3, "V2"): [(CV, 19, 1), (PV, W_A, 1, 1), (Q, 17), (Q, 18)],
             (3, "S2"): [(CS, 19, 0), (PS, W_A, 1, 0)],
@@ -582,7 +591,7 @@ def tile_gnn_s2_pa_t_kernel(
             times_vx(t - VX_LAG)
             if is_tile(t - VX_LAG):
                 load_vx(t - VX_LAG + VX_BUFS)
-            normalise(t - 2)
+            normalise(t - 2, [slice(0, C - NORM_SHARE)])
             if 0 < t < 4:
                 copy_transposed(t + 2)
             extra(t, "SA")
@@ -599,6 +608,7 @@ def tile_gnn_s2_pa_t_kernel(
                 copy_transposed(t + 2)
             edge_variance(t - 1)
             edge_inverse_deviation(t - 1)
+            normalise_on_scalar(t - 2)
             if t == TILES - 1:
                 half_squares(t, 0)
             extra(t, "S1")
@@ -705,9 +715,12 @@ def tile_gnn_s2_pa_t_kernel(
                 quantise_piece(k - 1)
             if 1 <= k <= 4:
                 quadruple_scales(k - 1)
-            if k >= 5:
-                repeat_x(k - 5)
-            if k == 11:
+            if k == 5:
+                repeat_x(0)
+            if 6 <= k <= 8:
+                repeat_x(2 * k - 11)
+                repeat_x(2 * k - 10)
+            if k == 9:
                 repeat_x(7)
             if k in (8, 9):
                 fill_bank(0, k - 8)

@@ -84,14 +84,14 @@ def tile_gnn_s2_pa_t_kernel(
         first_tanh = resident.tile([P, 1], F32, name="first_tanh")
         nc.scalar.activation(out=first_tanh[:], in_=minus_half[:], func=ACT.Tanh)
 
-        w_codes = [resident.tile([P, 2, C], U32, name="w_codes%d" % w, align_bytes=64) for w in range(5)]
-        w_scales = [resident.tile([P, 2, C], U8, name="w_scales%d" % w, align_bytes=64) for w in range(5)]
-        x_codes = resident.tile([P, 2, WORDS], U32, name="x_codes", align_bytes=64)
-        x_scales = resident.tile([P, 2, WORDS], U8, name="x_scales", align_bytes=64)
+        w_codes = [resident.tile([P, 2, C], U32, name="w_codes%d" % w, align_bytes=256) for w in range(5)]
+        w_scales = [resident.tile([P, 2, C], U8, name="w_scales%d" % w, align_bytes=256) for w in range(5)]
+        x_codes = resident.tile([P, 2, WORDS], U32, name="x_codes", align_bytes=256)
+        x_scales = resident.tile([P, 2, WORDS], U8, name="x_scales", align_bytes=256)
         x_scales4 = resident.tile([P, 8 * WORDS], U8, name="x_scales4", align_bytes=64)
         nc.vector.memset(x_scales[:].rearrange("p h w -> p (h w)").bitcast(I32), 0)
-        xj_codes = resident.tile([P, NODES, WORDS], U32, name="xj_codes", align_bytes=64)
-        xj_scales = resident.tile([P, NODES, WORDS], U8, name="xj_scales", align_bytes=64)
+        xj_codes = resident.tile([P, NODES, WORDS], U32, name="xj_codes", align_bytes=256)
+        xj_scales = resident.tile([P, NODES, WORDS], U8, name="xj_scales", align_bytes=256)
         ax = [resident.tile([P, C], F32, name="ax%d" % h) for h in range(2)]
         sum_exp0 = resident.tile([P, C], F32, name="sum_exp0")
         sum_ev0 = resident.tile([P, C], F32, name="sum_ev0")
@@ -271,10 +271,10 @@ def tile_gnn_s2_pa_t_kernel(
         def quantise_edges(t):
             if is_tile(t):
                 e_codes[t] = work.tile(
-                    [P, WORDS], U32, name="e_codes", tag="e_codes", bufs=E_CODES_BUFS, align_bytes=64
+                    [P, WORDS], U32, name="e_codes", tag="e_codes", bufs=E_CODES_BUFS, align_bytes=256
                 )
                 e_scales[t] = work.tile(
-                    [P, WORDS], U8, name="e_scales", tag="e_scales", bufs=E_CODES_BUFS, align_bytes=64
+                    [P, WORDS], U8, name="e_scales", tag="e_scales", bufs=E_CODES_BUFS, align_bytes=256
                 )
                 nc.vector.quantize_mx(out=e_codes[t][:].bitcast(FP8X4), scales=e_scales[t][:], in_=e_grouped[t][:])
 
@@ -660,8 +660,6 @@ def tile_gnn_s2_pa_t_kernel(
                 idle = psum.tile([P, BANK], F32, name="idle", tag="transposed", bufs=1)
                 nc.tensor.matmul(idle[:], lhsT=warm[:, :P], rhs=warm[:], start=True, stop=True)
 
-        keep_clock_up(6)
-
         x_grouped = []
         for h in range(2):
             x_bank = next_bank()
@@ -673,7 +671,6 @@ def tile_gnn_s2_pa_t_kernel(
                 h == 1, grouped[:].bitcast(F32).rearrange("p (g r u) -> p g r u", g=2, u=2), grouped_read(x_bank[:])
             )
             x_grouped.append(grouped)
-        keep_clock_up(2)
         for h in range(2):
             nc.vector.quantize_mx(
                 out=x_codes[:, h, :].bitcast(FP8X4), scales=x_scales[:, h, :], in_=x_grouped[h][:]
@@ -709,7 +706,6 @@ def tile_gnn_s2_pa_t_kernel(
             if k == 4:
                 load_edges(1, 0, 2)
             transpose_piece(k, next_bank if k < 8 else free_bank)
-            keep_clock_up([2,2,2,2,2,2,2,2,0,1,1,1][k])
             copy_piece(k, k in [3,7,9,11])
             if k > 0:
                 quantise_piece(k - 1)
@@ -765,7 +761,9 @@ def tile_gnn_s2_pa_t_kernel(
         last = TILES - 1
         add_half_sums(last)
         edge_average(last)
+        multiply_x(W_U, 1, 0, m_bank)
         sum_exp(last - 3)
+        multiply_x(W_U, 1, 1, m_bank)
         finish_edge_new(last - 2)
         scale_and_bias(last - 1)
         normalise(last - 1)
@@ -778,12 +776,11 @@ def tile_gnn_s2_pa_t_kernel(
         exp_half(last - 2)
         finish_edge_new(last - 1, halves)
         sum_exp(last - 2)
-        multiply_x(W_U, 1, 0, m_bank)
-        multiply_x(W_U, 1, 1, m_bank)
         multiply_x(W_U, 0, 0, transposed_bank)
         multiply_x(W_U, 0, 1, stats_bank)
         tanh_half(last - 1, halves)
         exp_half(last - 1, halves)
+        copy_product(W_U, 1, 0, True)
         scale_and_bias(last)
         normalise(last, halves)
         finish_edge_new(last, halves)
@@ -797,9 +794,9 @@ def tile_gnn_s2_pa_t_kernel(
         sum_ev(last - 1)
         times_vx(last, halves)
         sum_ev(last)
-        for h in (1, 0):
-            for n in range(2):
-                copy_product(W_U, h, n, True)
+        copy_product(W_U, 1, 1, True)
+        for n in range(2):
+            copy_product(W_U, 0, n, True)
 
         inverse[0], inverse[1] = sum_exp0, new_edge_new()
         for h in (1, 0):

@@ -596,6 +596,8 @@ def tile_gnn_s2_pa_t_kernel(
                 copy_transposed(t + 2)
             extra(t, "SA")
             tanh_half(t - 3)
+            if t > 0:
+                fill_bank(t, 1)
             edge_average(t - 1)
             if t == NODES + VX_LAG:
                 for n in range(2):
@@ -612,8 +614,6 @@ def tile_gnn_s2_pa_t_kernel(
             if t == TILES - 1:
                 half_squares(t, 0)
             extra(t, "S1")
-            if t > 0:
-                fill_bank(t, 1)
             if t < TILES - 1:
                 exp_half(t - 3)
             sum_exp(t - 4)

@@ -17,10 +17,12 @@ P = 128
 C = 1024
 BANK = 512
 NODES = 16
+BATCH = 16
 TILES = 32
+QUAD = 4
 WORDS = 256
 EPS = 1e-5
-SAMPLES = 16 * C
+SAMPLES = BATCH * C
 FLOPS = 2 * (4096 + 4 * 256) * C * C
 
 W_E, W_B, W_A, W_V, W_U = 0, 1, 2, 3, 4
@@ -28,8 +30,6 @@ PIECE = 256
 NODE_KEY = 100
 
 W_ROWS_BUFS = 4
-EARLY_PIECES = 11
-LOAD_BEHIND = {0: 11, 1: 12, 2: 13, 3: 14, 4: 15, 5: 16, 6: 17, 7: 18, 8: 19}
 W_GROUPED_BUFS = 4
 E_GROUPED_BUFS = 2
 E_CODES_BUFS = 4
@@ -38,8 +38,14 @@ EDGE_NEW_BUFS = 6
 EXP_BUFS = 3
 EV_BUFS = 3
 VX_BUFS = 4
-NORM_SHARE = 128
+SUMS_BUFS = 8
+EARLY_PIECES = W_ROWS_BUFS + VX_BUFS + EXP_BUFS
+PIECES = 20
 VX_LAG = 4
+NORM_SHARE = 128
+FREE_BANK_TILES = 4
+VECTOR_COPIES = (3, 7, 9, 11)
+EDGE_GAINS, EDGE_OFFSETS, NODE_GAINS, NODE_OFFSETS, PARAMS = 0, 32, 64, 80, 96
 
 
 def tile_gnn_s2_pa_t_kernel(
@@ -63,8 +69,6 @@ def tile_gnn_s2_pa_t_kernel(
         sum_tags = {"exp": ("sum_exp0", "sum_exp1"), "ev": ("sum_ev0", "sum_ev1")}
         ctx.enter_context(tc.manual_schedule())
 
-        warm = resident.tile([P, BANK], BF16, name="warm")
-        nc.vector.memset(warm[:], 0.0)
         ident = resident.tile([P, P], F32, name="ident")
         make_identity(nc, ident[:])
         same_l = resident.tile([P, 8], F32, name="same_l")
@@ -96,7 +100,7 @@ def tile_gnn_s2_pa_t_kernel(
         sum_exp0 = resident.tile([P, C], F32, name="sum_exp0")
         sum_ev0 = resident.tile([P, C], F32, name="sum_ev0")
         ux = [resident.tile([P, C], F32, name="ux%d" % h) for h in range(2)]
-        row_sums = resident.tile([P, 8, 8], F32, name="row_sums")
+        row_sums = resident.tile([P, SUMS_BUFS, 8], F32, name="row_sums")
 
         def transpose_words(bank, rows_as_words):
             for k in range(4):
@@ -128,12 +132,13 @@ def tile_gnn_s2_pa_t_kernel(
 
         def load_piece(k):
             w, part = k // 4, k % 4
-            if 4 <= k < 8 or 15 <= k < 19:
-                w_rows[k] = work.tile([P, 2, C], BF16, name="w_rows", tag="vx", bufs=VX_BUFS)
-            elif 8 <= k < EARLY_PIECES or k == 19:
-                w_rows[k] = work.tile([P, 2, C], BF16, name="w_rows", tag="exps", bufs=EXP_BUFS)
-            else:
+            turn = k % EARLY_PIECES
+            if turn < W_ROWS_BUFS:
                 w_rows[k] = staging.tile([P, 2, C], BF16, name="w_rows", tag="w_rows", bufs=W_ROWS_BUFS)
+            elif turn < W_ROWS_BUFS + VX_BUFS:
+                w_rows[k] = work.tile([P, 2, C], BF16, name="w_rows", tag="vx", bufs=VX_BUFS)
+            else:
+                w_rows[k] = work.tile([P, 2, C], BF16, name="w_rows", tag="exps", bufs=EXP_BUFS)
             nc.sync.dma_start(
                 out=w_rows[k][:],
                 in_=weights[w][part * PIECE:(part + 1) * PIECE, :].rearrange("(p a) k -> p a k", a=2),
@@ -159,8 +164,8 @@ def tile_gnn_s2_pa_t_kernel(
                             bank[:, slot * P:(slot + 1) * P], words[:, u * P:(u + 1) * P], ident[:]
                         )
                 piece_banks[k].append(bank)
-            if k in LOAD_BEHIND:
-                load_piece(LOAD_BEHIND[k])
+            if k + EARLY_PIECES < PIECES:
+                load_piece(k + EARLY_PIECES)
 
         def copy_half(k, g, vector):
             if k not in w_grouped:
@@ -214,7 +219,8 @@ def tile_gnn_s2_pa_t_kernel(
 
         def minus_mean_times_gain(t):
             nc.scalar.activation(
-                out=gain_pairs[:, t, 1:2], in_=moments[t][:, 0:1], func=ACT.Identity, scale=params[:, t:t + 1]
+                out=gain_pairs[:, t, 1:2], in_=moments[t][:, 0:1], func=ACT.Identity,
+                scale=params[:, EDGE_GAINS + t:EDGE_GAINS + t + 1],
             )
 
         def scale_and_bias(t):
@@ -243,16 +249,16 @@ def tile_gnn_s2_pa_t_kernel(
 
         def load_edges(q, lo, hi):
             if lo == 0:
-                edge_rows[q] = staging.tile([P, 4, C], BF16, name="edge_rows", tag="edge_rows", bufs=EDGE_ROWS_BUFS)
-            h, j = q // 4, 4 * (q % 4)
+                edge_rows[q] = staging.tile([P, QUAD, C], BF16, name="edge_rows", tag="edge_rows", bufs=EDGE_ROWS_BUFS)
+            h, j = QUAD * q // NODES, QUAD * q % NODES
             nc.sync.dma_start(out=edge_rows[q][:, lo:hi, :], in_=edge_view[:, h, j + lo:j + hi, :])
 
         def edge_of(t):
-            return edge_rows[t // 4][:, t % 4, :]
+            return edge_rows[t // QUAD][:, t % QUAD, :]
 
         def transpose_edges(t):
             if is_tile(t):
-                if t < 4:
+                if t < FREE_BANK_TILES:
                     transposed[t] = (next_bank if t == 0 else free_bank)()[:]
                 else:
                     transposed[t] = psum.tile([P, BANK], F32, name="transposed", tag="transposed", bufs=1)
@@ -294,7 +300,7 @@ def tile_gnn_s2_pa_t_kernel(
                     edge_new[t] = work.tile([P, C], F32, name="edge_new", tag="edge_new", bufs=EDGE_NEW_BUFS)
                 nc.vector.scalar_tensor_tensor(
                     out=edge_new[t][:, halves[n]], in0=m_ps[(t, n)][:], scalar=1.0, in1=ax[t // NODES][:, halves[n]],
-                    op0=ALU.mult, op1=ALU.add, accum_out=row_sums[:, t % 8, n:n + 1],
+                    op0=ALU.mult, op1=ALU.add, accum_out=row_sums[:, t % SUMS_BUFS, n:n + 1],
                 )
 
         def sum_squares(src, cols, dst):
@@ -310,14 +316,14 @@ def tile_gnn_s2_pa_t_kernel(
             return [rs[:, n:n + 3:2] for n in range(2)]
 
         def half_squares(t, n):
-            sum_squares(edge_new[t][:, halves[n]], halves[n], row_sums[:, t % 8, 2 + n:3 + n])
+            sum_squares(edge_new[t][:, halves[n]], halves[n], row_sums[:, t % SUMS_BUFS, 2 + n:3 + n])
 
         def add_half_sums(t):
-            sums_of[t] = half_sums(row_sums[:, t % 8, :])
+            sums_of[t] = half_sums(row_sums[:, t % SUMS_BUFS, :])
 
         def edge_squares(t):
             if is_tile(t):
-                complete_row_sums(t, edge_new[t][:], row_sums[:, t % 8, :])
+                complete_row_sums(t, edge_new[t][:], row_sums[:, t % SUMS_BUFS, :])
 
         def edge_average(t):
             if is_tile(t):
@@ -340,7 +346,7 @@ def tile_gnn_s2_pa_t_kernel(
             if is_tile(t):
                 scale_and_bias(t)
 
-        def normalise(t, parts=whole):
+        def normalise(t, parts):
             if is_tile(t):
                 for cols in parts:
                     apply_norm(t, edge_new[t][:, cols], edge_new[t][:, cols])
@@ -365,13 +371,10 @@ def tile_gnn_s2_pa_t_kernel(
                 for cols in parts:
                     nc.scalar.activation(out=exps[t][:, cols], in_=edge_new[t][:, cols], func=ACT.Tanh, scale=0.5)
 
-        def exp_of(t, cols):
-            nc.scalar.activation(out=exps[t][:, cols], in_=exps[t][:, cols], func=ACT.Exp, scale=0.5)
-
         def exp_half(t, parts=whole):
             if is_tile(t):
                 for cols in parts:
-                    exp_of(t, cols)
+                    nc.scalar.activation(out=exps[t][:, cols], in_=exps[t][:, cols], func=ACT.Exp, scale=0.5)
 
         def new_ev():
             ev = work.tile([P, C], F32, name="evs", tag="evs", bufs=EV_BUFS, align_bytes=64)
@@ -455,7 +458,8 @@ def tile_gnn_s2_pa_t_kernel(
             sb, ps = scale_bias[key], means_ps[key]
             nc.scalar.activation(out=mo[:, 0:1], in_=ps[:, 0:1], func=ACT.Identity, scale=-1.0)
             nc.scalar.activation(out=mo[:, 1:2], in_=ps[:, 1:2], func=ACT.Identity, bias=eps[:])
-            gain, offset = params[:, 64 + h:65 + h], params[:, 80 + h:81 + h]
+            gain = params[:, NODE_GAINS + h:NODE_GAINS + h + 1]
+            offset = params[:, NODE_OFFSETS + h:NODE_OFFSETS + h + 1]
             nc.scalar.activation(out=mo[:, 3:4], in_=mo[:, 0:1], func=ACT.Identity, scale=gain)
             nc.scalar.activation(
                 out=mo[:, 2:3], in_=ps[:, 0:1], func=ACT.Abs_reciprocal_sqrt, scale=mo[:, 0:1], bias=mo[:, 1:2]
@@ -495,9 +499,8 @@ def tile_gnn_s2_pa_t_kernel(
             bank = psum.tile([P, BANK], F32, name="stats_bank", tag="stats", bufs=1)
             return bank
 
-        params = resident.tile([P, 96], F32, name="params")
-
-        params_scaled = resident.tile([P, 96], F32, name="params_scaled")
+        params = resident.tile([P, PARAMS], F32, name="params")
+        params_scaled = resident.tile([P, PARAMS], F32, name="params_scaled")
 
         def scale_parameters():
             nc.vector.tensor_scalar(
@@ -505,7 +508,7 @@ def tile_gnn_s2_pa_t_kernel(
             )
 
         def spread_parameters():
-            params_ps = psum.tile([P, 96], F32, name="params_ps", tag="stats", bufs=1)
+            params_ps = psum.tile([P, PARAMS], F32, name="params_ps", tag="stats", bufs=1)
             nc.tensor.matmul(params_ps[:], lhsT=average[:], rhs=params_scaled[:], start=True, stop=True)
             return params_ps
 
@@ -527,74 +530,72 @@ def tile_gnn_s2_pa_t_kernel(
             if w == W_V and n == 1:
                 nc.sync.dma_start(out=x_new_view[:, h, :], in_=vx_rows[h][:])
 
-        def T(*ks):
+        def transpose_pieces(*ks):
             for k in ks:
                 transpose_piece(k, free_bank)
 
-        def Q(*ks):
-            for k in ks:
-                quantise_piece(k)
+        def scalar_copy(k, g):
+            copy_half(k, g, False)
 
-        def CS(k, a):
-            copy_half(k, a, False)
+        def vector_copy(k, g):
+            copy_half(k, g, True)
 
-        def CV(k, a):
-            copy_half(k, a, True)
-
-        def M(w, h, n):
+        def multiply(w, h, n):
             multiply_x(w, h, n, free_bank)
 
-        def MS(w, h, n):
-            multiply_x(w, h, n, stats_bank)
-
-        def PS(w, h, n):
+        def scalar_out(w, h, n):
             copy_product(w, h, n, False)
 
-        def PV(w, h, n):
+        def vector_out(w, h, n):
             copy_product(w, h, n, True)
 
         EXTRA = {
-            (1, "P1"): [(T, 13), (transpose_edges, 3)],
-            (1, "S1"): [(CS, 13, 0)],
-            (1, "V1"): [(Q, 12), (CV, 13, 1)],
-            (1, "P2"): [(T, 14, 15)],
-            (1, "V2"): [(Q, 13)],
-            (2, "S0"): [(CS, 14, 0), (CS, 14, 1), (CS, 15, 0)],
-            (2, "V0"): [(CV, 15, 1), (Q, 14), (Q, 15)],
-            (2, "P2"): [(M, W_V, 0, 0), (M, W_V, 1, 0), (M, W_V, 0, 1), (M, W_V, 1, 1), (T, 16, 17)],
-            (2, "S2"): [(PS, W_V, 0, 0), (PS, W_V, 1, 0), (CS, 16, 0), (CS, 17, 0)],
-            (2, "V2"): [(PV, W_V, 0, 1), (PV, W_V, 1, 1), (CV, 16, 1), (CV, 17, 1), (Q, 16)],
-            (3, "P1"): [(T, 18)],
-            (3, "SA"): [(CS, 18, 0)],
-            (3, "S1"): [(CS, 18, 1)],
-            (3, "P2"): [(T, 19), (M, W_A, 1, 0), (M, W_A, 1, 1)],
-            (3, "V2"): [(CV, 19, 1), (PV, W_A, 1, 1), (Q, 17), (Q, 18)],
-            (3, "S2"): [(CS, 19, 0), (PS, W_A, 1, 0)],
-            (4, "V2"): [(Q, 19)],
+            (1, "half_filled"): [(transpose_pieces, 13), (transpose_edges, 3)],
+            (1, "moments"): [(quantise_piece, 12), (vector_copy, 13, 1)],
+            (1, "variance"): [(scalar_copy, 13, 0)],
+            (1, "period_end"): [(transpose_pieces, 14, 15), (quantise_piece, 13)],
+            (2, "period_start"): [(scalar_copy, 14, 0), (scalar_copy, 14, 1), (scalar_copy, 15, 0)],
+            (2, "quantised"): [(vector_copy, 15, 1), (quantise_piece, 14), (quantise_piece, 15)],
+            (2, "period_end"): [
+                (multiply, W_V, 0, 0), (multiply, W_V, 1, 0), (multiply, W_V, 0, 1), (multiply, W_V, 1, 1),
+                (transpose_pieces, 16, 17),
+                (scalar_out, W_V, 0, 0), (scalar_out, W_V, 1, 0), (scalar_copy, 16, 0), (scalar_copy, 17, 0),
+                (vector_out, W_V, 0, 1), (vector_out, W_V, 1, 1), (vector_copy, 16, 1), (vector_copy, 17, 1),
+                (quantise_piece, 16),
+            ],
+            (3, "half_filled"): [(transpose_pieces, 18)],
+            (3, "before_tanh"): [(scalar_copy, 18, 0)],
+            (3, "variance"): [(scalar_copy, 18, 1)],
+            (3, "period_end"): [
+                (transpose_pieces, 19), (multiply, W_A, 1, 0), (multiply, W_A, 1, 1),
+                (scalar_copy, 19, 0), (scalar_out, W_A, 1, 0),
+                (vector_copy, 19, 1), (vector_out, W_A, 1, 1), (quantise_piece, 17), (quantise_piece, 18),
+            ],
+            (4, "period_end"): [(quantise_piece, 19)],
         }
 
-        def extra(t, slot):
-            for f, *args in EXTRA.get((t, slot), ()):
+        def extra(t, place):
+            for f, *args in EXTRA.get((t, place), ()):
                 f(*args)
 
         def period(t):
             edge_squares(t - 1)
-            extra(t, "S0")
+            extra(t, "period_start")
             finish_edge_new(t - 3)
             if t > 0:
                 quantise_edges(t + 1)
-            extra(t, "V0")
+            extra(t, "quantised")
             if t > 0:
                 fill_bank(t, 0)
-            extra(t, "P1")
+            extra(t, "half_filled")
             edge_scale_and_bias(t - 2)
             times_vx(t - VX_LAG)
             if is_tile(t - VX_LAG):
                 load_vx(t - VX_LAG + VX_BUFS)
             normalise(t - 2, [slice(0, C - NORM_SHARE)])
-            if 0 < t < 4:
+            if 0 < t < FREE_BANK_TILES:
                 copy_transposed(t + 2)
-            extra(t, "SA")
+            extra(t, "before_tanh")
             tanh_half(t - 3)
             if t > 0:
                 fill_bank(t, 1)
@@ -602,24 +603,24 @@ def tile_gnn_s2_pa_t_kernel(
             if t == NODES + VX_LAG:
                 for n in range(2):
                     copy_on(n == 1, sum_ev0[:, halves[n]], sums_ps[("ev", 0, n)][:])
+            normalise_on_scalar(t - 2)
             edge_moments(t - 1)
-            extra(t, "V1")
+            extra(t, "moments")
             if t > 0:
                 empty_bank(t, 0)
-            if t >= 4:
+            if t >= FREE_BANK_TILES:
                 copy_transposed(t + 2)
             edge_variance(t - 1)
             edge_inverse_deviation(t - 1)
-            normalise_on_scalar(t - 2)
             if t == TILES - 1:
                 half_squares(t, 0)
-            extra(t, "S1")
+            extra(t, "variance")
             if t < TILES - 1:
                 exp_half(t - 3)
             sum_exp(t - 4)
             if t == NODES + 3:
                 for n in range(2):
-                    copy_on(False, sum_exp0[:, halves[n]], sums_ps[("exp", 0, n)][:])
+                    copy_on(n == 1, sum_exp0[:, halves[n]], sums_ps[("exp", 0, n)][:])
             sum_ev(t - VX_LAG)
             if t > 0:
                 transpose_edges(t + 3)
@@ -627,9 +628,7 @@ def tile_gnn_s2_pa_t_kernel(
             if t == TILES - 1:
                 half_squares(t, 1)
                 exp_half(t - 3)
-            extra(t, "P2")
-            extra(t, "S2")
-            extra(t, "V2")
+            extra(t, "period_end")
 
         x_rows = work.tile([P, 2, C], BF16, name="x_rows", tag="edge_new", bufs=EDGE_NEW_BUFS)
         nc.sync.dma_start(out=x_rows[:], in_=x_view)
@@ -639,12 +638,14 @@ def tile_gnn_s2_pa_t_kernel(
                 load_edges(0, 0, 1)
             if k == 9:
                 load_edges(0, 1, 2)
-        params_rows = resident.tile([P, 96], BF16, name="params_rows")
+        params_rows = resident.tile([P, PARAMS], BF16, name="params_rows")
         nc.vector.memset(params_rows[:], 0.0)
-        nc.sync.dma_start(out=params_rows[0:8, 0:32], in_=bne_w.rearrange("(l x) -> l x", l=8))
-        nc.sync.dma_start(out=params_rows[0:8, 32:64], in_=bne_b.rearrange("(l x) -> l x", l=8))
-        nc.sync.dma_start(out=params_rows[0:8, 64:66], in_=bnv_w.rearrange("(l x) -> l x", l=8))
-        nc.sync.dma_start(out=params_rows[0:8, 80:82], in_=bnv_b.rearrange("(l x) -> l x", l=8))
+        for vector, col, width in (
+            (bne_w, EDGE_GAINS, TILES), (bne_b, EDGE_OFFSETS, TILES), (bnv_w, NODE_GAINS, 2), (bnv_b, NODE_OFFSETS, 2)
+        ):
+            nc.sync.dma_start(
+                out=params_rows[0:8, col:col + width], in_=vector.rearrange("(l x) -> l x", l=8)
+            )
 
         rotation = [("m", 2), ("m", 2)] + [(tag, 1) for tag in free_tags]
         banks_taken = [0]
@@ -654,11 +655,6 @@ def tile_gnn_s2_pa_t_kernel(
             banks_taken[0] += 1
             bank = psum.tile([P, BANK], F32, name="bank", tag=tag, bufs=bufs)
             return bank
-
-        def keep_clock_up(times):
-            for i in range(times):
-                idle = psum.tile([P, BANK], F32, name="idle", tag="transposed", bufs=1)
-                nc.tensor.matmul(idle[:], lhsT=warm[:, :P], rhs=warm[:], start=True, stop=True)
 
         x_grouped = []
         for h in range(2):
@@ -706,7 +702,7 @@ def tile_gnn_s2_pa_t_kernel(
             if k == 4:
                 load_edges(1, 0, 2)
             transpose_piece(k, next_bank if k < 8 else free_bank)
-            copy_piece(k, k in [3,7,9,11])
+            copy_piece(k, k in VECTOR_COPIES)
             if k > 0:
                 quantise_piece(k - 1)
             if 1 <= k <= 4:
@@ -736,8 +732,8 @@ def tile_gnn_s2_pa_t_kernel(
         params_ps = spread_parameters()
         quantise_piece(11)
         nc.vector.tensor_copy(out=params[:], in_=params_ps[:])
-        nc.vector.tensor_copy(out=gain_pairs[:, :, 0], in_=params_ps[:, 0:32])
-        nc.vector.tensor_copy(out=offset_pairs[:, :, 1], in_=params_ps[:, 32:64])
+        nc.vector.tensor_copy(out=gain_pairs[:, :, 0], in_=params_ps[:, EDGE_GAINS:EDGE_GAINS + TILES])
+        nc.vector.tensor_copy(out=offset_pairs[:, :, 1], in_=params_ps[:, EDGE_OFFSETS:EDGE_OFFSETS + TILES])
         empty_bank(0, 0)
         transpose_piece(12, free_bank)
         bank = product_half(W_A, 0, 1, free_bank())
@@ -746,17 +742,17 @@ def tile_gnn_s2_pa_t_kernel(
         copy_transposed(2)
         copy_piece(12, True)
         empty_bank(0, 1)
-        load_edges(1, 2, 4)
+        load_edges(1, 2, QUAD)
 
         for t in range(TILES):
             period(t)
             if t == 1:
-                load_edges(2, 0, 4)
+                load_edges(2, 0, QUAD)
             if t == 2:
                 for u in range(VX_BUFS):
                     load_vx(u)
-            if t % 4 == 2 and 6 <= t <= 22:
-                load_edges((t + 6) // 4, 0, 4)
+            if t % QUAD == 2 and 6 <= t <= TILES - 10:
+                load_edges((t + 6) // QUAD, 0, QUAD)
 
         last = TILES - 1
         add_half_sums(last)
@@ -766,7 +762,7 @@ def tile_gnn_s2_pa_t_kernel(
         multiply_x(W_U, 1, 1, m_bank)
         finish_edge_new(last - 2)
         scale_and_bias(last - 1)
-        normalise(last - 1)
+        normalise(last - 1, whole)
         times_vx(last - 3)
         sum_ev(last - 3)
         edge_moments(last)

from contextlib import ExitStack

import concourse.mybir as mybir
from concourse.masks import make_identity

F32 = mybir.dt.float32
BF16 = mybir.dt.bfloat16
U32 = mybir.dt.uint32
I32 = mybir.dt.int32
U8 = mybir.dt.uint8
FP8X4 = mybir.dt.float8_e4m3fn_x4
ACT = mybir.ActivationFunctionType
ALU = mybir.AluOpType
AX = mybir.AxisListType

P = 128
C = 1024
BANK = 512
NODES = 16
BATCH = 16
TILES = 32
QUAD = 4
WORDS = 256
EPS = 1e-5
SAMPLES = BATCH * C
FLOPS = 2 * (4096 + 4 * 256) * C * C

W_E, W_B, W_A, W_V, W_U = 0, 1, 2, 3, 4
PIECE = 256
NODE_KEY = 100

W_ROWS_BUFS = 4
W_GROUPED_BUFS = 4
E_GROUPED_BUFS = 2
E_CODES_BUFS = 4
EDGE_ROWS_BUFS = 3
EDGE_NEW_BUFS = 6
EXP_BUFS = 3
EV_BUFS = 3
VX_BUFS = 4
SUMS_BUFS = 8
EARLY_PIECES = W_ROWS_BUFS + VX_BUFS + EXP_BUFS
PIECES = 20
VX_LAG = 4
NORM_SHARE = 128
FREE_BANK_TILES = 4
VECTOR_COPIES = (3, 7, 9, 11)
EDGE_GAINS, EDGE_OFFSETS, NODE_GAINS, NODE_OFFSETS, PARAMS = 0, 32, 64, 80, 96


def tile_gnn_s2_pa_t_kernel(
    tc, x, edge, Wu, Wv, Wa, Wb, We, bnv_w, bnv_b, bne_w, bne_b, out_0, out_1
):
    nc = tc.nc
    weights = [We, Wb, Wa, Wv, Wu]
    edge_view = edge.rearrange("b (l h j) c -> (b l) h j c", h=2, j=NODES)
    edge_new_view = out_1.rearrange("b (l h j) c -> (b l) h j c", h=2, j=NODES)
    x_view = x.rearrange("b (l h) c -> (b l) h c", h=2)
    x_new_view = out_0.rearrange("b (l h) c -> (b l) h c", h=2)
    halves = [slice(0, BANK), slice(BANK, C)]
    whole = [slice(0, C)]

    with ExitStack() as ctx:
        resident = ctx.enter_context(tc.tile_pool(name="resident", bufs=1))
        staging = ctx.enter_context(tc.tile_pool(name="staging", bufs=2))
        work = ctx.enter_context(tc.tile_pool(name="work", bufs=2))
        columns = ctx.enter_context(tc.tile_pool(name="columns", bufs=8))
        psum = ctx.enter_context(tc.psum_pool(name="psum", bufs=1))
        sum_tags = {"exp": ("sum_exp0", "sum_exp1"), "ev": ("sum_ev0", "sum_ev1")}
        ctx.enter_context(tc.manual_schedule())

        ident = resident.tile([P, P], F32, name="ident")
        make_identity(nc, ident[:])
        same_l = resident.tile([P, 8], F32, name="same_l")
        nc.vector.tensor_reduce(
            out=same_l[:], in_=ident[:].rearrange("p (b l) -> p l b", l=8), axis=AX.X, op=ALU.add
        )
        average = resident.tile([P, P], F32, name="average")
        nc.vector.tensor_scalar(
            out=average[:].rearrange("p (b l) -> p b l", l=8),
            in0=same_l[:].unsqueeze(1).to_broadcast([P, 16, 8]),
            scalar1=1.0 / SAMPLES, scalar2=None, op0=ALU.mult,
        )
        minus_half = resident.tile([P, 1], F32, name="minus_half")
        nc.vector.memset(minus_half[:], -0.5)
        eps = resident.tile([P, 1], F32, name="eps")
        nc.vector.memset(eps[:], EPS)
        first_tanh = resident.tile([P, 1], F32, name="first_tanh")
        nc.scalar.activation(out=first_tanh[:], in_=minus_half[:], func=ACT.Tanh)

        w_codes = [resident.tile([P, 2, C], U32, name="w_codes%d" % w, align_bytes=256) for w in range(5)]
        w_scales = [resident.tile([P, 2, C], U8, name="w_scales%d" % w, align_bytes=256) for w in range(5)]
        x_codes = resident.tile([P, 2, WORDS], U32, name="x_codes", align_bytes=256)
        x_scales = resident.tile([P, 2, WORDS], U8, name="x_scales", align_bytes=256)
        x_scales4 = resident.tile([P, 8 * WORDS], U8, name="x_scales4", align_bytes=64)
        nc.vector.memset(x_scales[:].rearrange("p h w -> p (h w)").bitcast(I32), 0)
        xj_codes = resident.tile([P, NODES, WORDS], U32, name="xj_codes", align_bytes=256)
        xj_scales = resident.tile([P, NODES, WORDS], U8, name="xj_scales", align_bytes=256)
        ax = [resident.tile([P, C], F32, name="ax%d" % h) for h in range(2)]
        sum_exp0 = resident.tile([P, C], F32, name="sum_exp0")
        sum_ev0 = resident.tile([P, C], F32, name="sum_ev0")
        ux = [resident.tile([P, C], F32, name="ux%d" % h) for h in range(2)]
        row_sums = resident.tile([P, SUMS_BUFS, 8], F32, name="row_sums")

        def transpose_words(bank, rows_as_words):
            for k in range(4):
                nc.tensor.transpose(
                    bank[:, k * P:(k + 1) * P], rows_as_words[:, k * P:(k + 1) * P], ident[:]
                )

        def grouped_read(bank):
            return bank.rearrange("p (g u r) -> p g r u", g=2, u=2)

        def mx_group(acc, operands):
            last = len(operands) - 1
            for i, (l_codes, l_scales, r_codes, r_scales) in enumerate(operands):
                nc.tensor.matmul_mx(
                    out=acc, lhsT=l_codes.bitcast(FP8X4), lhsT_scale=l_scales,
                    rhs=r_codes.bitcast(FP8X4), rhs_scale=r_scales,
                    start=(i == 0), stop=(i == last),
                )

        def passes(codes, scales, w, cols):
            return [
                (codes[:, g * P:(g + 1) * P], scales[:, g * P:(g + 1) * P],
                 w_codes[w][:, g, cols], w_scales[w][:, g, cols])
                for g in range(2)
            ]

        w_rows = {}
        w_grouped = {}

        def load_piece(k):
            w, part = k // 4, k % 4
            turn = k % EARLY_PIECES
            if turn < W_ROWS_BUFS:
                w_rows[k] = staging.tile([P, 2, C], BF16, name="w_rows", tag="w_rows", bufs=W_ROWS_BUFS)
            elif turn < W_ROWS_BUFS + VX_BUFS:
                w_rows[k] = work.tile([P, 2, C], BF16, name="w_rows", tag="vx", bufs=VX_BUFS)
            else:
                w_rows[k] = work.tile([P, 2, C], BF16, name="w_rows", tag="exps", bufs=EXP_BUFS)
            nc.sync.dma_start(
                out=w_rows[k][:],
                in_=weights[w][part * PIECE:(part + 1) * PIECE, :].rearrange("(p a) k -> p a k", a=2),
            )

        def copy_on(vector, out, in_):
            if vector:
                nc.vector.tensor_copy(out=out, in_=in_)
            else:
                nc.scalar.copy(out=out, in_=in_)

        piece_banks = {}

        def transpose_piece(k, next_bank):
            piece_banks[k] = []
            for g in range(2):
                bank = next_bank()
                for a in range(2):
                    words = w_rows[k][:].bitcast(F32)[:, a, g * WORDS:(g + 1) * WORDS]
                    for u in range(2):
                        slot = 2 * a + u
                        nc.tensor.transpose(
                            bank[:, slot * P:(slot + 1) * P], words[:, u * P:(u + 1) * P], ident[:]
                        )
                piece_banks[k].append(bank)
            if k + EARLY_PIECES < PIECES:
                load_piece(k + EARLY_PIECES)

        def copy_half(k, g, vector):
            if k not in w_grouped:
                w_grouped[k] = staging.tile(
                    [P, 2048], BF16, name="w_grouped", tag="w_grouped", bufs=W_GROUPED_BUFS, align_bytes=64
                )
            dst = w_grouped[k][:].bitcast(F32).rearrange("p (g r a u) -> p g r a u", g=2, a=2, u=2)
            copy_on(vector, dst[:, g, :, :, :], piece_banks[k][g][:].rearrange("p (a u r) -> p r a u", a=2, u=2))

        def copy_piece(k, vector):
            copy_half(k, 0, False)
            copy_half(k, 1, vector)

        def quantise_piece(k):
            w, part = k // 4, k % 4
            cols = slice(part * PIECE, (part + 1) * PIECE)
            for g in range(2):
                nc.vector.quantize_mx(
                    out=w_codes[w][:, g, cols].bitcast(FP8X4), scales=w_scales[w][:, g, cols],
                    in_=w_grouped[k][:, g * 1024:(g + 1) * 1024],
                )

        sums_of, means_ps, moments, scale_bias = {}, {}, {}, {}

        def add_columns(dst, one, other):
            nc.scalar.activation(out=dst, in_=one, func=ACT.Identity, bias=other)

        def average_over_batches(key):
            means_ps[key] = psum.tile([P, 2], F32, name="means_ps", tag="stats", bufs=1)
            last_part = len(sums_of[key]) - 1
            for i, sums in enumerate(sums_of[key]):
                nc.tensor.matmul(
                    means_ps[key][:], lhsT=average[:], rhs=sums, start=(i == 0), stop=(i == last_part)
                )

        def minus_mean_and_squares(key):
            moments[key] = columns.tile([P, 4], F32, name="moments", tag="moments")
            mo, ps = moments[key], means_ps[key]
            nc.scalar.activation(out=mo[:, 0:1], in_=ps[:, 0:1], func=ACT.Identity, scale=-1.0)
            nc.scalar.activation(out=mo[:, 1:2], in_=ps[:, 1:2], func=ACT.Identity, bias=eps[:])

        def variance(key):
            mo = moments[key]
            nc.scalar.activation(
                out=mo[:, 2:3], in_=means_ps[key][:, 0:1], func=ACT.Identity, scale=mo[:, 0:1], bias=mo[:, 1:2]
            )

        def inverse_deviation(t):
            mo = moments[t]
            nc.gpsimd.tensor_tensor(out=mo[:, 2:3], in0=mo[:, 2:3], in1=minus_half[:], op=ALU.pow)

        def minus_mean_times_gain(t):
            nc.scalar.activation(
                out=gain_pairs[:, t, 1:2], in_=moments[t][:, 0:1], func=ACT.Identity,
                scale=params[:, EDGE_GAINS + t:EDGE_GAINS + t + 1],
            )

        def scale_and_bias(t):
            scale_bias[t] = columns.tile([P, 2], F32, name="scale_bias", tag="scale_bias")
            nc.vector.scalar_tensor_tensor(
                out=scale_bias[t][:], in0=gain_pairs[:, t, :], scalar=moments[t][:, 2:3], in1=offset_pairs[:, t, :],
                op0=ALU.mult, op1=ALU.add,
            )

        def apply_norm(key, dst, src):
            nc.vector.tensor_scalar(
                out=dst, in0=src, scalar1=scale_bias[key][:, 0:1], scalar2=scale_bias[key][:, 1:2],
                op0=ALU.mult, op1=ALU.add,
            )

        def add_residual(dst, src, residual):
            nc.vector.scalar_tensor_tensor(out=dst, in0=src, scalar=0.0, in1=residual, op0=ALU.max, op1=ALU.add)

        edge_rows, transposed, e_grouped, e_codes, e_scales, m_ps, edge_new, exps, evs, vx = (
            {}, {}, {}, {}, {}, {}, {}, {}, {}, {}
        )
        sums_ps = {}

        def is_tile(t):
            return 0 <= t < TILES

        def load_edges(q, lo, hi):
            if lo == 0:
                edge_rows[q] = staging.tile([P, QUAD, C], BF16, name="edge_rows", tag="edge_rows", bufs=EDGE_ROWS_BUFS)
            h, j = QUAD * q // NODES, QUAD * q % NODES
            nc.sync.dma_start(out=edge_rows[q][:, lo:hi, :], in_=edge_view[:, h, j + lo:j + hi, :])

        def edge_of(t):
            return edge_rows[t // QUAD][:, t % QUAD, :]

        def transpose_edges(t):
            if is_tile(t):
                if t < FREE_BANK_TILES:
                    transposed[t] = (next_bank if t == 0 else free_bank)()[:]
                else:
                    transposed[t] = psum.tile([P, BANK], F32, name="transposed", tag="transposed", bufs=1)
                transpose_words(transposed[t], edge_of(t).bitcast(F32))

        def copy_transposed(t):
            if is_tile(t):
                e_grouped[t] = work.tile(
                    [P, C], BF16, name="e_grouped", tag="e_grouped", bufs=E_GROUPED_BUFS, align_bytes=64
                )
                nc.scalar.copy(
                    out=e_grouped[t][:].bitcast(F32).rearrange("p (g r u) -> p g r u", g=2, u=2),
                    in_=grouped_read(transposed[t]),
                )

        def quantise_edges(t):
            if is_tile(t):
                e_codes[t] = work.tile(
                    [P, WORDS], U32, name="e_codes", tag="e_codes", bufs=E_CODES_BUFS, align_bytes=256
                )
                e_scales[t] = work.tile(
                    [P, WORDS], U8, name="e_scales", tag="e_scales", bufs=E_CODES_BUFS, align_bytes=256
                )
                nc.vector.quantize_mx(out=e_codes[t][:].bitcast(FP8X4), scales=e_scales[t][:], in_=e_grouped[t][:])

        def fill_bank(t, n):
            if is_tile(t):
                j = t % NODES
                m_ps[(t, n)] = psum.tile([P, BANK], F32, name="m_ps", tag="m", bufs=2)
                mx_group(
                    m_ps[(t, n)][:],
                    passes(e_codes[t], e_scales[t], W_E, halves[n])
                    + passes(xj_codes[:, j, :], xj_scales[:, j, :], W_B, halves[n]),
                )

        def empty_bank(t, n):
            if is_tile(t):
                if n == 0:
                    edge_new[t] = work.tile([P, C], F32, name="edge_new", tag="edge_new", bufs=EDGE_NEW_BUFS)
                nc.vector.scalar_tensor_tensor(
                    out=edge_new[t][:, halves[n]], in0=m_ps[(t, n)][:], scalar=1.0, in1=ax[t // NODES][:, halves[n]],
                    op0=ALU.mult, op1=ALU.add, accum_out=row_sums[:, t % SUMS_BUFS, n:n + 1],
                )

        def sum_squares(src, cols, dst):
            squares = work.tile([P, C], BF16, name="squares", tag="squares", bufs=2)
            nc.scalar.activation(out=squares[:, cols], in_=src, func=ACT.Square, accum_out=dst)

        def complete_row_sums(key, src, rs):
            sum_squares(src, whole[0], rs[:, 5:6])
            add_columns(rs[:, 4:5], rs[:, 0:1], rs[:, 1:2])
            sums_of[key] = [rs[:, 4:6]]

        def half_sums(rs):
            return [rs[:, n:n + 3:2] for n in range(2)]

        def half_squares(t, n):
            sum_squares(edge_new[t][:, halves[n]], halves[n], row_sums[:, t % SUMS_BUFS, 2 + n:3 + n])

        def add_half_sums(t):
            sums_of[t] = half_sums(row_sums[:, t % SUMS_BUFS, :])

        def edge_squares(t):
            if is_tile(t):
                complete_row_sums(t, edge_new[t][:], row_sums[:, t % SUMS_BUFS, :])

        def edge_average(t):
            if is_tile(t):
                average_over_batches(t)

        def edge_moments(t):
            if is_tile(t):
                minus_mean_and_squares(t)

        def edge_variance(t):
            if is_tile(t):
                variance(t)

        def edge_inverse_deviation(t):
            if is_tile(t):
                minus_mean_times_gain(t)
                inverse_deviation(t)

        def edge_scale_and_bias(t):
            if is_tile(t):
                scale_and_bias(t)

        def normalise(t, parts):
            if is_tile(t):
                for cols in parts:
                    apply_norm(t, edge_new[t][:, cols], edge_new[t][:, cols])

        def normalise_on_scalar(t):
            if is_tile(t):
                cols, sb = slice(C - NORM_SHARE, C), scale_bias[t]
                nc.scalar.activation(
                    out=edge_new[t][:, cols], in_=edge_new[t][:, cols], func=ACT.Identity,
                    scale=sb[:, 0:1], bias=sb[:, 1:2],
                )

        def finish_edge_new(t, parts=whole):
            if is_tile(t):
                for cols in parts:
                    add_residual(edge_new[t][:, cols], edge_new[t][:, cols], edge_of(t)[:, cols])
                nc.sync.dma_start(out=edge_new_view[:, t // NODES, t % NODES, :], in_=edge_new[t][:])

        def tanh_half(t, parts=whole):
            if is_tile(t):
                exps[t] = work.tile([P, C], F32, name="exps", tag="exps", bufs=EXP_BUFS)
                for cols in parts:
                    nc.scalar.activation(out=exps[t][:, cols], in_=edge_new[t][:, cols], func=ACT.Tanh, scale=0.5)

        def exp_half(t, parts=whole):
            if is_tile(t):
                for cols in parts:
                    nc.scalar.activation(out=exps[t][:, cols], in_=exps[t][:, cols], func=ACT.Exp, scale=0.5)

        def new_ev():
            ev = work.tile([P, C], F32, name="evs", tag="evs", bufs=EV_BUFS, align_bytes=64)
            return ev

        def load_vx(t):
            if is_tile(t):
                vx[t] = work.tile([P, C], F32, name="vx", tag="vx", bufs=VX_BUFS)
                nc.sync.dma_start(out=vx[t][:], in_=out_0[:, t % NODES, :].unsqueeze(1).to_broadcast([16, 8, C]))

        def times_vx(t, parts=whole):
            if is_tile(t):
                evs[t] = new_ev()
                for cols in parts:
                    nc.vector.tensor_tensor(out=evs[t][:, cols], in0=exps[t][:, cols], in1=vx[t][:, cols], op=ALU.mult)

        def add_to_sums(what, t, addend):
            h, j = t // NODES, t % NODES
            for n in range(2):
                if j == 0:
                    sums_ps[(what, h, n)] = psum.tile([P, BANK], F32, name="sums_ps", tag=sum_tags[what][n], bufs=1)
                for k in range(4):
                    col = n * BANK + k * P
                    nc.tensor.matmul(
                        sums_ps[(what, h, n)][:, k * P:(k + 1) * P], lhsT=addend[:, col:col + P], rhs=ident[:],
                        start=(j == 0 and k == 0), stop=(j == NODES - 1 and k == 3), is_transpose=True,
                    )

        def sum_exp(t):
            if is_tile(t):
                add_to_sums("exp", t, exps[t])

        def sum_ev(t):
            if is_tile(t):
                add_to_sums("ev", t, evs[t])

        inverse, agg, back, y, node_sums = {}, {}, {}, {}, {}

        def new_edge_new():
            tile = work.tile([P, C], F32, name="edge_new", tag="edge_new", bufs=EDGE_NEW_BUFS)
            return tile

        def node_agg(h, n):
            if n == 0:
                agg[h] = new_ev()
            nc.vector.tensor_tensor(
                out=agg[h][:, halves[n]], in0=sums_ps[("ev", 1, n)][:] if h == 1 else sum_ev0[:, halves[n]],
                in1=inverse[h][:, halves[n]], op=ALU.mult,
            )
            tag, bufs = ("m", 2) if h == 0 else (sum_tags["exp"][n], 1)
            back[(h, n)] = psum.tile([P, BANK], F32, name="back", tag=tag, bufs=bufs)
            transpose_words(back[(h, n)], agg[h][:, halves[n]])

        def node_y(h, n):
            if n == 0:
                y[h] = new_edge_new()
                node_sums[h] = columns.tile([P, 8], F32, name="node_sums", tag="node_sums", bufs=2)
            nc.vector.scalar_tensor_tensor(
                out=y[h][:, halves[n]], in0=back[(h, n)][:], scalar=1.0 / NODES, in1=ux[h][:, halves[n]],
                op0=ALU.mult, op1=ALU.add, accum_out=node_sums[h][:, n:n + 1],
            )

        def node_row_sums(h):
            for n in range(2):
                dst = node_sums[h][:, 2 + n:3 + n]
                if h == 1:
                    sum_squares(y[h][:, halves[n]], halves[n], dst)
                else:
                    squares = work.tile([P, C], BF16, name="squares", tag="squares", bufs=2)
                    nc.vector.scalar_tensor_tensor(
                        out=squares[:, halves[n]], in0=y[h][:, halves[n]], scalar=1.0, in1=y[h][:, halves[n]],
                        op0=ALU.mult, op1=ALU.mult, accum_out=dst,
                    )
            sums_of[NODE_KEY + h] = half_sums(node_sums[h])

        def node_scale_and_bias(h):
            key = NODE_KEY + h
            average_over_batches(key)
            scale_bias[key] = columns.tile([P, 2], F32, name="scale_bias", tag="scale_bias")
            mo = columns.tile([P, 4], F32, name="moments", tag="moments")
            sb, ps = scale_bias[key], means_ps[key]
            nc.scalar.activation(out=mo[:, 0:1], in_=ps[:, 0:1], func=ACT.Identity, scale=-1.0)
            nc.scalar.activation(out=mo[:, 1:2], in_=ps[:, 1:2], func=ACT.Identity, bias=eps[:])
            gain = params[:, NODE_GAINS + h:NODE_GAINS + h + 1]
            offset = params[:, NODE_OFFSETS + h:NODE_OFFSETS + h + 1]
            nc.scalar.activation(out=mo[:, 3:4], in_=mo[:, 0:1], func=ACT.Identity, scale=gain)
            nc.scalar.activation(
                out=mo[:, 2:3], in_=ps[:, 0:1], func=ACT.Abs_reciprocal_sqrt, scale=mo[:, 0:1], bias=mo[:, 1:2]
            )
            nc.scalar.activation(out=sb[:, 0:1], in_=mo[:, 2:3], func=ACT.Identity, scale=gain)
            nc.scalar.activation(out=sb[:, 1:2], in_=mo[:, 2:3], func=ACT.Identity, scale=mo[:, 3:4], bias=offset)

        def node_out(h):
            for n in range(2):
                apply_norm(NODE_KEY + h, ux[h][:, halves[n]], y[h][:, halves[n]])
            for n in range(2):
                add_residual(ux[h][:, halves[n]], ux[h][:, halves[n]], y[h][:, halves[n]])
                nc.sync.dma_start(out=x_new_view[:, h, halves[n]], in_=ux[h][:, halves[n]])

        def product_half(w, h, n, bank):
            mx_group(bank[:], passes(x_codes[:, h, :], x_scales[:, h, :], w, halves[n]))
            return bank

        free_tags = sum_tags["exp"] + sum_tags["ev"]
        free_taken = [0]

        def free_bank():
            tag = free_tags[free_taken[0] % 4]
            free_taken[0] += 1
            bank = psum.tile([P, BANK], F32, name="free_bank", tag=tag, bufs=1)
            return bank

        def m_bank():
            bank = psum.tile([P, BANK], F32, name="m_bank", tag="m", bufs=2)
            return bank

        def transposed_bank():
            bank = psum.tile([P, BANK], F32, name="transposed_bank", tag="transposed", bufs=1)
            return bank

        def stats_bank():
            bank = psum.tile([P, BANK], F32, name="stats_bank", tag="stats", bufs=1)
            return bank

        params = resident.tile([P, PARAMS], F32, name="params")
        params_scaled = resident.tile([P, PARAMS], F32, name="params_scaled")

        def scale_parameters():
            nc.vector.tensor_scalar(
                out=params_scaled[:], in0=params_rows[:], scalar1=float(SAMPLES), scalar2=None, op0=ALU.mult
            )

        def spread_parameters():
            params_ps = psum.tile([P, PARAMS], F32, name="params_ps", tag="stats", bufs=1)
            nc.tensor.matmul(params_ps[:], lhsT=average[:], rhs=params_scaled[:], start=True, stop=True)
            return params_ps

        gain_pairs = resident.tile([P, TILES, 2], F32, name="gain_pairs")
        offset_pairs = resident.tile([P, TILES, 2], F32, name="offset_pairs")
        nc.vector.memset(offset_pairs[:], 0.0)

        products = {}
        vx_rows = {}

        def multiply_x(w, h, n, next_bank):
            products[(w, h, n)] = product_half(w, h, n, next_bank())

        def copy_product(w, h, n, vector):
            if w == W_V and n == 0:
                vx_rows[h] = new_ev()
            dst = {W_A: ax, W_U: ux, W_V: vx_rows}[w][h]
            copy_on(vector, dst[:, halves[n]], products[(w, h, n)][:])
            if w == W_V and n == 1:
                nc.sync.dma_start(out=x_new_view[:, h, :], in_=vx_rows[h][:])

        def transpose_pieces(*ks):
            for k in ks:
                transpose_piece(k, free_bank)

        def scalar_copy(k, g):
            copy_half(k, g, False)

        def vector_copy(k, g):
            copy_half(k, g, True)

        def multiply(w, h, n):
            multiply_x(w, h, n, free_bank)

        def scalar_out(w, h, n):
            copy_product(w, h, n, False)

        def vector_out(w, h, n):
            copy_product(w, h, n, True)

        EXTRA = {
            (1, "half_filled"): [(transpose_pieces, 13), (transpose_edges, 3)],
            (1, "moments"): [(quantise_piece, 12), (vector_copy, 13, 1)],
            (1, "variance"): [(scalar_copy, 13, 0)],
            (1, "period_end"): [(transpose_pieces, 14, 15), (quantise_piece, 13)],
            (2, "period_start"): [(scalar_copy, 14, 0), (scalar_copy, 14, 1), (scalar_copy, 15, 0)],
            (2, "quantised"): [(vector_copy, 15, 1), (quantise_piece, 14), (quantise_piece, 15)],
            (2, "period_end"): [
                (multiply, W_V, 0, 0), (multiply, W_V, 1, 0), (multiply, W_V, 0, 1), (multiply, W_V, 1, 1),
                (transpose_pieces, 16, 17),
                (scalar_out, W_V, 0, 0), (scalar_out, W_V, 1, 0), (scalar_copy, 16, 0), (scalar_copy, 17, 0),
                (vector_out, W_V, 0, 1), (vector_out, W_V, 1, 1), (vector_copy, 16, 1), (vector_copy, 17, 1),
                (quantise_piece, 16),
            ],
            (3, "half_filled"): [(transpose_pieces, 18)],
            (3, "before_tanh"): [(scalar_copy, 18, 0)],
            (3, "variance"): [(scalar_copy, 18, 1)],
            (3, "period_end"): [
                (transpose_pieces, 19), (multiply, W_A, 1, 0), (multiply, W_A, 1, 1),
                (scalar_copy, 19, 0), (scalar_out, W_A, 1, 0),
                (vector_copy, 19, 1), (vector_out, W_A, 1, 1), (quantise_piece, 17), (quantise_piece, 18),
            ],
            (4, "period_end"): [(quantise_piece, 19)],
        }

        def extra(t, place):
            for f, *args in EXTRA.get((t, place), ()):
                f(*args)

        def period(t):
            edge_squares(t - 1)
            extra(t, "period_start")
            finish_edge_new(t - 3)
            if t > 0:
                quantise_edges(t + 1)
            extra(t, "quantised")
            if t > 0:
                fill_bank(t, 0)
            extra(t, "half_filled")
            edge_scale_and_bias(t - 2)
            times_vx(t - VX_LAG)
            if is_tile(t - VX_LAG):
                load_vx(t - VX_LAG + VX_BUFS)
            normalise(t - 2, [slice(0, C - NORM_SHARE)])
            if 0 < t < FREE_BANK_TILES:
                copy_transposed(t + 2)
            extra(t, "before_tanh")
            tanh_half(t - 3)
            if t > 0:
                fill_bank(t, 1)
            edge_average(t - 1)
            if t == NODES + VX_LAG:
                for n in range(2):
                    copy_on(n == 1, sum_ev0[:, halves[n]], sums_ps[("ev", 0, n)][:])
            normalise_on_scalar(t - 2)
            edge_moments(t - 1)
            extra(t, "moments")
            if t > 0:
                empty_bank(t, 0)
            if t >= FREE_BANK_TILES:
                copy_transposed(t + 2)
            edge_variance(t - 1)
            edge_inverse_deviation(t - 1)
            if t == TILES - 1:
                half_squares(t, 0)
            extra(t, "variance")
            if t < TILES - 1:
                exp_half(t - 3)
            sum_exp(t - 4)
            if t == NODES + 3:
                for n in range(2):
                    copy_on(n == 1, sum_exp0[:, halves[n]], sums_ps[("exp", 0, n)][:])
            sum_ev(t - VX_LAG)
            if t > 0:
                transpose_edges(t + 3)
                empty_bank(t, 1)
            if t == TILES - 1:
                half_squares(t, 1)
                exp_half(t - 3)
            extra(t, "period_end")

        x_rows = work.tile([P, 2, C], BF16, name="x_rows", tag="edge_new", bufs=EDGE_NEW_BUFS)
        nc.sync.dma_start(out=x_rows[:], in_=x_view)
        for k in range(EARLY_PIECES):
            load_piece(k)
            if k == 3:
                load_edges(0, 0, 1)
            if k == 9:
                load_edges(0, 1, 2)
        params_rows = resident.tile([P, PARAMS], BF16, name="params_rows")
        nc.vector.memset(params_rows[:], 0.0)
        for vector, col, width in (
            (bne_w, EDGE_GAINS, TILES), (bne_b, EDGE_OFFSETS, TILES), (bnv_w, NODE_GAINS, 2), (bnv_b, NODE_OFFSETS, 2)
        ):
            nc.sync.dma_start(
                out=params_rows[0:8, col:col + width], in_=vector.rearrange("(l x) -> l x", l=8)
            )

        rotation = [("m", 2), ("m", 2)] + [(tag, 1) for tag in free_tags]
        banks_taken = [0]

        def next_bank():
            tag, bufs = rotation[banks_taken[0] % len(rotation)]
            banks_taken[0] += 1
            bank = psum.tile([P, BANK], F32, name="bank", tag=tag, bufs=bufs)
            return bank

        x_grouped = []
        for h in range(2):
            x_bank = next_bank()
            transpose_words(x_bank[:], x_rows[:].bitcast(F32)[:, h, :])
            grouped = work.tile(
                [P, C], BF16, name="e_grouped", tag="e_grouped", bufs=E_GROUPED_BUFS, align_bytes=64
            )
            copy_on(
                h == 1, grouped[:].bitcast(F32).rearrange("p (g r u) -> p g r u", g=2, u=2), grouped_read(x_bank[:])
            )
            x_grouped.append(grouped)
        for h in range(2):
            nc.vector.quantize_mx(
                out=x_codes[:, h, :].bitcast(FP8X4), scales=x_scales[:, h, :], in_=x_grouped[h][:]
            )

        def quadruple_scales(i):
            nc.vector.tensor_copy(
                out=x_scales4[:].rearrange("p (n i) -> p n i", i=4)[:, :, i],
                in_=x_scales[:].rearrange("p h w -> p (h w)"),
            )

        def repeat_x(q):
            def repeated(words, times):
                per_node = words.rearrange("p (hg b l) -> p hg b l", hg=4, b=16, l=8)[:, :, :, q]
                return per_node.unsqueeze(3).to_broadcast([P, 4, 16, times])

            nc.vector.tensor_copy(
                out=xj_codes[:, 2 * q:2 * q + 2, :].rearrange("p j w -> p (j w)").bitcast(I32).rearrange(
                    "p (jg b l) -> p jg b l", jg=4, b=16, l=8
                ),
                in_=repeated(x_codes[:].rearrange("p h w -> p (h w)").bitcast(I32), 8),
            )
            nc.vector.tensor_copy(
                out=xj_scales[:, 2 * q:2 * q + 2, :].rearrange("p j w -> p (j w)").bitcast(I32).rearrange(
                    "p (jg b l) -> p jg b l", jg=4, b=16, l=2
                ),
                in_=repeated(x_scales4[:].bitcast(I32), 2),
            )

        for k in range(12):
            if k == 1:
                load_edges(0, 2, 4)
            if k == 4:
                load_edges(1, 0, 2)
            transpose_piece(k, next_bank if k < 8 else free_bank)
            copy_piece(k, k in VECTOR_COPIES)
            if k > 0:
                quantise_piece(k - 1)
            if 1 <= k <= 4:
                quadruple_scales(k - 1)
            if k == 5:
                repeat_x(0)
            if 6 <= k <= 8:
                repeat_x(2 * k - 11)
                repeat_x(2 * k - 10)
            if k == 9:
                repeat_x(7)
            if k in (8, 9):
                fill_bank(0, k - 8)
            if k == 4:
                transpose_edges(0)
                copy_transposed(0)
            if k == 6:
                quantise_edges(0)
            if k == 9:
                transpose_edges(1)
                copy_transposed(1)
            if k == 10:
                scale_parameters()
                bank = product_half(W_A, 0, 0, free_bank())
                nc.scalar.copy(out=ax[0][:, halves[0]], in_=bank[:])
        transpose_edges(2)
        params_ps = spread_parameters()
        quantise_piece(11)
        nc.vector.tensor_copy(out=params[:], in_=params_ps[:])
        nc.vector.tensor_copy(out=gain_pairs[:, :, 0], in_=params_ps[:, EDGE_GAINS:EDGE_GAINS + TILES])
        nc.vector.tensor_copy(out=offset_pairs[:, :, 1], in_=params_ps[:, EDGE_OFFSETS:EDGE_OFFSETS + TILES])
        empty_bank(0, 0)
        transpose_piece(12, free_bank)
        bank = product_half(W_A, 0, 1, free_bank())
        nc.scalar.copy(out=ax[0][:, halves[1]], in_=bank[:])
        quantise_edges(1)
        copy_transposed(2)
        copy_piece(12, True)
        empty_bank(0, 1)
        load_edges(1, 2, QUAD)

        for t in range(TILES):
            period(t)
            if t == 1:
                load_edges(2, 0, QUAD)
            if t == 2:
                for u in range(VX_BUFS):
                    load_vx(u)
            if t % QUAD == 2 and 6 <= t <= TILES - 10:
                load_edges((t + 6) // QUAD, 0, QUAD)

        last = TILES - 1
        add_half_sums(last)
        edge_average(last)
        multiply_x(W_U, 1, 0, m_bank)
        sum_exp(last - 3)
        multiply_x(W_U, 1, 1, m_bank)
        finish_edge_new(last - 2)
        scale_and_bias(last - 1)
        normalise(last - 1, whole)
        times_vx(last - 3)
        sum_ev(last - 3)
        edge_moments(last)
        tanh_half(last - 2)
        edge_variance(last)
        edge_inverse_deviation(last)
        exp_half(last - 2)
        finish_edge_new(last - 1, halves)
        sum_exp(last - 2)
        multiply_x(W_U, 0, 0, transposed_bank)
        multiply_x(W_U, 0, 1, stats_bank)
        tanh_half(last - 1, halves)
        exp_half(last - 1, halves)
        copy_product(W_U, 1, 0, True)
        scale_and_bias(last)
        normalise(last, halves)
        finish_edge_new(last, halves)
        sum_exp(last - 1)
        times_vx(last - 2)
        sum_ev(last - 2)
        tanh_half(last, halves)
        times_vx(last - 1)
        exp_half(last, halves)
        sum_exp(last)
        sum_ev(last - 1)
        times_vx(last, halves)
        sum_ev(last)
        copy_product(W_U, 1, 1, True)
        for n in range(2):
            copy_product(W_U, 0, n, True)

        inverse[0], inverse[1] = sum_exp0, new_edge_new()
        for h in (1, 0):
            for func in (ACT.Abs_reciprocal_sqrt, ACT.Square):
                for n in range(2):
                    cols = inverse[h][:, halves[n]]
                    src = sums_ps[("exp", 1, n)][:] if h == 1 and func == ACT.Abs_reciprocal_sqrt else cols
                    nc.scalar.activation(out=cols, in_=src, func=func)
        node_agg(1, 0)
        node_agg(1, 1)
        node_y(1, 0)
        node_y(1, 1)
        node_agg(0, 0)
        node_agg(0, 1)
        node_row_sums(1)
        node_scale_and_bias(1)
        node_y(0, 0)
        node_y(0, 1)
        node_row_sums(0)
        node_scale_and_bias(0)
        node_out(1)
        node_out(0)
